import numpy as np
import ml_dtypes


def mxq(x, axis, fmt="e4m3"):
    dtype, down = {"e4m3": (ml_dtypes.float8_e4m3fn, 7), "e5m2": (ml_dtypes.float8_e5m2, 14)}[fmt]
    v = np.moveaxis(np.asarray(x, np.float32).astype(ml_dtypes.bfloat16).astype(np.float64), axis, -1)
    blocks = v.reshape(v.shape[:-1] + (-1, 32))
    amax = np.abs(blocks).max(-1, keepdims=True)
    byte = np.maximum(np.where(amax > 0, np.frexp(amax)[1] - 1 + 127, 0) - down, 1)
    scale = np.exp2(byte - 127.0)
    codes = (blocks / scale).astype(np.float32).astype(dtype).astype(np.float64)
    return np.moveaxis((codes * scale).reshape(v.shape), -1, axis)


WIDE = False


def mx_kscale(k):
    if not WIDE:
        return np.ones(k)
    levels = np.array([10, -10, 5, -5, 0])
    a = np.random.permutation(np.resize(levels, k // 512 * 4)).reshape(k // 512, 4)
    idx = np.arange(k)
    return np.exp2(a[idx // 512, idx % 128 // 32])


BF16 = ml_dtypes.bfloat16


def bf(x):
    return np.asarray(x, np.float32).astype(BF16)


def f64(x):
    return np.asarray(x).astype(np.float64)


N, K, F, NB = 4096, 512, 128, 32
EPS = 1e-6


def erf(v):
    a = np.minimum(np.abs(v), 6.0)
    term = a.copy()
    total = a.copy()
    for n in range(1, 130):
        term = term * (2.0 * a * a / (2.0 * n + 1.0))
        total = total + term
    return np.sign(v) * (2.0 / np.sqrt(np.pi)) * np.exp(-a * a) * total


def gelu(v):
    return 0.5 * v * (1.0 + erf(v / np.sqrt(2.0)))


def setup_inputs():
    s = mx_kscale(K)
    edge = np.random.random_sample((N, N)) < NB / N
    return {"x": bf(np.random.standard_normal((N, K)) * s),
            "adj": bf(np.random.random_sample((N, N)) * edge),
            "W1": bf(np.random.standard_normal((K, F)) * 3.0 / np.sqrt(K) / s[:, None]),
            "b1": bf(np.random.standard_normal(F) * 0.3),
            "ln_gamma": bf(1.0 + 0.1 * np.random.standard_normal(F)),
            "ln_beta": bf(0.1 * np.random.standard_normal(F))}


def reference(x, adj, W1, b1, ln_gamma, ln_beta):
    a = f64(adj)
    h = (mxq(f64(x), 1, "e4m3") @ mxq(f64(W1), 0, "e4m3")) + f64(b1)
    deg = a.sum(axis=1) + 1.0
    dinv = np.where(deg > 0, deg ** -0.5, 0.0)
    hs = dinv[:, None] * h
    agg = (mxq(a, 1, "e4m3") @ mxq(hs, 0, "e4m3")) + hs
    g = gelu(dinv[:, None] * agg)
    mu = g.mean(axis=-1, keepdims=True)
    var = ((g - mu) ** 2).mean(axis=-1, keepdims=True)
    return (g - mu) / np.sqrt(var + EPS) * f64(ln_gamma) + f64(ln_beta)

@@ -1,0 +1,334 @@
+from contextlib import ExitStack
+
+import concourse.mybir as mybir
+from concourse.masks import make_identity
+
+F32 = mybir.dt.float32
+BF16 = mybir.dt.bfloat16
+U32 = mybir.dt.uint32
+U8 = mybir.dt.uint8
+FP8X4 = mybir.dt.float8_e4m3fn_x4
+ALU = mybir.AluOpType
+ACTF = mybir.ActivationFunctionType
+AX = mybir.AxisListType
+
+P = 128
+N_NODES = 4096
+K_IN = 512
+F_OUT = 128
+EPS = 1e-6
+N_TILES = 32
+N_GROUPS = 8
+N_X = 4
+N_ITEMS = N_X + N_TILES
+ND = 12
+
+FLOPS = 2 * N_NODES * K_IN * F_OUT + 2 * N_NODES * N_NODES * F_OUT
+
+
+def tile_gcnlayer_pa_t_kernel(tc, x, adj, W1, b1, ln_gamma, ln_beta, out):
+    nc = tc.nc
+    xv = x.rearrange("(s a p e) k -> s p a e k", s=N_X, a=4, p=P, e=2)
+    adjv = adj.rearrange("(g u p e) j -> g u e p j", g=N_GROUPS, u=2, p=P, e=2)
+    outv = out.rearrange("(g u p e) f -> g p u e f", g=N_GROUPS, u=2, p=P, e=2)
+
+    with ExitStack() as ctx:
+        keep = ctx.enter_context(tc.tile_pool(name="keep", bufs=1))
+        small = ctx.enter_context(tc.tile_pool(name="small", bufs=3))
+        psum = ctx.enter_context(tc.psum_pool(name="psum", bufs=1))
+
+        ident = keep.tile([P, P], F32, name="ident")
+        make_identity(nc, ident[:])
+        ones = keep.tile([P, P], BF16, name="ones")
+        nc.vector.memset(ones[:], 1.0)
+        zrow = keep.tile([P, 512], BF16, name="zrow")
+        nc.vector.memset(zrow[:], 0.0)
+        nc.scalar.dma_start(out=zrow[0:1, 0:128], in_=b1.rearrange("(o f) -> o f", o=1))
+        nc.scalar.dma_start(out=zrow[0:1, 128:256], in_=ln_gamma.rearrange("(o f) -> o f", o=1))
+        nc.scalar.dma_start(out=zrow[0:1, 256:384], in_=ln_beta.rearrange("(o f) -> o f", o=1))
+        w1n = keep.tile([P, 4, F_OUT], BF16, name="w1n")
+        nc.scalar.dma_start(
+            out=w1n[:].rearrange("q (u e) f -> q u e f", u=2),
+            in_=W1.rearrange("(u q e) f -> q u e f", u=2, q=P, e=2),
+        )
+        mhalf = keep.tile([P, 4], F32, name="mhalf")
+        nc.vector.memset(mhalf[:], -0.5)
+        dmy = keep.tile([P, 1], F32, name="dmy")
+        nc.vector.memset(dmy[:], 0.0)
+        dmy2 = keep.tile([P, 1], F32, name="dmy2")
+        nc.scalar.activation(out=dmy2[:], in_=dmy[:], func=ACTF.Gelu)
+
+        rsel = keep.tile([P, 32], F32, name="rsel")
+        nc.vector.tensor_reduce(
+            out=rsel[:], in_=ident[:].rearrange("k (a t) -> k a t", t=4), axis=AX.X, op=ALU.add
+        )
+        sel4 = keep.tile([P, 4, P], F32, name="sel4")
+        nc.vector.memset(sel4[:], 0.0)
+        for s in range(4):
+            nc.vector.tensor_copy(out=sel4[:, s, 32 * s : 32 * s + 32], in_=rsel[:])
+
+        bcps = psum.tile([P, 512], F32, tag="hps", name="bcps")
+        nc.tensor.matmul(out=bcps[:], lhsT=ones[:], rhs=zrow[:], start=True, stop=True)
+        bc = keep.tile([P, 384], F32, name="bc")
+        nc.vector.tensor_copy(out=bc[:], in_=bcps[:, 0:384])
+
+        w1g = keep.tile([P, F_OUT, 4], BF16, name="w1g", align_bytes=64)
+        nc.vector.tensor_copy(out=w1g[:], in_=w1n[:].rearrange("q t f -> q f t"))
+        w1c = keep.tile([P, F_OUT], U32, name="w1c", align_bytes=64)
+        w1s = keep.tile([P, F_OUT], U8, name="w1s", align_bytes=64)
+        nc.vector.quantize_mx(
+            out=w1c[:].bitcast(FP8X4), scales=w1s[:], in_=w1g[:].rearrange("q f t -> q (f t)")
+        )
+
+        codes = [
+            keep.tile([P, 1024], U32, name="codes%d" % t, align_bytes=64) for t in range(N_TILES)
+        ]
+        planes = [
+            keep.tile([P, 1024], U8, name="planes%d" % g, align_bytes=64) for g in range(N_GROUPS)
+        ]
+        h = keep.tile([P, N_TILES, F_OUT], F32, name="h")
+        hcod = keep.tile([P, N_GROUPS * F_OUT], U32, name="hcod", align_bytes=64)
+        hscl = keep.tile([P, N_GROUPS * F_OUT], U8, name="hscl", align_bytes=64)
+        deg1 = keep.tile([P, N_TILES], F32, name="deg1")
+        dinv = keep.tile([P, N_TILES], F32, name="dinv")
+        rdeg = keep.tile([P, N_TILES], F32, name="rdeg")
+
+        nats = {}
+        grps = {}
+        dps = {}
+        dsbs = {}
+        o2s = {}
+
+        def slot_of(k):
+            return k - N_X if k >= N_X else N_TILES - N_X + k
+
+        def load(k, natp):
+            nat = natp.tile([P, 4096], BF16, tag="nat", name="nat%d" % k)
+            nats[k] = nat
+            if k < N_X:
+                nc.sync.dma_start(
+                    out=nat[:].rearrange("p (a e k) -> p a e k", a=4, e=2, k=K_IN), in_=xv[k]
+                )
+            else:
+                t = k - N_X
+                nc.sync.dma_start(out=nat[:], in_=adjv[t // 4, (t % 4) // 2, t % 2])
+
+        def transp(k, grp):
+            nat_w = nats[k][:].bitcast(F32)
+            gt = grp.tile([P, 4096], BF16, tag="G", name="G%d" % k, align_bytes=64)
+            grps[k] = gt
+            g_w = gt[:].bitcast(F32).rearrange("p (c i u) -> p c i u", c=8, i=P, u=2)
+            for b in range(4):
+                xt = psum.tile([P, 2, 2, P], F32, tag="xt", bufs=5, name="xt%d_%d" % (k, b))
+                for cc in range(2):
+                    for u in range(2):
+                        w0 = 256 * (2 * b + cc) + 128 * u
+                        nc.tensor.transpose(xt[:, cc, u, :], nat_w[:, w0 : w0 + 128], ident[:])
+                src = xt[:].rearrange("p c u i -> p c i u")
+                dst = g_w[:, 2 * b : 2 * b + 2, :, :]
+                if b == 3 and k % 2 == 1:
+                    nc.vector.tensor_copy(out=dst, in_=src)
+                else:
+                    nc.scalar.copy(out=dst, in_=src)
+
+        def quant(k):
+            sl = slot_of(k)
+            kk = 4 * (sl % 4)
+            for hf in range(2):
+                nc.vector.quantize_mx(
+                    out=codes[sl][:, 512 * hf : 512 * hf + 512].bitcast(FP8X4),
+                    scales=planes[sl // 4][kk:P, 512 * hf : 512 * hf + 512],
+                    in_=grps[k][:, 2048 * hf : 2048 * hf + 2048],
+                )
+
+        def mx1(k):
+            sl = slot_of(k)
+            kk = 4 * (sl % 4)
+            for gg in range(2):
+                g = 2 * k + gg
+                hps = psum.tile([P, 4, F_OUT], F32, tag="hps", name="hps%d" % g)
+                for t4 in range(4):
+                    c0 = 128 * (4 * gg + t4)
+                    nc.tensor.matmul_mx(
+                        out=hps[:, t4, :],
+                        lhsT=codes[sl][:, c0 : c0 + 128].bitcast(FP8X4),
+                        lhsT_scale=planes[sl // 4][kk:P, c0 : c0 + 128],
+                        rhs=w1c[:].bitcast(FP8X4),
+                        rhs_scale=w1s[:],
+                        start=True,
+                        stop=True,
+                    )
+                nc.vector.tensor_tensor(
+                    out=h[:, 4 * g : 4 * g + 4, :],
+                    in0=hps[:],
+                    in1=bc[:, 0:128].unsqueeze(1).to_broadcast([P, 4, F_OUT]),
+                    op=ALU.add,
+                )
+
+        def degmm(k):
+            t = k - N_X
+            g = t // 4
+            t4 = t % 4
+            if t4 == 0:
+                dps[g] = psum.tile([P, 4, 4, ND], F32, tag="D", name="D%d" % g)
+            dp = dps[g]
+            gt = grps[k]
+            for s in range(4):
+                for c in range(8):
+                    c0 = 512 * c + 128 * s
+                    nc.tensor.matmul(
+                        out=dp[:, t4, s, :],
+                        lhsT=gt[:, c0 : c0 + 128],
+                        rhs=ones[:, 0:ND],
+                        start=(c == 0),
+                        stop=(c == 7),
+                    )
+
+        def chain1(g):
+            dsb = small.tile([P, 4, 4], F32, tag="dsb", name="dsb%d" % g)
+            dsbs[g] = dsb
+            nc.vector.tensor_copy(out=dsb[:], in_=dps[g][:, :, :, 0].rearrange("p t s -> p s t"))
+
+        def chain2(g):
+            o2 = psum.tile([P, 4], F32, tag="o2", name="o2_%d" % g)
+            o2s[g] = o2
+            for s in range(4):
+                nc.tensor.matmul(
+                    out=o2[:], lhsT=sel4[:, s, :], rhs=dsbs[g][:, s, :], start=(s == 0), stop=(s == 3)
+                )
+
+        def chain3(g):
+            sl = slice(4 * g, 4 * g + 4)
+            nc.vector.tensor_scalar_add(out=deg1[:, sl], in0=o2s[g][:], scalar1=1.0)
+            nc.gpsimd.tensor_tensor(out=dinv[:, sl], in0=deg1[:, sl], in1=mhalf[:], op=ALU.pow)
+            nc.vector.reciprocal(out=rdeg[:, sl], in_=deg1[:, sl])
+
+        def chain4(g):
+            sl = slice(4 * g, 4 * g + 4)
+            hsb = small.tile([P, F_OUT, 4], BF16, tag="hsb", name="hsb%d" % g, align_bytes=64)
+            nc.vector.tensor_tensor(
+                out=hsb[:],
+                in0=h[:, sl, :].rearrange("p t f -> p f t"),
+                in1=dinv[:, sl].unsqueeze(1).to_broadcast([P, F_OUT, 4]),
+                op=ALU.mult,
+            )
+            nc.vector.tensor_tensor(
+                out=h[:, sl, :],
+                in0=h[:, sl, :],
+                in1=rdeg[:, sl].unsqueeze(2).to_broadcast([P, 4, F_OUT]),
+                op=ALU.mult,
+            )
+            nc.vector.quantize_mx(
+                out=hcod[:, 128 * g : 128 * g + 128].bitcast(FP8X4),
+                scales=hscl[:, 128 * g : 128 * g + 128],
+                in_=hsb[:].rearrange("p f t -> p (f t)"),
+            )
+
+        def mx2(acc, g, t4, c):
+            t = 4 * g + t4
+            nc.tensor.matmul_mx(
+                out=acc[:, t4, :],
+                lhsT=codes[t][:, 128 * c : 128 * c + 128].bitcast(FP8X4),
+                lhsT_scale=planes[g][4 * t4 : P, 128 * c : 128 * c + 128],
+                rhs=hcod[:, 128 * c : 128 * c + 128].bitcast(FP8X4),
+                rhs_scale=hscl[:, 128 * c : 128 * c + 128],
+                start=(c == 0),
+                stop=(c == 7),
+            )
+
+        acc_tags = ["xt", "xt", "xt", "xt", "xt", "hps", "D", "o2"]
+        accs = {}
+        n_pre = 6
+        with tc.tile_pool(name="natp", bufs=4) as natp, tc.tile_pool(name="grp", bufs=3) as grp:
+            for k in range(4):
+                load(k, natp)
+            for it in range(N_ITEMS + 3):
+                if it < N_ITEMS:
+                    transp(it, grp)
+                    if it + 4 < N_ITEMS:
+                        load(it + 4, natp)
+                k = it - 1
+                if N_X <= k < N_ITEMS:
+                    degmm(k)
+                if 0 <= k < N_ITEMS:
+                    quant(k)
+                if 0 <= it - 2 < N_X:
+                    mx1(it - 2)
+                if it >= 8 and (it - 8) % 4 == 0 and (it - 8) // 4 < N_GROUPS:
+                    chain1((it - 8) // 4)
+                if it >= 9 and (it - 9) % 4 == 0 and (it - 9) // 4 < N_GROUPS:
+                    chain2((it - 9) // 4)
+                    chain3((it - 9) // 4)
+                if it >= 10 and (it - 10) % 4 == 0 and (it - 10) // 4 < N_GROUPS:
+                    chain4((it - 10) // 4)
+                if it == N_ITEMS:
+                    for g in range(n_pre):
+                        accs[g] = psum.tile(
+                            [P, 4, F_OUT], F32, tag=acc_tags[g], bufs=(5 if g < 5 else 1), name="acc%d" % g
+                        )
+                        for c in range(7):
+                            mx2(accs[g], g, 0, c)
+
+        with tc.tile_pool(name="ep", bufs=3) as ep:
+            for g in range(N_GROUPS):
+                if g < n_pre:
+                    acc = accs[g]
+                    mx2(acc, g, 0, 7)
+                else:
+                    acc = psum.tile([P, 4, F_OUT], F32, tag=acc_tags[g], name="acc%d" % g)
+                    for c in range(8):
+                        mx2(acc, g, 0, c)
+                for t4 in range(1, 4):
+                    for c in range(8):
+                        mx2(acc, g, t4, c)
+
+                z = ep.tile([P, 4, F_OUT], F32, tag="z", name="z%d" % g)
+                for t4 in range(4):
+                    t = 4 * g + t4
+                    nc.vector.scalar_tensor_tensor(
+                        out=z[:, t4, :],
+                        in0=acc[:, t4, :],
+                        scalar=dinv[:, t : t + 1],
+                        in1=h[:, t, :],
+                        op0=ALU.mult,
+                        op1=ALU.add,
+                    )
+                gl = ep.tile([P, 4, F_OUT], F32, tag="gl", name="gl%d" % g)
+                nc.scalar.activation(out=gl[:], in_=z[:], func=ACTF.Gelu)
+                st = small.tile([P, 4, 6], F32, tag="st", name="st%d" % g)
+                mv = small.tile([P, 4, 2], F32, tag="mv", name="mv%d" % g)
+                for t4 in range(4):
+                    nc.vector.bn_stats(out=st[:, t4, :], in_=gl[:, t4, :])
+                for t4 in range(4):
+                    nc.vector.bn_aggr(out=mv[:, t4, :], in_=st[:, t4, :])
+                ve = small.tile([P, 4], F32, tag="ve", name="ve%d" % g)
+                nc.vector.tensor_scalar_add(out=ve[:], in0=mv[:, :, 1], scalar1=EPS)
+                rstd = small.tile([P, 4], F32, tag="rstd", name="rstd%d" % g)
+                nc.gpsimd.tensor_tensor(out=rstd[:], in0=ve[:], in1=mhalf[:], op=ALU.pow)
+                nmr = small.tile([P, 4], F32, tag="nmr", name="nmr%d" % g)
+                nc.vector.scalar_tensor_tensor(
+                    out=nmr[:], in0=mv[:, :, 0], scalar=-1.0, in1=rstd[:], op0=ALU.mult, op1=ALU.mult
+                )
+                yn = ep.tile([P, 4, F_OUT], F32, tag="yn", name="yn%d" % g)
+                for t4 in range(4):
+                    nc.scalar.activation(
+                        out=yn[:, t4, :],
+                        in_=gl[:, t4, :],
+                        func=ACTF.Identity,
+                        scale=rstd[:, t4 : t4 + 1],
+                        bias=nmr[:, t4 : t4 + 1],
+                    )
+                y = ep.tile([P, 4, F_OUT], F32, tag="y", name="y%d" % g)
+                nc.gpsimd.tensor_tensor(
+                    out=y[:],
+                    in0=yn[:],
+                    in1=bc[:, 128:256].unsqueeze(1).to_broadcast([P, 4, F_OUT]),
+                    op=ALU.mult,
+                )
+                nc.vector.tensor_tensor(
+                    out=y[:],
+                    in0=y[:],
+                    in1=bc[:, 256:384].unsqueeze(1).to_broadcast([P, 4, F_OUT]),
+                    op=ALU.add,
+                )
+                nc.sync.dma_start(out=outv[g], in_=y[:].rearrange("p (u e) f -> p u e f", u=2))

@@ -22,6 +22,9 @@ N_GROUPS = 8
 N_X = 4
 N_ITEMS = N_X + N_TILES
 ND = 12
+PIN = True
+N_WARM = 8
+N_HOLD = 1
 
 FLOPS = 2 * N_NODES * K_IN * F_OUT + 2 * N_NODES * N_NODES * F_OUT
 
@@ -34,92 +37,119 @@ def tile_gcnlayer_pa_t_kernel(tc, x, adj, W1, b1, ln_gamma, ln_beta, out):
 
     with ExitStack() as ctx:
         keep = ctx.enter_context(tc.tile_pool(name="keep", bufs=1))
-        small = ctx.enter_context(tc.tile_pool(name="small", bufs=3))
+        small = ctx.enter_context(tc.tile_pool(name="small", bufs=4))
         psum = ctx.enter_context(tc.psum_pool(name="psum", bufs=1))
 
-        ident = keep.tile([P, P], F32, name="ident")
-        make_identity(nc, ident[:])
-        ones = keep.tile([P, P], BF16, name="ones")
-        nc.vector.memset(ones[:], 1.0)
-        zrow = keep.tile([P, 512], BF16, name="zrow")
-        nc.vector.memset(zrow[:], 0.0)
-        nc.scalar.dma_start(out=zrow[0:1, 0:128], in_=b1.rearrange("(o f) -> o f", o=1))
-        nc.scalar.dma_start(out=zrow[0:1, 128:256], in_=ln_gamma.rearrange("(o f) -> o f", o=1))
-        nc.scalar.dma_start(out=zrow[0:1, 256:384], in_=ln_beta.rearrange("(o f) -> o f", o=1))
-        w1n = keep.tile([P, 4, F_OUT], BF16, name="w1n")
-        nc.scalar.dma_start(
-            out=w1n[:].rearrange("q (u e) f -> q u e f", u=2),
-            in_=W1.rearrange("(u q e) f -> q u e f", u=2, q=P, e=2),
-        )
-        mhalf = keep.tile([P, 4], F32, name="mhalf")
-        nc.vector.memset(mhalf[:], -0.5)
-        dmy = keep.tile([P, 1], F32, name="dmy")
-        nc.vector.memset(dmy[:], 0.0)
-        dmy2 = keep.tile([P, 1], F32, name="dmy2")
-        nc.scalar.activation(out=dmy2[:], in_=dmy[:], func=ACTF.Gelu)
+        def body(natp, grp):
+            nats = {}
+            grps = {}
+            dps = {}
+            dsbs = {}
+            o2s = {}
+            hpss = {}
 
-        rsel = keep.tile([P, 32], F32, name="rsel")
-        nc.vector.tensor_reduce(
-            out=rsel[:], in_=ident[:].rearrange("k (a t) -> k a t", t=4), axis=AX.X, op=ALU.add
-        )
-        sel4 = keep.tile([P, 4, P], F32, name="sel4")
-        nc.vector.memset(sel4[:], 0.0)
-        for s in range(4):
-            nc.vector.tensor_copy(out=sel4[:, s, 32 * s : 32 * s + 32], in_=rsel[:])
+            def load(k):
+                nat = natp.tile([P, 4096], BF16, tag="nat", name="nat%d" % k)
+                nats[k] = nat
+                if k == 0:
+                    for a in range(4):
+                        nc.sync.dma_start(
+                            out=nat[:, 1024 * a : 1024 * a + 1024].rearrange("p (e k) -> p e k", e=2),
+                            in_=xv[0][:, a],
+                        )
+                elif k < N_X:
+                    nc.sync.dma_start(
+                        out=nat[:].rearrange("p (a e k) -> p a e k", a=4, e=2, k=K_IN), in_=xv[k]
+                    )
+                else:
+                    t = k - N_X
+                    nc.sync.dma_start(out=nat[:], in_=adjv[t // 4, (t % 4) // 2, t % 2])
 
-        bcps = psum.tile([P, 512], F32, tag="hps", name="bcps")
-        nc.tensor.matmul(out=bcps[:], lhsT=ones[:], rhs=zrow[:], start=True, stop=True)
-        bc = keep.tile([P, 384], F32, name="bc")
-        nc.vector.tensor_copy(out=bc[:], in_=bcps[:, 0:384])
+            for k in range(4):
+                load(k)
 
-        w1g = keep.tile([P, F_OUT, 4], BF16, name="w1g", align_bytes=64)
-        nc.vector.tensor_copy(out=w1g[:], in_=w1n[:].rearrange("q t f -> q f t"))
-        w1c = keep.tile([P, F_OUT], U32, name="w1c", align_bytes=64)
-        w1s = keep.tile([P, F_OUT], U8, name="w1s", align_bytes=64)
-        nc.vector.quantize_mx(
-            out=w1c[:].bitcast(FP8X4), scales=w1s[:], in_=w1g[:].rearrange("q f t -> q (f t)")
-        )
+            dsrc = grp.tile([P, 4096], BF16, tag="G", name="dsrc", align_bytes=64)
+            nc.vector.memset(dsrc[:, 0:2048], 1.0)
+            dcod = keep.tile([P, 512], U32, name="dcod", align_bytes=64)
+            dscl = keep.tile([P, 512], U8, name="dscl", align_bytes=64)
+            nc.vector.quantize_mx(out=dcod[:].bitcast(FP8X4), scales=dscl[:], in_=dsrc[:, 0:2048])
+            ident = keep.tile([P, P], F32, name="ident")
+            make_identity(nc, ident[:])
+            ones = keep.tile([P, P], BF16, name="ones")
+            nc.vector.memset(ones[:], 1.0)
+            zrow = keep.tile([P, 512], BF16, name="zrow")
+            nc.vector.memset(zrow[:], 0.0)
+            w1n = keep.tile([P, 4, F_OUT], BF16, name="w1n")
+            nc.scalar.dma_start(
+                out=w1n[:].rearrange("q (u e) f -> q u e f", u=2),
+                in_=W1.rearrange("(u q e) f -> q u e f", u=2, q=P, e=2),
+            )
+            nc.scalar.dma_start(out=zrow[0:1, 0:128], in_=b1.rearrange("(o f) -> o f", o=1))
+            nc.scalar.dma_start(out=zrow[0:1, 128:256], in_=ln_gamma.rearrange("(o f) -> o f", o=1))
+            nc.scalar.dma_start(out=zrow[0:1, 256:384], in_=ln_beta.rearrange("(o f) -> o f", o=1))
+            mhalf = keep.tile([P, 4], F32, name="mhalf")
+            nc.vector.memset(mhalf[:], -0.5)
+            dmy = keep.tile([P, 1], F32, name="dmy")
+            nc.vector.memset(dmy[:], 0.0)
+            dmy2 = keep.tile([P, 1], F32, name="dmy2")
+            nc.scalar.activation(out=dmy2[:], in_=dmy[:], func=ACTF.Gelu)
 
-        codes = [
-            keep.tile([P, 1024], U32, name="codes%d" % t, align_bytes=64) for t in range(N_TILES)
-        ]
-        planes = [
-            keep.tile([P, 1024], U8, name="planes%d" % g, align_bytes=64) for g in range(N_GROUPS)
-        ]
-        h = keep.tile([P, N_TILES, F_OUT], F32, name="h")
-        hcod = keep.tile([P, N_GROUPS * F_OUT], U32, name="hcod", align_bytes=64)
-        hscl = keep.tile([P, N_GROUPS * F_OUT], U8, name="hscl", align_bytes=64)
-        deg1 = keep.tile([P, N_TILES], F32, name="deg1")
-        dinv = keep.tile([P, N_TILES], F32, name="dinv")
-        rdeg = keep.tile([P, N_TILES], F32, name="rdeg")
+            dm = psum.tile([P, 512], F32, tag="dm", name="dm")
 
-        nats = {}
-        grps = {}
-        dps = {}
-        dsbs = {}
-        o2s = {}
-
-        def slot_of(k):
-            return k - N_X if k >= N_X else N_TILES - N_X + k
-
-        def load(k, natp):
-            nat = natp.tile([P, 4096], BF16, tag="nat", name="nat%d" % k)
-            nats[k] = nat
-            if k < N_X:
-                nc.sync.dma_start(
-                    out=nat[:].rearrange("p (a e k) -> p a e k", a=4, e=2, k=K_IN), in_=xv[k]
+            def hold():
+                nc.tensor.matmul_mx(
+                    out=dm[:],
+                    lhsT=dcod[:, 0:128].bitcast(FP8X4),
+                    lhsT_scale=dscl[:, 0:128],
+                    rhs=dcod[:].bitcast(FP8X4),
+                    rhs_scale=dscl[:],
+                    start=True,
+                    stop=True,
                 )
-            else:
-                t = k - N_X
-                nc.sync.dma_start(out=nat[:], in_=adjv[t // 4, (t % 4) // 2, t % 2])
 
-        def transp(k, grp):
-            nat_w = nats[k][:].bitcast(F32)
-            gt = grp.tile([P, 4096], BF16, tag="G", name="G%d" % k, align_bytes=64)
-            grps[k] = gt
-            g_w = gt[:].bitcast(F32).rearrange("p (c i u) -> p c i u", c=8, i=P, u=2)
-            for b in range(4):
-                xt = psum.tile([P, 2, 2, P], F32, tag="xt", bufs=5, name="xt%d_%d" % (k, b))
+            for w in range(N_WARM):
+                hold()
+
+            rsel = keep.tile([P, 32], F32, name="rsel")
+            nc.vector.tensor_reduce(
+                out=rsel[:], in_=ident[:].rearrange("k (a t) -> k a t", t=4), axis=AX.X, op=ALU.add
+            )
+            sel4 = keep.tile([P, 4, P], F32, name="sel4")
+            nc.vector.memset(sel4[:], 0.0)
+            for s in range(4):
+                nc.vector.tensor_copy(out=sel4[:, s, 32 * s : 32 * s + 32], in_=rsel[:])
+
+            w1g = keep.tile([P, F_OUT, 4], BF16, name="w1g", align_bytes=64)
+            nc.vector.tensor_copy(out=w1g[:], in_=w1n[:].rearrange("q t f -> q f t"))
+            w1c = keep.tile([P, F_OUT], U32, name="w1c", align_bytes=64)
+            w1s = keep.tile([P, F_OUT], U8, name="w1s", align_bytes=64)
+            nc.vector.quantize_mx(
+                out=w1c[:].bitcast(FP8X4), scales=w1s[:], in_=w1g[:].rearrange("q f t -> q (f t)")
+            )
+            bc = keep.tile([P, 384], F32, name="bc")
+
+            codes = [
+                keep.tile([P, 1024], U32, name="codes%d" % t, align_bytes=64) for t in range(N_TILES)
+            ]
+            planes = [
+                keep.tile([P, 1024], U8, name="planes%d" % g, align_bytes=64) for g in range(N_GROUPS)
+            ]
+            h = keep.tile([P, N_TILES, F_OUT], F32, name="h")
+            hcod = keep.tile([P, N_GROUPS * F_OUT], U32, name="hcod", align_bytes=64)
+            hscl = keep.tile([P, N_GROUPS * F_OUT], U8, name="hscl", align_bytes=64)
+            deg1 = keep.tile([P, N_TILES], F32, name="deg1")
+            dinv = keep.tile([P, N_TILES], F32, name="dinv")
+            rdeg = keep.tile([P, N_TILES], F32, name="rdeg")
+
+            def slot_of(k):
+                return k - N_X if k >= N_X else N_TILES - N_X + k
+
+            def transp(k, b, grp):
+                if b == 0:
+                    grps[k] = grp.tile([P, 4096], BF16, tag="G", name="G%d" % k, align_bytes=64)
+                nat_w = nats[k][:].bitcast(F32)
+                g_w = grps[k][:].bitcast(F32).rearrange("p (c i u) -> p c i u", c=8, i=P, u=2)
+                xt = psum.tile([P, 2, 2, P], F32, tag="xt", bufs=4, name="xt%d_%d" % (k, b))
                 for cc in range(2):
                     for u in range(2):
                         w0 = 256 * (2 * b + cc) + 128 * u
@@ -131,204 +161,289 @@ def tile_gcnlayer_pa_t_kernel(tc, x, adj, W1, b1, ln_gamma, ln_beta, out):
                 else:
                     nc.scalar.copy(out=dst, in_=src)
 
-        def quant(k):
-            sl = slot_of(k)
-            kk = 4 * (sl % 4)
-            for hf in range(2):
-                nc.vector.quantize_mx(
-                    out=codes[sl][:, 512 * hf : 512 * hf + 512].bitcast(FP8X4),
-                    scales=planes[sl // 4][kk:P, 512 * hf : 512 * hf + 512],
-                    in_=grps[k][:, 2048 * hf : 2048 * hf + 2048],
-                )
-
-        def mx1(k):
-            sl = slot_of(k)
-            kk = 4 * (sl % 4)
-            for gg in range(2):
-                g = 2 * k + gg
-                hps = psum.tile([P, 4, F_OUT], F32, tag="hps", name="hps%d" % g)
-                for t4 in range(4):
-                    c0 = 128 * (4 * gg + t4)
-                    nc.tensor.matmul_mx(
-                        out=hps[:, t4, :],
-                        lhsT=codes[sl][:, c0 : c0 + 128].bitcast(FP8X4),
-                        lhsT_scale=planes[sl // 4][kk:P, c0 : c0 + 128],
-                        rhs=w1c[:].bitcast(FP8X4),
-                        rhs_scale=w1s[:],
-                        start=True,
-                        stop=True,
+            def quant(k):
+                sl = slot_of(k)
+                kk = 4 * (sl % 4)
+                for hf in range(2):
+                    nc.vector.quantize_mx(
+                        out=codes[sl][:, 512 * hf : 512 * hf + 512].bitcast(FP8X4),
+                        scales=planes[sl // 4][kk:P, 512 * hf : 512 * hf + 512],
+                        in_=grps[k][:, 2048 * hf : 2048 * hf + 2048],
                     )
-                nc.vector.tensor_tensor(
-                    out=h[:, 4 * g : 4 * g + 4, :],
-                    in0=hps[:],
-                    in1=bc[:, 0:128].unsqueeze(1).to_broadcast([P, 4, F_OUT]),
-                    op=ALU.add,
-                )
 
-        def degmm(k):
-            t = k - N_X
-            g = t // 4
-            t4 = t % 4
-            if t4 == 0:
-                dps[g] = psum.tile([P, 4, 4, ND], F32, tag="D", name="D%d" % g)
-            dp = dps[g]
-            gt = grps[k]
-            for s in range(4):
+            def mx1(k):
+                sl = slot_of(k)
+                kk = 4 * (sl % 4)
+                for gg in range(2):
+                    g = 2 * k + gg
+                    hps = psum.tile([P, 4, F_OUT], F32, tag=("hps" if gg == 0 else "D"), name="hps%d" % g)
+                    hpss[g] = hps
+                    for t4 in range(4):
+                        c0 = 128 * (4 * gg + t4)
+                        nc.tensor.matmul_mx(
+                            out=hps[:, t4, :],
+                            lhsT=codes[sl][:, c0 : c0 + 128].bitcast(FP8X4),
+                            lhsT_scale=planes[sl // 4][kk:P, c0 : c0 + 128],
+                            rhs=w1c[:].bitcast(FP8X4),
+                            rhs_scale=w1s[:],
+                            start=True,
+                            stop=True,
+                        )
+
+            def hadd(k):
+                for gg in range(2):
+                    g = 2 * k + gg
+                    nc.vector.tensor_tensor(
+                        out=h[:, 4 * g : 4 * g + 4, :],
+                        in0=hpss[g][:],
+                        in1=bc[:, 0:128].unsqueeze(1).to_broadcast([P, 4, F_OUT]),
+                        op=ALU.add,
+                    )
+
+            def degmm(k, s):
+                t = k - N_X
+                g = t // 4
+                t4 = t % 4
+                if t4 == 0 and s == 0:
+                    dps[g] = psum.tile([P, 4, 4, ND], F32, tag="D", name="D%d" % g)
                 for c in range(8):
                     c0 = 512 * c + 128 * s
                     nc.tensor.matmul(
-                        out=dp[:, t4, s, :],
-                        lhsT=gt[:, c0 : c0 + 128],
+                        out=dps[g][:, t4, s, :],
+                        lhsT=grps[k][:, c0 : c0 + 128],
                         rhs=ones[:, 0:ND],
                         start=(c == 0),
                         stop=(c == 7),
                     )
 
-        def chain1(g):
-            dsb = small.tile([P, 4, 4], F32, tag="dsb", name="dsb%d" % g)
-            dsbs[g] = dsb
-            nc.vector.tensor_copy(out=dsb[:], in_=dps[g][:, :, :, 0].rearrange("p t s -> p s t"))
+            def chain1(g):
+                dsb = small.tile([P, 4, 4], F32, tag="dsb", name="dsb%d" % g)
+                dsbs[g] = dsb
+                nc.vector.tensor_copy(out=dsb[:], in_=dps[g][:, :, :, 0].rearrange("p t s -> p s t"))
 
-        def chain2(g):
-            o2 = psum.tile([P, 4], F32, tag="o2", name="o2_%d" % g)
-            o2s[g] = o2
-            for s in range(4):
-                nc.tensor.matmul(
-                    out=o2[:], lhsT=sel4[:, s, :], rhs=dsbs[g][:, s, :], start=(s == 0), stop=(s == 3)
+            def chain2(g):
+                o2 = psum.tile([P, 4], F32, tag="o2", name="o2_%d" % g)
+                o2s[g] = o2
+                for s in range(4):
+                    nc.tensor.matmul(
+                        out=o2[:], lhsT=sel4[:, s, :], rhs=dsbs[g][:, s, :], start=(s == 0), stop=(s == 3)
+                    )
+
+            def chain3(g):
+                sl = slice(4 * g, 4 * g + 4)
+                nc.vector.tensor_scalar_add(out=deg1[:, sl], in0=o2s[g][:], scalar1=1.0)
+                nc.gpsimd.tensor_tensor(out=dinv[:, sl], in0=deg1[:, sl], in1=mhalf[:], op=ALU.pow)
+                nc.vector.reciprocal(out=rdeg[:, sl], in_=deg1[:, sl])
+
+            def chain4(g):
+                sl = slice(4 * g, 4 * g + 4)
+                hsb = small.tile([P, F_OUT, 4], BF16, tag="hsb", name="hsb%d" % g, align_bytes=64)
+                nc.vector.tensor_tensor(
+                    out=hsb[:],
+                    in0=h[:, sl, :].rearrange("p t f -> p f t"),
+                    in1=dinv[:, sl].unsqueeze(1).to_broadcast([P, F_OUT, 4]),
+                    op=ALU.mult,
+                )
+                nc.vector.tensor_tensor(
+                    out=h[:, sl, :],
+                    in0=h[:, sl, :],
+                    in1=rdeg[:, sl].unsqueeze(2).to_broadcast([P, 4, F_OUT]),
+                    op=ALU.mult,
+                )
+                nc.vector.quantize_mx(
+                    out=hcod[:, 128 * g : 128 * g + 128].bitcast(FP8X4),
+                    scales=hscl[:, 128 * g : 128 * g + 128],
+                    in_=hsb[:].rearrange("p f t -> p (f t)"),
                 )
 
-        def chain3(g):
-            sl = slice(4 * g, 4 * g + 4)
-            nc.vector.tensor_scalar_add(out=deg1[:, sl], in0=o2s[g][:], scalar1=1.0)
-            nc.gpsimd.tensor_tensor(out=dinv[:, sl], in0=deg1[:, sl], in1=mhalf[:], op=ALU.pow)
-            nc.vector.reciprocal(out=rdeg[:, sl], in_=deg1[:, sl])
+            def mx2(acc, g, t4, c):
+                t = 4 * g + t4
+                nc.tensor.matmul_mx(
+                    out=acc[:, t4, :],
+                    lhsT=codes[t][:, 128 * c : 128 * c + 128].bitcast(FP8X4),
+                    lhsT_scale=planes[g][4 * t4 : P, 128 * c : 128 * c + 128],
+                    rhs=hcod[:, 128 * c : 128 * c + 128].bitcast(FP8X4),
+                    rhs_scale=hscl[:, 128 * c : 128 * c + 128],
+                    start=(c == 0),
+                    stop=(c == 7),
+                )
 
-        def chain4(g):
-            sl = slice(4 * g, 4 * g + 4)
-            hsb = small.tile([P, F_OUT, 4], BF16, tag="hsb", name="hsb%d" % g, align_bytes=64)
-            nc.vector.tensor_tensor(
-                out=hsb[:],
-                in0=h[:, sl, :].rearrange("p t f -> p f t"),
-                in1=dinv[:, sl].unsqueeze(1).to_broadcast([P, F_OUT, 4]),
-                op=ALU.mult,
-            )
-            nc.vector.tensor_tensor(
-                out=h[:, sl, :],
-                in0=h[:, sl, :],
-                in1=rdeg[:, sl].unsqueeze(2).to_broadcast([P, 4, F_OUT]),
-                op=ALU.mult,
-            )
-            nc.vector.quantize_mx(
-                out=hcod[:, 128 * g : 128 * g + 128].bitcast(FP8X4),
-                scales=hscl[:, 128 * g : 128 * g + 128],
-                in_=hsb[:].rearrange("p f t -> p (f t)"),
-            )
+            acc_tags = ["xt", "xt", "xt", "xt", "hps", "dm", "D", "o2"]
+            accs = {}
+            n_pre = 6
 
-        def mx2(acc, g, t4, c):
-            t = 4 * g + t4
-            nc.tensor.matmul_mx(
-                out=acc[:, t4, :],
-                lhsT=codes[t][:, 128 * c : 128 * c + 128].bitcast(FP8X4),
-                lhsT_scale=planes[g][4 * t4 : P, 128 * c : 128 * c + 128],
-                rhs=hcod[:, 128 * c : 128 * c + 128].bitcast(FP8X4),
-                rhs_scale=hscl[:, 128 * c : 128 * c + 128],
-                start=(c == 0),
-                stop=(c == 7),
-            )
+            def pre(g):
+                accs[g] = psum.tile(
+                    [P, 4, F_OUT], F32, tag=acc_tags[g], bufs=(4 if g < 4 else 1), name="acc%d" % g
+                )
+                for c in range(7):
+                    mx2(accs[g], g, 0, c)
 
-        acc_tags = ["xt", "xt", "xt", "xt", "xt", "hps", "D", "o2"]
-        accs = {}
-        n_pre = 6
-        with tc.tile_pool(name="natp", bufs=4) as natp, tc.tile_pool(name="grp", bufs=3) as grp:
-            for k in range(4):
-                load(k, natp)
-            for it in range(N_ITEMS + 3):
-                if it < N_ITEMS:
-                    transp(it, grp)
-                    if it + 4 < N_ITEMS:
-                        load(it + 4, natp)
-                k = it - 1
-                if N_X <= k < N_ITEMS:
-                    degmm(k)
-                if 0 <= k < N_ITEMS:
-                    quant(k)
-                if 0 <= it - 2 < N_X:
-                    mx1(it - 2)
-                if it >= 8 and (it - 8) % 4 == 0 and (it - 8) // 4 < N_GROUPS:
-                    chain1((it - 8) // 4)
-                if it >= 9 and (it - 9) % 4 == 0 and (it - 9) // 4 < N_GROUPS:
-                    chain2((it - 9) // 4)
-                    chain3((it - 9) // 4)
-                if it >= 10 and (it - 10) % 4 == 0 and (it - 10) // 4 < N_GROUPS:
-                    chain4((it - 10) // 4)
-                if it == N_ITEMS:
-                    for g in range(n_pre):
-                        accs[g] = psum.tile(
-                            [P, 4, F_OUT], F32, tag=acc_tags[g], bufs=(5 if g < 5 else 1), name="acc%d" % g
-                        )
-                        for c in range(7):
-                            mx2(accs[g], g, 0, c)
+            if PIN:
+                ctx.enter_context(tc.manual_schedule())
 
-        with tc.tile_pool(name="ep", bufs=3) as ep:
-            for g in range(N_GROUPS):
+            if True:
+                for it in range(N_ITEMS + 3):
+                    k = it - 1
+                    if 0 <= k < N_ITEMS:
+                        quant(k)
+                    if 0 <= it - 2 < N_X:
+                        hadd(it - 2)
+                    if it >= 10 and (it - 10) % 4 == 0:
+                        chain4((it - 10) // 4)
+                    has_t = it < N_ITEMS
+                    has_d = N_X <= k < N_ITEMS
+                    if has_t:
+                        transp(it, 0, grp)
+                        transp(it, 1, grp)
+                    if it == 1:
+                        bcps = psum.tile([P, 512], F32, tag="o2", name="bcps")
+                        nc.tensor.matmul(out=bcps[:], lhsT=ones[:], rhs=zrow[:], start=True, stop=True)
+                        nc.vector.tensor_copy(out=bc[:], in_=bcps[:, 0:384])
+                    if has_d:
+                        degmm(k, 0)
+                    if it >= 9 and (it - 9) % 4 == 0:
+                        if it == N_ITEMS + 1:
+                            pre(0)
+                            pre(1)
+                        chain2((it - 9) // 4)
+                    if has_t:
+                        transp(it, 2, grp)
+                    if has_d:
+                        degmm(k, 1)
+                        if has_t:
+                            for w in range(N_HOLD):
+                                hold()
+                        degmm(k, 2)
+                    if has_t:
+                        transp(it, 3, grp)
+                    if has_d:
+                        degmm(k, 3)
+                    if 0 <= k < N_X:
+                        mx1(k)
+                    if it >= 8 and (it - 8) % 4 == 0:
+                        chain1((it - 8) // 4)
+                    if it >= 9 and (it - 9) % 4 == 0:
+                        chain3((it - 9) // 4)
+                    if has_t and it + 4 < N_ITEMS:
+                        load(it + 4)
+                    if it == N_ITEMS + 1:
+                        for g in range(2, n_pre):
+                            pre(g)
+
+            zs = {}
+            gls = {}
+            mvs = {}
+            ves = {}
+            rstds = {}
+            nmrs = {}
+            yns = {}
+            ys = {}
+
+            def main(g):
                 if g < n_pre:
-                    acc = accs[g]
-                    mx2(acc, g, 0, 7)
+                    mx2(accs[g], g, 0, 7)
                 else:
-                    acc = psum.tile([P, 4, F_OUT], F32, tag=acc_tags[g], name="acc%d" % g)
+                    accs[g] = psum.tile([P, 4, F_OUT], F32, tag=acc_tags[g], name="acc%d" % g)
                     for c in range(8):
-                        mx2(acc, g, 0, c)
+                        mx2(accs[g], g, 0, c)
                 for t4 in range(1, 4):
                     for c in range(8):
-                        mx2(acc, g, t4, c)
+                        mx2(accs[g], g, t4, c)
 
-                z = ep.tile([P, 4, F_OUT], F32, tag="z", name="z%d" % g)
+            def e1(g, ep):
+                zs[g] = ep.tile([P, 4, F_OUT], F32, tag="z", bufs=2, name="z%d" % g)
                 for t4 in range(4):
                     t = 4 * g + t4
                     nc.vector.scalar_tensor_tensor(
-                        out=z[:, t4, :],
-                        in0=acc[:, t4, :],
+                        out=zs[g][:, t4, :],
+                        in0=accs[g][:, t4, :],
                         scalar=dinv[:, t : t + 1],
                         in1=h[:, t, :],
                         op0=ALU.mult,
                         op1=ALU.add,
                     )
-                gl = ep.tile([P, 4, F_OUT], F32, tag="gl", name="gl%d" % g)
-                nc.scalar.activation(out=gl[:], in_=z[:], func=ACTF.Gelu)
+
+            def e2(g, ep):
+                gls[g] = ep.tile([P, 4, F_OUT], F32, tag="gl", bufs=3, name="gl%d" % g)
+                nc.scalar.activation(out=gls[g][:], in_=zs[g][:], func=ACTF.Gelu)
+
+            def e3(g):
                 st = small.tile([P, 4, 6], F32, tag="st", name="st%d" % g)
-                mv = small.tile([P, 4, 2], F32, tag="mv", name="mv%d" % g)
+                mvs[g] = small.tile([P, 4, 2], F32, tag="mv", name="mv%d" % g)
                 for t4 in range(4):
-                    nc.vector.bn_stats(out=st[:, t4, :], in_=gl[:, t4, :])
+                    nc.vector.bn_stats(out=st[:, t4, :], in_=gls[g][:, t4, :])
                 for t4 in range(4):
-                    nc.vector.bn_aggr(out=mv[:, t4, :], in_=st[:, t4, :])
-                ve = small.tile([P, 4], F32, tag="ve", name="ve%d" % g)
-                nc.vector.tensor_scalar_add(out=ve[:], in0=mv[:, :, 1], scalar1=EPS)
-                rstd = small.tile([P, 4], F32, tag="rstd", name="rstd%d" % g)
-                nc.gpsimd.tensor_tensor(out=rstd[:], in0=ve[:], in1=mhalf[:], op=ALU.pow)
-                nmr = small.tile([P, 4], F32, tag="nmr", name="nmr%d" % g)
+                    nc.vector.bn_aggr(out=mvs[g][:, t4, :], in_=st[:, t4, :])
+                ves[g] = small.tile([P, 4], F32, tag="ve", name="ve%d" % g)
+                nc.vector.tensor_scalar_add(out=ves[g][:], in0=mvs[g][:, :, 1], scalar1=EPS)
+
+            def e4(g):
+                rstds[g] = small.tile([P, 4], F32, tag="rstd", name="rstd%d" % g)
+                nc.gpsimd.tensor_tensor(out=rstds[g][:], in0=ves[g][:], in1=mhalf[:], op=ALU.pow)
+
+            def e5(g):
+                nmrs[g] = small.tile([P, 4], F32, tag="nmr", name="nmr%d" % g)
                 nc.vector.scalar_tensor_tensor(
-                    out=nmr[:], in0=mv[:, :, 0], scalar=-1.0, in1=rstd[:], op0=ALU.mult, op1=ALU.mult
+                    out=nmrs[g][:],
+                    in0=mvs[g][:, :, 0],
+                    scalar=-1.0,
+                    in1=rstds[g][:],
+                    op0=ALU.mult,
+                    op1=ALU.mult,
                 )
-                yn = ep.tile([P, 4, F_OUT], F32, tag="yn", name="yn%d" % g)
+
+            def e6(g, ep):
+                yns[g] = ep.tile([P, 4, F_OUT], F32, tag="yn", bufs=2, name="yn%d" % g)
                 for t4 in range(4):
                     nc.scalar.activation(
-                        out=yn[:, t4, :],
-                        in_=gl[:, t4, :],
+                        out=yns[g][:, t4, :],
+                        in_=gls[g][:, t4, :],
                         func=ACTF.Identity,
-                        scale=rstd[:, t4 : t4 + 1],
-                        bias=nmr[:, t4 : t4 + 1],
+                        scale=rstds[g][:, t4 : t4 + 1],
+                        bias=nmrs[g][:, t4 : t4 + 1],
                     )
-                y = ep.tile([P, 4, F_OUT], F32, tag="y", name="y%d" % g)
+
+            def e7(g, ep):
+                ys[g] = ep.tile([P, 4, F_OUT], F32, tag="y", bufs=4, name="y%d" % g)
                 nc.gpsimd.tensor_tensor(
-                    out=y[:],
-                    in0=yn[:],
+                    out=ys[g][:],
+                    in0=yns[g][:],
                     in1=bc[:, 128:256].unsqueeze(1).to_broadcast([P, 4, F_OUT]),
                     op=ALU.mult,
                 )
+
+            def e8(g):
                 nc.vector.tensor_tensor(
-                    out=y[:],
-                    in0=y[:],
+                    out=ys[g][:],
+                    in0=ys[g][:],
                     in1=bc[:, 256:384].unsqueeze(1).to_broadcast([P, 4, F_OUT]),
                     op=ALU.add,
                 )
-                nc.sync.dma_start(out=outv[g], in_=y[:].rearrange("p (u e) f -> p u e f", u=2))
+                nc.sync.dma_start(out=outv[g], in_=ys[g][:].rearrange("p (u e) f -> p u e f", u=2))
+
+            def tail():
+                with tc.tile_pool(name="ep", bufs=4) as ep:
+                    for j in range(N_GROUPS + 3):
+                        if j < N_GROUPS:
+                            main(j)
+                            e1(j, ep)
+                        if 0 <= j - 3 < N_GROUPS:
+                            e8(j - 3)
+                        if 0 <= j - 1 < N_GROUPS:
+                            e5(j - 1)
+                        if j < N_GROUPS:
+                            e2(j, ep)
+                        if 0 <= j - 1 < N_GROUPS:
+                            e6(j - 1, ep)
+                        if j < N_GROUPS:
+                            e3(j)
+                            e4(j)
+                        if 0 <= j - 1 < N_GROUPS:
+                            e7(j - 1, ep)
+
+            return tail
+
+        with tc.tile_pool(name="natp", bufs=4) as natp, tc.tile_pool(name="grp", bufs=3) as grp:
+            tail = body(natp, grp)
+        tail()

@@ -10,7 +10,6 @@ U8 = mybir.dt.uint8
 FP8X4 = mybir.dt.float8_e4m3fn_x4
 ALU = mybir.AluOpType
 ACTF = mybir.ActivationFunctionType
-AX = mybir.AxisListType
 
 P = 128
 N_NODES = 4096
@@ -21,10 +20,8 @@ N_TILES = 32
 N_GROUPS = 8
 N_X = 4
 N_ITEMS = N_X + N_TILES
-ND = 12
-PIN = True
-N_WARM = 8
-N_HOLD = 1
+CV = 3072
+XT_BUFS = 6
 
 FLOPS = 2 * N_NODES * K_IN * F_OUT + 2 * N_NODES * N_NODES * F_OUT
 
@@ -43,9 +40,6 @@ def tile_gcnlayer_pa_t_kernel(tc, x, adj, W1, b1, ln_gamma, ln_beta, out):
         def body(natp, grp):
             nats = {}
             grps = {}
-            dps = {}
-            dsbs = {}
-            o2s = {}
             hpss = {}
 
             def load(k):
@@ -68,11 +62,6 @@ def tile_gcnlayer_pa_t_kernel(tc, x, adj, W1, b1, ln_gamma, ln_beta, out):
             for k in range(4):
                 load(k)
 
-            dsrc = grp.tile([P, 4096], BF16, tag="G", name="dsrc", align_bytes=64)
-            nc.vector.memset(dsrc[:, 0:2048], 1.0)
-            dcod = keep.tile([P, 512], U32, name="dcod", align_bytes=64)
-            dscl = keep.tile([P, 512], U8, name="dscl", align_bytes=64)
-            nc.vector.quantize_mx(out=dcod[:].bitcast(FP8X4), scales=dscl[:], in_=dsrc[:, 0:2048])
             ident = keep.tile([P, P], F32, name="ident")
             make_identity(nc, ident[:])
             ones = keep.tile([P, P], BF16, name="ones")
@@ -94,31 +83,6 @@ def tile_gcnlayer_pa_t_kernel(tc, x, adj, W1, b1, ln_gamma, ln_beta, out):
             dmy2 = keep.tile([P, 1], F32, name="dmy2")
             nc.scalar.activation(out=dmy2[:], in_=dmy[:], func=ACTF.Gelu)
 
-            dm = psum.tile([P, 512], F32, tag="dm", name="dm")
-
-            def hold():
-                nc.tensor.matmul_mx(
-                    out=dm[:],
-                    lhsT=dcod[:, 0:128].bitcast(FP8X4),
-                    lhsT_scale=dscl[:, 0:128],
-                    rhs=dcod[:].bitcast(FP8X4),
-                    rhs_scale=dscl[:],
-                    start=True,
-                    stop=True,
-                )
-
-            for w in range(N_WARM):
-                hold()
-
-            rsel = keep.tile([P, 32], F32, name="rsel")
-            nc.vector.tensor_reduce(
-                out=rsel[:], in_=ident[:].rearrange("k (a t) -> k a t", t=4), axis=AX.X, op=ALU.add
-            )
-            sel4 = keep.tile([P, 4, P], F32, name="sel4")
-            nc.vector.memset(sel4[:], 0.0)
-            for s in range(4):
-                nc.vector.tensor_copy(out=sel4[:, s, 32 * s : 32 * s + 32], in_=rsel[:])
-
             w1g = keep.tile([P, F_OUT, 4], BF16, name="w1g", align_bytes=64)
             nc.vector.tensor_copy(out=w1g[:], in_=w1n[:].rearrange("q t f -> q f t"))
             w1c = keep.tile([P, F_OUT], U32, name="w1c", align_bytes=64)
@@ -137,29 +101,48 @@ def tile_gcnlayer_pa_t_kernel(tc, x, adj, W1, b1, ln_gamma, ln_beta, out):
             h = keep.tile([P, N_TILES, F_OUT], F32, name="h")
             hcod = keep.tile([P, N_GROUPS * F_OUT], U32, name="hcod", align_bytes=64)
             hscl = keep.tile([P, N_GROUPS * F_OUT], U8, name="hscl", align_bytes=64)
+            degv = keep.tile([P, N_TILES], F32, name="degv")
+            dega = keep.tile([P, N_TILES], F32, name="dega")
             deg1 = keep.tile([P, N_TILES], F32, name="deg1")
             dinv = keep.tile([P, N_TILES], F32, name="dinv")
             rdeg = keep.tile([P, N_TILES], F32, name="rdeg")
+            junkv = keep.tile([P, CV], BF16, name="junkv")
+            junka = keep.tile([P, 4096 - CV], BF16, name="junka")
 
             def slot_of(k):
                 return k - N_X if k >= N_X else N_TILES - N_X + k
 
-            def transp(k, b, grp):
+            def transp(k, b):
                 if b == 0:
                     grps[k] = grp.tile([P, 4096], BF16, tag="G", name="G%d" % k, align_bytes=64)
                 nat_w = nats[k][:].bitcast(F32)
                 g_w = grps[k][:].bitcast(F32).rearrange("p (c i u) -> p c i u", c=8, i=P, u=2)
-                xt = psum.tile([P, 2, 2, P], F32, tag="xt", bufs=4, name="xt%d_%d" % (k, b))
+                xt = psum.tile([P, 2, 2, P], F32, tag="xt", bufs=XT_BUFS, name="xt%d_%d" % (k, b))
                 for cc in range(2):
                     for u in range(2):
                         w0 = 256 * (2 * b + cc) + 128 * u
                         nc.tensor.transpose(xt[:, cc, u, :], nat_w[:, w0 : w0 + 128], ident[:])
-                src = xt[:].rearrange("p c u i -> p c i u")
-                dst = g_w[:, 2 * b : 2 * b + 2, :, :]
-                if b == 3 and k % 2 == 1:
-                    nc.vector.tensor_copy(out=dst, in_=src)
-                else:
-                    nc.scalar.copy(out=dst, in_=src)
+                nc.scalar.copy(
+                    out=g_w[:, 2 * b : 2 * b + 2, :, :], in_=xt[:].rearrange("p c u i -> p c i u")
+                )
+
+            def sum_v(k):
+                t = k - N_X
+                nc.vector.tensor_scalar(
+                    out=junkv[:],
+                    in0=nats[k][:, 0:CV],
+                    scalar1=1.0,
+                    scalar2=1.0,
+                    op0=ALU.mult,
+                    op1=ALU.add,
+                    accum_out=degv[:, t : t + 1],
+                )
+
+            def sum_a(k):
+                t = k - N_X
+                nc.scalar.activation(
+                    out=junka[:], in_=nats[k][:, CV:4096], func=ACTF.Copy, accum_out=dega[:, t : t + 1]
+                )
 
             def quant(k):
                 sl = slot_of(k)
@@ -176,7 +159,7 @@ def tile_gcnlayer_pa_t_kernel(tc, x, adj, W1, b1, ln_gamma, ln_beta, out):
                 kk = 4 * (sl % 4)
                 for gg in range(2):
                     g = 2 * k + gg
-                    hps = psum.tile([P, 4, F_OUT], F32, tag=("hps" if gg == 0 else "D"), name="hps%d" % g)
+                    hps = psum.tile([P, 4, F_OUT], F32, tag="hps", bufs=2, name="hps%d" % g)
                     hpss[g] = hps
                     for t4 in range(4):
                         c0 = 128 * (4 * gg + t4)
@@ -200,38 +183,9 @@ def tile_gcnlayer_pa_t_kernel(tc, x, adj, W1, b1, ln_gamma, ln_beta, out):
                         op=ALU.add,
                     )
 
-            def degmm(k, s):
-                t = k - N_X
-                g = t // 4
-                t4 = t % 4
-                if t4 == 0 and s == 0:
-                    dps[g] = psum.tile([P, 4, 4, ND], F32, tag="D", name="D%d" % g)
-                for c in range(8):
-                    c0 = 512 * c + 128 * s
-                    nc.tensor.matmul(
-                        out=dps[g][:, t4, s, :],
-                        lhsT=grps[k][:, c0 : c0 + 128],
-                        rhs=ones[:, 0:ND],
-                        start=(c == 0),
-                        stop=(c == 7),
-                    )
-
-            def chain1(g):
-                dsb = small.tile([P, 4, 4], F32, tag="dsb", name="dsb%d" % g)
-                dsbs[g] = dsb
-                nc.vector.tensor_copy(out=dsb[:], in_=dps[g][:, :, :, 0].rearrange("p t s -> p s t"))
-
-            def chain2(g):
-                o2 = psum.tile([P, 4], F32, tag="o2", name="o2_%d" % g)
-                o2s[g] = o2
-                for s in range(4):
-                    nc.tensor.matmul(
-                        out=o2[:], lhsT=sel4[:, s, :], rhs=dsbs[g][:, s, :], start=(s == 0), stop=(s == 3)
-                    )
-
             def chain3(g):
                 sl = slice(4 * g, 4 * g + 4)
-                nc.vector.tensor_scalar_add(out=deg1[:, sl], in0=o2s[g][:], scalar1=1.0)
+                nc.vector.tensor_tensor(out=deg1[:, sl], in0=degv[:, sl], in1=dega[:, sl], op=ALU.add)
                 nc.gpsimd.tensor_tensor(out=dinv[:, sl], in0=deg1[:, sl], in1=mhalf[:], op=ALU.pow)
                 nc.vector.reciprocal(out=rdeg[:, sl], in_=deg1[:, sl])
 
@@ -268,68 +222,47 @@ def tile_gcnlayer_pa_t_kernel(tc, x, adj, W1, b1, ln_gamma, ln_beta, out):
                     stop=(c == 7),
                 )
 
-            acc_tags = ["xt", "xt", "xt", "xt", "hps", "dm", "D", "o2"]
             accs = {}
-            n_pre = 6
 
             def pre(g):
-                accs[g] = psum.tile(
-                    [P, 4, F_OUT], F32, tag=acc_tags[g], bufs=(4 if g < 4 else 1), name="acc%d" % g
-                )
+                if g < XT_BUFS:
+                    accs[g] = psum.tile([P, 4, F_OUT], F32, tag="xt", bufs=XT_BUFS, name="acc%d" % g)
+                else:
+                    accs[g] = psum.tile([P, 4, F_OUT], F32, tag="hps", bufs=2, name="acc%d" % g)
                 for c in range(7):
                     mx2(accs[g], g, 0, c)
 
-            if PIN:
-                ctx.enter_context(tc.manual_schedule())
+            ctx.enter_context(tc.manual_schedule())
 
-            if True:
-                for it in range(N_ITEMS + 3):
-                    k = it - 1
-                    if 0 <= k < N_ITEMS:
-                        quant(k)
-                    if 0 <= it - 2 < N_X:
-                        hadd(it - 2)
-                    if it >= 10 and (it - 10) % 4 == 0:
-                        chain4((it - 10) // 4)
-                    has_t = it < N_ITEMS
-                    has_d = N_X <= k < N_ITEMS
-                    if has_t:
-                        transp(it, 0, grp)
-                        transp(it, 1, grp)
-                    if it == 1:
-                        bcps = psum.tile([P, 512], F32, tag="o2", name="bcps")
-                        nc.tensor.matmul(out=bcps[:], lhsT=ones[:], rhs=zrow[:], start=True, stop=True)
-                        nc.vector.tensor_copy(out=bc[:], in_=bcps[:, 0:384])
-                    if has_d:
-                        degmm(k, 0)
-                    if it >= 9 and (it - 9) % 4 == 0:
-                        if it == N_ITEMS + 1:
-                            pre(0)
-                            pre(1)
-                        chain2((it - 9) // 4)
-                    if has_t:
-                        transp(it, 2, grp)
-                    if has_d:
-                        degmm(k, 1)
-                        if has_t:
-                            for w in range(N_HOLD):
-                                hold()
-                        degmm(k, 2)
-                    if has_t:
-                        transp(it, 3, grp)
-                    if has_d:
-                        degmm(k, 3)
-                    if 0 <= k < N_X:
-                        mx1(k)
-                    if it >= 8 and (it - 8) % 4 == 0:
-                        chain1((it - 8) // 4)
-                    if it >= 9 and (it - 9) % 4 == 0:
-                        chain3((it - 9) // 4)
-                    if has_t and it + 4 < N_ITEMS:
-                        load(it + 4)
-                    if it == N_ITEMS + 1:
-                        for g in range(2, n_pre):
-                            pre(g)
+            for it in range(N_ITEMS + 1):
+                k = it - 1
+                if it >= 8 and (it - 8) % 4 == 0:
+                    chain3((it - 8) // 4)
+                if 0 <= k < N_ITEMS:
+                    quant(k)
+                if 0 <= it - 2 < N_X:
+                    hadd(it - 2)
+                if it >= 8 and (it - 8) % 4 == 0:
+                    chain4((it - 8) // 4)
+                if N_X <= it < N_ITEMS:
+                    sum_v(it)
+                    sum_a(it)
+                if it < N_ITEMS:
+                    transp(it, 0)
+                    transp(it, 1)
+                if it == 1:
+                    bcps = psum.tile([P, 512], F32, tag="hps", bufs=2, name="bcps")
+                    nc.tensor.matmul(out=bcps[:], lhsT=ones[:], rhs=zrow[:], start=True, stop=True)
+                    nc.vector.tensor_copy(out=bc[:], in_=bcps[:, 0:384])
+                if it < N_ITEMS:
+                    transp(it, 2)
+                    transp(it, 3)
+                if 0 <= k < N_X:
+                    mx1(k)
+                if it + 4 < N_ITEMS:
+                    load(it + 4)
+            for g in range(N_GROUPS):
+                pre(g)
 
             zs = {}
             gls = {}
@@ -341,12 +274,7 @@ def tile_gcnlayer_pa_t_kernel(tc, x, adj, W1, b1, ln_gamma, ln_beta, out):
             ys = {}
 
             def main(g):
-                if g < n_pre:
-                    mx2(accs[g], g, 0, 7)
-                else:
-                    accs[g] = psum.tile([P, 4, F_OUT], F32, tag=acc_tags[g], name="acc%d" % g)
-                    for c in range(8):
-                        mx2(accs[g], g, 0, c)
+                mx2(accs[g], g, 0, 7)
                 for t4 in range(1, 4):
                     for c in range(8):
                         mx2(accs[g], g, t4, c)

@@ -10,6 +10,7 @@ U8 = mybir.dt.uint8
 FP8X4 = mybir.dt.float8_e4m3fn_x4
 ALU = mybir.AluOpType
 ACTF = mybir.ActivationFunctionType
+AX = mybir.AxisListType
 
 P = 128
 N_NODES = 4096
@@ -20,8 +21,10 @@ N_TILES = 32
 N_GROUPS = 8
 N_X = 4
 N_ITEMS = N_X + N_TILES
-CV = 3072
-XT_BUFS = 6
+HV = 1280
+PE_CHUNKS = 2
+ND = 32
+XT_BUFS = 4
 
 FLOPS = 2 * N_NODES * K_IN * F_OUT + 2 * N_NODES * N_NODES * F_OUT
 
@@ -41,6 +44,9 @@ def tile_gcnlayer_pa_t_kernel(tc, x, adj, W1, b1, ln_gamma, ln_beta, out):
             nats = {}
             grps = {}
             hpss = {}
+            dps = {}
+            dsbs = {}
+            o2s = {}
 
             def load(k):
                 nat = natp.tile([P, 4096], BF16, tag="nat", name="nat%d" % k)
@@ -83,6 +89,15 @@ def tile_gcnlayer_pa_t_kernel(tc, x, adj, W1, b1, ln_gamma, ln_beta, out):
             dmy2 = keep.tile([P, 1], F32, name="dmy2")
             nc.scalar.activation(out=dmy2[:], in_=dmy[:], func=ACTF.Gelu)
 
+            rsel = keep.tile([P, 32], F32, name="rsel")
+            nc.vector.tensor_reduce(
+                out=rsel[:], in_=ident[:].rearrange("k (a t) -> k a t", t=4), axis=AX.X, op=ALU.add
+            )
+            sel4 = keep.tile([P, 4, P], F32, name="sel4")
+            nc.vector.memset(sel4[:], 0.0)
+            for s in range(4):
+                nc.vector.tensor_copy(out=sel4[:, s, 32 * s : 32 * s + 32], in_=rsel[:])
+
             w1g = keep.tile([P, F_OUT, 4], BF16, name="w1g", align_bytes=64)
             nc.vector.tensor_copy(out=w1g[:], in_=w1n[:].rearrange("q t f -> q f t"))
             w1c = keep.tile([P, F_OUT], U32, name="w1c", align_bytes=64)
@@ -106,8 +121,12 @@ def tile_gcnlayer_pa_t_kernel(tc, x, adj, W1, b1, ln_gamma, ln_beta, out):
             deg1 = keep.tile([P, N_TILES], F32, name="deg1")
             dinv = keep.tile([P, N_TILES], F32, name="dinv")
             rdeg = keep.tile([P, N_TILES], F32, name="rdeg")
-            junkv = keep.tile([P, CV], BF16, name="junkv")
-            junka = keep.tile([P, 4096 - CV], BF16, name="junka")
+            degs = keep.tile([P, N_TILES], F32, name="degs")
+            junkv = keep.tile([P, HV], F32, name="junkv")
+            junka = keep.tile([P, 4096 - 2 * HV], BF16, name="junka")
+
+            def pe_chunks(g):
+                return PE_CHUNKS if g < N_GROUPS - 1 else 0
 
             def slot_of(k):
                 return k - N_X if k >= N_X else N_TILES - N_X + k
@@ -128,11 +147,11 @@ def tile_gcnlayer_pa_t_kernel(tc, x, adj, W1, b1, ln_gamma, ln_beta, out):
 
             def sum_v(k):
                 t = k - N_X
-                nc.vector.tensor_scalar(
+                nc.vector.scalar_tensor_tensor(
                     out=junkv[:],
-                    in0=nats[k][:, 0:CV],
-                    scalar1=1.0,
-                    scalar2=1.0,
+                    in0=nats[k][:, 0:HV],
+                    scalar=1.0,
+                    in1=nats[k][:, HV : 2 * HV],
                     op0=ALU.mult,
                     op1=ALU.add,
                     accum_out=degv[:, t : t + 1],
@@ -140,9 +159,43 @@ def tile_gcnlayer_pa_t_kernel(tc, x, adj, W1, b1, ln_gamma, ln_beta, out):
 
             def sum_a(k):
                 t = k - N_X
+                hi = 4096 - 512 * pe_chunks(t // 4)
                 nc.scalar.activation(
-                    out=junka[:], in_=nats[k][:, CV:4096], func=ACTF.Copy, accum_out=dega[:, t : t + 1]
+                    out=junka[:, 0 : hi - 2 * HV],
+                    in_=nats[k][:, 2 * HV : hi],
+                    func=ACTF.Copy,
+                    accum_out=dega[:, t : t + 1],
                 )
+
+            def degmm(k):
+                t = k - N_X
+                g = t // 4
+                t4 = t % 4
+                if t4 == 0:
+                    dps[g] = psum.tile([P, 4, 4, ND], F32, tag="D", name="D%d" % g)
+                for s in range(4):
+                    for c in range(8 - PE_CHUNKS, 8):
+                        c0 = 512 * c + 128 * s
+                        nc.tensor.matmul(
+                            out=dps[g][:, t4, s, :],
+                            lhsT=grps[k][:, c0 : c0 + 128],
+                            rhs=ones[:, 0:ND],
+                            start=(c == 8 - PE_CHUNKS),
+                            stop=(c == 7),
+                        )
+
+            def chain1(g):
+                dsb = small.tile([P, 4, 4], F32, tag="dsb", name="dsb%d" % g)
+                dsbs[g] = dsb
+                nc.vector.tensor_copy(out=dsb[:], in_=dps[g][:, :, :, 0].rearrange("p t s -> p s t"))
+
+            def chain2(g):
+                o2 = psum.tile([P, 4], F32, tag="o2", name="o2_%d" % g)
+                o2s[g] = o2
+                for s in range(4):
+                    nc.tensor.matmul(
+                        out=o2[:], lhsT=sel4[:, s, :], rhs=dsbs[g][:, s, :], start=(s == 0), stop=(s == 3)
+                    )
 
             def quant(k):
                 sl = slot_of(k)
@@ -185,7 +238,13 @@ def tile_gcnlayer_pa_t_kernel(tc, x, adj, W1, b1, ln_gamma, ln_beta, out):
 
             def chain3(g):
                 sl = slice(4 * g, 4 * g + 4)
-                nc.vector.tensor_tensor(out=deg1[:, sl], in0=degv[:, sl], in1=dega[:, sl], op=ALU.add)
+                nc.vector.tensor_tensor(out=degs[:, sl], in0=degv[:, sl], in1=dega[:, sl], op=ALU.add)
+                if pe_chunks(g) > 0:
+                    nc.vector.scalar_tensor_tensor(
+                        out=deg1[:, sl], in0=o2s[g][:], scalar=1.0, in1=degs[:, sl], op0=ALU.add, op1=ALU.add
+                    )
+                else:
+                    nc.vector.tensor_scalar_add(out=deg1[:, sl], in0=degs[:, sl], scalar1=1.0)
                 nc.gpsimd.tensor_tensor(out=dinv[:, sl], in0=deg1[:, sl], in1=mhalf[:], op=ALU.pow)
                 nc.vector.reciprocal(out=rdeg[:, sl], in_=deg1[:, sl])
 
@@ -224,29 +283,38 @@ def tile_gcnlayer_pa_t_kernel(tc, x, adj, W1, b1, ln_gamma, ln_beta, out):
 
             accs = {}
 
+            acc_tags = [("xt", XT_BUFS)] * XT_BUFS + [("hps", 2), ("hps", 2), ("D", 1), ("o2", 1)]
+
             def pre(g):
-                if g < XT_BUFS:
-                    accs[g] = psum.tile([P, 4, F_OUT], F32, tag="xt", bufs=XT_BUFS, name="acc%d" % g)
-                else:
-                    accs[g] = psum.tile([P, 4, F_OUT], F32, tag="hps", bufs=2, name="acc%d" % g)
+                accs[g] = psum.tile(
+                    [P, 4, F_OUT], F32, tag=acc_tags[g][0], bufs=acc_tags[g][1], name="acc%d" % g
+                )
                 for c in range(7):
                     mx2(accs[g], g, 0, c)
 
             ctx.enter_context(tc.manual_schedule())
 
+            last = N_GROUPS - 1
             for it in range(N_ITEMS + 1):
                 k = it - 1
-                if it >= 8 and (it - 8) % 4 == 0:
-                    chain3((it - 8) // 4)
+                g8 = (it - 8) // 4 if (it >= 8 and (it - 8) % 4 == 0) else -1
+                g9 = (it - 9) // 4 if (it >= 9 and (it - 9) % 4 == 0) else -1
+                if g8 == last:
+                    chain3(last)
                 if 0 <= k < N_ITEMS:
                     quant(k)
                 if 0 <= it - 2 < N_X:
                     hadd(it - 2)
-                if it >= 8 and (it - 8) % 4 == 0:
-                    chain4((it - 8) // 4)
+                if g8 == last:
+                    chain4(last)
+                if 0 <= g9 < last:
+                    chain2(g9)
+                    chain3(g9)
                 if N_X <= it < N_ITEMS:
                     sum_v(it)
                     sum_a(it)
+                if 0 <= g9 < last:
+                    chain4(g9)
                 if it < N_ITEMS:
                     transp(it, 0)
                     transp(it, 1)
@@ -254,6 +322,10 @@ def tile_gcnlayer_pa_t_kernel(tc, x, adj, W1, b1, ln_gamma, ln_beta, out):
                     bcps = psum.tile([P, 512], F32, tag="hps", bufs=2, name="bcps")
                     nc.tensor.matmul(out=bcps[:], lhsT=ones[:], rhs=zrow[:], start=True, stop=True)
                     nc.vector.tensor_copy(out=bc[:], in_=bcps[:, 0:384])
+                if N_X <= k < N_ITEMS and pe_chunks((k - N_X) // 4) > 0:
+                    degmm(k)
+                if 0 <= g8 < last:
+                    chain1(g8)
                 if it < N_ITEMS:
                     transp(it, 2)
                     transp(it, 3)

@@ -82,12 +82,10 @@ def tile_gcnlayer_pa_t_kernel(tc, x, adj, W1, b1, ln_gamma, ln_beta, out):
             nc.scalar.dma_start(out=zrow[0:1, 0:128], in_=b1.rearrange("(o f) -> o f", o=1))
             nc.scalar.dma_start(out=zrow[0:1, 128:256], in_=ln_gamma.rearrange("(o f) -> o f", o=1))
             nc.scalar.dma_start(out=zrow[0:1, 256:384], in_=ln_beta.rearrange("(o f) -> o f", o=1))
-            mhalf = keep.tile([P, 4], F32, name="mhalf")
-            nc.vector.memset(mhalf[:], -0.5)
             dmy = keep.tile([P, 1], F32, name="dmy")
-            nc.vector.memset(dmy[:], 0.0)
+            nc.vector.memset(dmy[:], 1.0)
             dmy2 = keep.tile([P, 1], F32, name="dmy2")
-            nc.scalar.activation(out=dmy2[:], in_=dmy[:], func=ACTF.Gelu)
+            nc.scalar.activation(out=dmy2[:], in_=dmy[:], func=ACTF.Sqrt)
 
             rsel = keep.tile([P, 32], F32, name="rsel")
             nc.vector.tensor_reduce(
@@ -121,6 +119,7 @@ def tile_gcnlayer_pa_t_kernel(tc, x, adj, W1, b1, ln_gamma, ln_beta, out):
             deg1 = keep.tile([P, N_TILES], F32, name="deg1")
             dinv = keep.tile([P, N_TILES], F32, name="dinv")
             rdeg = keep.tile([P, N_TILES], F32, name="rdeg")
+            sqd = keep.tile([P, N_TILES], F32, name="sqd")
             degs = keep.tile([P, N_TILES], F32, name="degs")
             junkv = keep.tile([P, HV], F32, name="junkv")
             junka = keep.tile([P, 4096 - 2 * HV], BF16, name="junka")
@@ -236,7 +235,7 @@ def tile_gcnlayer_pa_t_kernel(tc, x, adj, W1, b1, ln_gamma, ln_beta, out):
                         op=ALU.add,
                     )
 
-            def chain3(g):
+            def chain3a(g):
                 sl = slice(4 * g, 4 * g + 4)
                 nc.vector.tensor_tensor(out=degs[:, sl], in0=degv[:, sl], in1=dega[:, sl], op=ALU.add)
                 if pe_chunks(g) > 0:
@@ -245,8 +244,15 @@ def tile_gcnlayer_pa_t_kernel(tc, x, adj, W1, b1, ln_gamma, ln_beta, out):
                     )
                 else:
                     nc.vector.tensor_scalar_add(out=deg1[:, sl], in0=degs[:, sl], scalar1=1.0)
-                nc.gpsimd.tensor_tensor(out=dinv[:, sl], in0=deg1[:, sl], in1=mhalf[:], op=ALU.pow)
+
+            def chain3s(g):
+                sl = slice(4 * g, 4 * g + 4)
+                nc.scalar.activation(out=sqd[:, sl], in_=deg1[:, sl], func=ACTF.Sqrt)
+
+            def chain3b(g):
+                sl = slice(4 * g, 4 * g + 4)
                 nc.vector.reciprocal(out=rdeg[:, sl], in_=deg1[:, sl])
+                nc.vector.reciprocal(out=dinv[:, sl], in_=sqd[:, sl])
 
             def chain4(g):
                 sl = slice(4 * g, 4 * g + 4)
@@ -300,24 +306,29 @@ def tile_gcnlayer_pa_t_kernel(tc, x, adj, W1, b1, ln_gamma, ln_beta, out):
                 g8 = (it - 8) // 4 if (it >= 8 and (it - 8) % 4 == 0) else -1
                 g9 = (it - 9) // 4 if (it >= 9 and (it - 9) % 4 == 0) else -1
                 if g8 == last:
-                    chain3(last)
+                    chain3a(last)
+                    chain3s(last)
+                    nc.scalar.activation(out=dmy2[:], in_=dmy[:], func=ACTF.Gelu)
                 if 0 <= k < N_ITEMS:
                     quant(k)
                 if 0 <= it - 2 < N_X:
                     hadd(it - 2)
                 if g8 == last:
+                    chain3b(last)
                     chain4(last)
                 if 0 <= g9 < last:
                     chain2(g9)
-                    chain3(g9)
+                    chain3a(g9)
                 if N_X <= it < N_ITEMS:
                     sum_v(it)
                     sum_a(it)
-                if 0 <= g9 < last:
-                    chain4(g9)
                 if it < N_ITEMS:
                     transp(it, 0)
                     transp(it, 1)
+                if 0 <= g9 < last:
+                    chain3s(g9)
+                    chain3b(g9)
+                    chain4(g9)
                 if it == 1:
                     bcps = psum.tile([P, 512], F32, tag="hps", bufs=2, name="bcps")
                     nc.tensor.matmul(out=bcps[:], lhsT=ones[:], rhs=zrow[:], start=True, stop=True)
@@ -338,12 +349,12 @@ def tile_gcnlayer_pa_t_kernel(tc, x, adj, W1, b1, ln_gamma, ln_beta, out):
 
             zs = {}
             gls = {}
-            mvs = {}
-            ves = {}
-            rstds = {}
-            nmrs = {}
-            yns = {}
             ys = {}
+            mvall = keep.tile([P, N_TILES, 2], F32, name="mvall")
+            veall = keep.tile([P, N_TILES], F32, name="veall")
+            sdall = keep.tile([P, N_TILES], F32, name="sdall")
+            rstd = keep.tile([P, N_TILES], F32, name="rstd")
+            nmr = keep.tile([P, N_TILES], F32, name="nmr")
 
             def main(g):
                 mx2(accs[g], g, 0, 7)
@@ -352,7 +363,7 @@ def tile_gcnlayer_pa_t_kernel(tc, x, adj, W1, b1, ln_gamma, ln_beta, out):
                         mx2(accs[g], g, t4, c)
 
             def e1(g, ep):
-                zs[g] = ep.tile([P, 4, F_OUT], F32, tag="z", bufs=2, name="z%d" % g)
+                zs[g] = ep.tile([P, 4, F_OUT], F32, tag="z", bufs=3, name="z%d" % g)
                 for t4 in range(4):
                     t = 4 * g + t4
                     nc.vector.scalar_tensor_tensor(
@@ -365,50 +376,33 @@ def tile_gcnlayer_pa_t_kernel(tc, x, adj, W1, b1, ln_gamma, ln_beta, out):
                     )
 
             def e2(g, ep):
-                gls[g] = ep.tile([P, 4, F_OUT], F32, tag="gl", bufs=3, name="gl%d" % g)
+                gls[g] = ep.tile([P, 4, F_OUT], F32, tag="gl", bufs=N_GROUPS, name="gl%d" % g)
                 nc.scalar.activation(out=gls[g][:], in_=zs[g][:], func=ACTF.Gelu)
 
             def e3(g):
                 st = small.tile([P, 4, 6], F32, tag="st", name="st%d" % g)
-                mvs[g] = small.tile([P, 4, 2], F32, tag="mv", name="mv%d" % g)
                 for t4 in range(4):
                     nc.vector.bn_stats(out=st[:, t4, :], in_=gls[g][:, t4, :])
                 for t4 in range(4):
-                    nc.vector.bn_aggr(out=mvs[g][:, t4, :], in_=st[:, t4, :])
-                ves[g] = small.tile([P, 4], F32, tag="ve", name="ve%d" % g)
-                nc.vector.tensor_scalar_add(out=ves[g][:], in0=mvs[g][:, :, 1], scalar1=EPS)
-
-            def e4(g):
-                rstds[g] = small.tile([P, 4], F32, tag="rstd", name="rstd%d" % g)
-                nc.gpsimd.tensor_tensor(out=rstds[g][:], in0=ves[g][:], in1=mhalf[:], op=ALU.pow)
-
-            def e5(g):
-                nmrs[g] = small.tile([P, 4], F32, tag="nmr", name="nmr%d" % g)
-                nc.vector.scalar_tensor_tensor(
-                    out=nmrs[g][:],
-                    in0=mvs[g][:, :, 0],
-                    scalar=-1.0,
-                    in1=rstds[g][:],
-                    op0=ALU.mult,
-                    op1=ALU.mult,
-                )
+                    nc.vector.bn_aggr(out=mvall[:, 4 * g + t4, :], in_=st[:, t4, :])
 
             def e6(g, ep):
-                yns[g] = ep.tile([P, 4, F_OUT], F32, tag="yn", bufs=2, name="yn%d" % g)
+                ys[g] = ep.tile([P, 4, F_OUT], F32, tag="y", bufs=4, name="y%d" % g)
                 for t4 in range(4):
+                    t = 4 * g + t4
                     nc.scalar.activation(
-                        out=yns[g][:, t4, :],
+                        out=ys[g][:, t4, :],
                         in_=gls[g][:, t4, :],
                         func=ACTF.Identity,
-                        scale=rstds[g][:, t4 : t4 + 1],
-                        bias=nmrs[g][:, t4 : t4 + 1],
+                        scale=rstd[:, t : t + 1],
+                        bias=nmr[:, t : t + 1],
                     )
 
-            def e7(g, ep):
-                ys[g] = ep.tile([P, 4, F_OUT], F32, tag="y", bufs=4, name="y%d" % g)
-                nc.gpsimd.tensor_tensor(
+            def e7(g):
+                eng = nc.gpsimd if g % 2 == 0 else nc.vector
+                eng.tensor_tensor(
                     out=ys[g][:],
-                    in0=yns[g][:],
+                    in0=ys[g][:],
                     in1=bc[:, 128:256].unsqueeze(1).to_broadcast([P, 4, F_OUT]),
                     op=ALU.mult,
                 )
@@ -424,23 +418,26 @@ def tile_gcnlayer_pa_t_kernel(tc, x, adj, W1, b1, ln_gamma, ln_beta, out):
 
             def tail():
                 with tc.tile_pool(name="ep", bufs=4) as ep:
-                    for j in range(N_GROUPS + 3):
+                    for j in range(N_GROUPS + 1):
                         if j < N_GROUPS:
                             main(j)
                             e1(j, ep)
-                        if 0 <= j - 3 < N_GROUPS:
-                            e8(j - 3)
-                        if 0 <= j - 1 < N_GROUPS:
-                            e5(j - 1)
-                        if j < N_GROUPS:
                             e2(j, ep)
-                        if 0 <= j - 1 < N_GROUPS:
-                            e6(j - 1, ep)
+                        if j >= 1:
+                            e3(j - 1)
+                    nc.vector.tensor_scalar_add(out=veall[:], in0=mvall[:, :, 1], scalar1=EPS)
+                    nc.scalar.activation(out=sdall[:], in_=veall[:], func=ACTF.Sqrt)
+                    nc.vector.reciprocal(out=rstd[:], in_=sdall[:])
+                    nc.vector.scalar_tensor_tensor(
+                        out=nmr[:], in0=mvall[:, :, 0], scalar=-1.0, in1=rstd[:], op0=ALU.mult, op1=ALU.mult
+                    )
+                    for j in range(N_GROUPS + 2):
                         if j < N_GROUPS:
-                            e3(j)
-                            e4(j)
+                            e6(j, ep)
                         if 0 <= j - 1 < N_GROUPS:
-                            e7(j - 1, ep)
+                            e7(j - 1)
+                        if 0 <= j - 2 < N_GROUPS:
+                            e8(j - 2)
 
             return tail
 

@@ -21,8 +21,8 @@ N_TILES = 32
 N_GROUPS = 8
 N_X = 4
 N_ITEMS = N_X + N_TILES
-HV = 1280
-PE_CHUNKS = 2
+HV = 1024
+PE_CHUNKS = 3
 ND = 32
 XT_BUFS = 4
 
@@ -196,10 +196,10 @@ def tile_gcnlayer_pa_t_kernel(tc, x, adj, W1, b1, ln_gamma, ln_beta, out):
                         out=o2[:], lhsT=sel4[:, s, :], rhs=dsbs[g][:, s, :], start=(s == 0), stop=(s == 3)
                     )
 
-            def quant(k):
+            def quant(k, halves=(0, 1)):
                 sl = slot_of(k)
                 kk = 4 * (sl % 4)
-                for hf in range(2):
+                for hf in halves:
                     nc.vector.quantize_mx(
                         out=codes[sl][:, 512 * hf : 512 * hf + 512].bitcast(FP8X4),
                         scales=planes[sl // 4][kk:P, 512 * hf : 512 * hf + 512],
@@ -254,7 +254,7 @@ def tile_gcnlayer_pa_t_kernel(tc, x, adj, W1, b1, ln_gamma, ln_beta, out):
                 nc.vector.reciprocal(out=rdeg[:, sl], in_=deg1[:, sl])
                 nc.vector.reciprocal(out=dinv[:, sl], in_=sqd[:, sl])
 
-            def chain4(g):
+            def chain4(g, between=None):
                 sl = slice(4 * g, 4 * g + 4)
                 hsb = small.tile([P, F_OUT, 4], BF16, tag="hsb", name="hsb%d" % g, align_bytes=64)
                 nc.vector.tensor_tensor(
@@ -263,17 +263,25 @@ def tile_gcnlayer_pa_t_kernel(tc, x, adj, W1, b1, ln_gamma, ln_beta, out):
                     in1=dinv[:, sl].unsqueeze(1).to_broadcast([P, F_OUT, 4]),
                     op=ALU.mult,
                 )
+                if between is not None:
+                    quant(between, (1,))
+                    nc.vector.quantize_mx(
+                        out=hcod[:, 128 * g : 128 * g + 128].bitcast(FP8X4),
+                        scales=hscl[:, 128 * g : 128 * g + 128],
+                        in_=hsb[:].rearrange("p f t -> p (f t)"),
+                    )
                 nc.vector.tensor_tensor(
                     out=h[:, sl, :],
                     in0=h[:, sl, :],
                     in1=rdeg[:, sl].unsqueeze(2).to_broadcast([P, 4, F_OUT]),
                     op=ALU.mult,
                 )
-                nc.vector.quantize_mx(
-                    out=hcod[:, 128 * g : 128 * g + 128].bitcast(FP8X4),
-                    scales=hscl[:, 128 * g : 128 * g + 128],
-                    in_=hsb[:].rearrange("p f t -> p (f t)"),
-                )
+                if between is None:
+                    nc.vector.quantize_mx(
+                        out=hcod[:, 128 * g : 128 * g + 128].bitcast(FP8X4),
+                        scales=hscl[:, 128 * g : 128 * g + 128],
+                        in_=hsb[:].rearrange("p f t -> p (f t)"),
+                    )
 
             def mx2(acc, g, t4, c):
                 t = 4 * g + t4
@@ -309,13 +317,14 @@ def tile_gcnlayer_pa_t_kernel(tc, x, adj, W1, b1, ln_gamma, ln_beta, out):
                     chain3a(last)
                     chain3s(last)
                     nc.scalar.activation(out=dmy2[:], in_=dmy[:], func=ACTF.Gelu)
-                if 0 <= k < N_ITEMS:
+                if 0 <= k < N_ITEMS - 1:
                     quant(k)
                 if 0 <= it - 2 < N_X:
                     hadd(it - 2)
                 if g8 == last:
+                    quant(k, (0,))
                     chain3b(last)
-                    chain4(last)
+                    chain4(last, k)
                 if 0 <= g9 < last:
                     chain2(g9)
                     chain3a(g9)
@@ -354,7 +363,7 @@ def tile_gcnlayer_pa_t_kernel(tc, x, adj, W1, b1, ln_gamma, ln_beta, out):
             veall = keep.tile([P, N_TILES], F32, name="veall")
             sdall = keep.tile([P, N_TILES], F32, name="sdall")
             rstd = keep.tile([P, N_TILES], F32, name="rstd")
-            nmr = keep.tile([P, N_TILES], F32, name="nmr")
+            nmu = keep.tile([P, N_TILES], F32, name="nmu")
 
             def main(g):
                 mx2(accs[g], g, 0, 7)
@@ -386,7 +395,50 @@ def tile_gcnlayer_pa_t_kernel(tc, x, adj, W1, b1, ln_gamma, ln_beta, out):
                 for t4 in range(4):
                     nc.vector.bn_aggr(out=mvall[:, 4 * g + t4, :], in_=st[:, t4, :])
 
-            def e6(g, ep):
+            def centre(g):
+                sl = slice(4 * g, 4 * g + 4)
+                nc.vector.tensor_scalar_mul(out=nmu[:, sl], in0=mvall[:, sl, 0], scalar1=-1.0)
+                for t4 in range(4):
+                    t = 4 * g + t4
+                    nc.scalar.activation(
+                        out=gls[g][:, t4, :],
+                        in_=gls[g][:, t4, :],
+                        func=ACTF.Identity,
+                        bias=nmu[:, t : t + 1],
+                    )
+                nc.gpsimd.tensor_tensor(
+                    out=gls[g][:],
+                    in0=gls[g][:],
+                    in1=bc[:, 128:256].unsqueeze(1).to_broadcast([P, 4, F_OUT]),
+                    op=ALU.mult,
+                )
+
+            def centre_v(g):
+                for t4 in range(4):
+                    t = 4 * g + t4
+                    nc.vector.scalar_tensor_tensor(
+                        out=gls[g][:, t4, :],
+                        in0=gls[g][:, t4, :],
+                        scalar=mvall[:, t, 0:1],
+                        in1=bc[:, 128:256],
+                        op0=ALU.subtract,
+                        op1=ALU.mult,
+                    )
+
+            def finish_v(g, ep):
+                ys[g] = ep.tile([P, 4, F_OUT], F32, tag="y", bufs=4, name="y%d" % g)
+                for t4 in range(4):
+                    t = 4 * g + t4
+                    nc.vector.scalar_tensor_tensor(
+                        out=ys[g][:, t4, :],
+                        in0=gls[g][:, t4, :],
+                        scalar=rstd[:, t : t + 1],
+                        in1=bc[:, 256:384],
+                        op0=ALU.mult,
+                        op1=ALU.add,
+                    )
+
+            def finish_a(g, ep):
                 ys[g] = ep.tile([P, 4, F_OUT], F32, tag="y", bufs=4, name="y%d" % g)
                 for t4 in range(4):
                     t = 4 * g + t4
@@ -395,25 +447,17 @@ def tile_gcnlayer_pa_t_kernel(tc, x, adj, W1, b1, ln_gamma, ln_beta, out):
                         in_=gls[g][:, t4, :],
                         func=ACTF.Identity,
                         scale=rstd[:, t : t + 1],
-                        bias=nmr[:, t : t + 1],
                     )
 
-            def e7(g):
-                eng = nc.gpsimd if g % 2 == 0 else nc.vector
-                eng.tensor_tensor(
-                    out=ys[g][:],
-                    in0=ys[g][:],
-                    in1=bc[:, 128:256].unsqueeze(1).to_broadcast([P, 4, F_OUT]),
-                    op=ALU.mult,
-                )
-
-            def e8(g):
-                nc.vector.tensor_tensor(
+            def finish_p(g):
+                nc.gpsimd.tensor_tensor(
                     out=ys[g][:],
                     in0=ys[g][:],
                     in1=bc[:, 256:384].unsqueeze(1).to_broadcast([P, 4, F_OUT]),
                     op=ALU.add,
                 )
+
+            def store(g):
                 nc.sync.dma_start(out=outv[g], in_=ys[g][:].rearrange("p (u e) f -> p u e f", u=2))
 
             def tail():
@@ -425,19 +469,31 @@ def tile_gcnlayer_pa_t_kernel(tc, x, adj, W1, b1, ln_gamma, ln_beta, out):
                             e2(j, ep)
                         if j >= 1:
                             e3(j - 1)
+                            if j < N_GROUPS:
+                                centre(j - 1)
                     nc.vector.tensor_scalar_add(out=veall[:], in0=mvall[:, :, 1], scalar1=EPS)
                     nc.scalar.activation(out=sdall[:], in_=veall[:], func=ACTF.Sqrt)
+                    centre_v(N_GROUPS - 1)
                     nc.vector.reciprocal(out=rstd[:], in_=sdall[:])
-                    nc.vector.scalar_tensor_tensor(
-                        out=nmr[:], in0=mvall[:, :, 0], scalar=-1.0, in1=rstd[:], op0=ALU.mult, op1=ALU.mult
-                    )
-                    for j in range(N_GROUPS + 2):
-                        if j < N_GROUPS:
-                            e6(j, ep)
-                        if 0 <= j - 1 < N_GROUPS:
-                            e7(j - 1)
-                        if 0 <= j - 2 < N_GROUPS:
-                            e8(j - 2)
+                    finish_a(0, ep)
+                    finish_v(1, ep)
+                    store(1)
+                    finish_p(0)
+                    store(0)
+                    finish_a(2, ep)
+                    finish_v(3, ep)
+                    store(3)
+                    finish_p(2)
+                    store(2)
+                    finish_a(4, ep)
+                    finish_v(5, ep)
+                    store(5)
+                    finish_p(4)
+                    store(4)
+                    finish_v(6, ep)
+                    store(6)
+                    finish_v(7, ep)
+                    store(7)
 
             return tail
 

@@ -22,6 +22,7 @@ N_GROUPS = 8
 N_X = 4
 N_ITEMS = N_X + N_TILES
 HV = 1024
+HV_LAST = 1536
 PE_CHUNKS = 3
 ND = 32
 XT_BUFS = 4
@@ -121,8 +122,11 @@ def tile_gcnlayer_pa_t_kernel(tc, x, adj, W1, b1, ln_gamma, ln_beta, out):
             rdeg = keep.tile([P, N_TILES], F32, name="rdeg")
             sqd = keep.tile([P, N_TILES], F32, name="sqd")
             degs = keep.tile([P, N_TILES], F32, name="degs")
-            junkv = keep.tile([P, HV], F32, name="junkv")
-            junka = keep.tile([P, 4096 - 2 * HV], BF16, name="junka")
+            junkv = keep.tile([P, HV_LAST], F32, name="junkv")
+            junka = keep.tile([P, 1024], BF16, name="junka")
+
+            def hv_of(g):
+                return HV if g < N_GROUPS - 1 else HV_LAST
 
             def pe_chunks(g):
                 return PE_CHUNKS if g < N_GROUPS - 1 else 0
@@ -146,11 +150,12 @@ def tile_gcnlayer_pa_t_kernel(tc, x, adj, W1, b1, ln_gamma, ln_beta, out):
 
             def sum_v(k):
                 t = k - N_X
+                hv = hv_of(t // 4)
                 nc.vector.scalar_tensor_tensor(
-                    out=junkv[:],
-                    in0=nats[k][:, 0:HV],
+                    out=junkv[:, 0:hv],
+                    in0=nats[k][:, 0:hv],
                     scalar=1.0,
-                    in1=nats[k][:, HV : 2 * HV],
+                    in1=nats[k][:, hv : 2 * hv],
                     op0=ALU.mult,
                     op1=ALU.add,
                     accum_out=degv[:, t : t + 1],
@@ -159,9 +164,10 @@ def tile_gcnlayer_pa_t_kernel(tc, x, adj, W1, b1, ln_gamma, ln_beta, out):
             def sum_a(k):
                 t = k - N_X
                 hi = 4096 - 512 * pe_chunks(t // 4)
+                hv = hv_of(t // 4)
                 nc.scalar.activation(
-                    out=junka[:, 0 : hi - 2 * HV],
-                    in_=nats[k][:, 2 * HV : hi],
+                    out=junka[:, 0 : hi - 2 * hv],
+                    in_=nats[k][:, 2 * hv : hi],
                     func=ACTF.Copy,
                     accum_out=dega[:, t : t + 1],
                 )
@@ -313,6 +319,7 @@ def tile_gcnlayer_pa_t_kernel(tc, x, adj, W1, b1, ln_gamma, ln_beta, out):
                 k = it - 1
                 g8 = (it - 8) // 4 if (it >= 8 and (it - 8) % 4 == 0) else -1
                 g9 = (it - 9) // 4 if (it >= 9 and (it - 9) % 4 == 0) else -1
+                g10 = (it - 10) // 4 if (it >= 10 and (it - 10) % 4 == 0) else -1
                 if g8 == last:
                     chain3a(last)
                     chain3s(last)
@@ -325,23 +332,21 @@ def tile_gcnlayer_pa_t_kernel(tc, x, adj, W1, b1, ln_gamma, ln_beta, out):
                     quant(k, (0,))
                     chain3b(last)
                     chain4(last, k)
-                if 0 <= g9 < last:
-                    chain2(g9)
-                    chain3a(g9)
+                if 0 <= g10 < last:
+                    chain3b(g10)
+                    chain4(g10)
                 if N_X <= it < N_ITEMS:
                     sum_v(it)
                     sum_a(it)
                 if it < N_ITEMS:
                     transp(it, 0)
                     transp(it, 1)
-                if 0 <= g9 < last:
-                    chain3s(g9)
-                    chain3b(g9)
-                    chain4(g9)
                 if it == 1:
                     bcps = psum.tile([P, 512], F32, tag="hps", bufs=2, name="bcps")
                     nc.tensor.matmul(out=bcps[:], lhsT=ones[:], rhs=zrow[:], start=True, stop=True)
                     nc.vector.tensor_copy(out=bc[:], in_=bcps[:, 0:384])
+                if 0 <= g9 < last:
+                    chain2(g9)
                 if N_X <= k < N_ITEMS and pe_chunks((k - N_X) // 4) > 0:
                     degmm(k)
                 if 0 <= g8 < last:
@@ -349,6 +354,9 @@ def tile_gcnlayer_pa_t_kernel(tc, x, adj, W1, b1, ln_gamma, ln_beta, out):
                 if it < N_ITEMS:
                     transp(it, 2)
                     transp(it, 3)
+                if 0 <= g9 < last:
+                    chain3a(g9)
+                    chain3s(g9)
                 if 0 <= k < N_X:
                     mx1(k)
                 if it + 4 < N_ITEMS:

@@ -23,8 +23,8 @@ N_X = 4
 N_ITEMS = N_X + N_TILES
 HV = 1024
 HV_LAST = 1536
-PE_CHUNKS = 3
-ND = 32
+PE_CHUNKS = 4
+ND = 24
 XT_BUFS = 4
 
 FLOPS = 2 * N_NODES * K_IN * F_OUT + 2 * N_NODES * N_NODES * F_OUT
@@ -172,6 +172,23 @@ def tile_gcnlayer_pa_t_kernel(tc, x, adj, W1, b1, ln_gamma, ln_beta, out):
                     accum_out=dega[:, t : t + 1],
                 )
 
+            def warm(k, n):
+                for i in range(n):
+                    wps = psum.tile([P, 512], F32, tag="hps", bufs=2, name="warm%d_%d" % (k, i))
+                    if k < N_ITEMS - 5:
+                        c, p = codes[N_TILES - N_X], planes[N_GROUPS - 1]
+                    else:
+                        c, p = hcod, hscl
+                    nc.tensor.matmul_mx(
+                        out=wps[:],
+                        lhsT=c[:, 0:128].bitcast(FP8X4),
+                        lhsT_scale=p[:, 0:128],
+                        rhs=c[:, 0:512].bitcast(FP8X4),
+                        rhs_scale=p[:, 0:512],
+                        start=True,
+                        stop=True,
+                    )
+
             def degmm(k):
                 t = k - N_X
                 g = t // 4
@@ -243,12 +260,12 @@ def tile_gcnlayer_pa_t_kernel(tc, x, adj, W1, b1, ln_gamma, ln_beta, out):
 
             def chain3a(g):
                 sl = slice(4 * g, 4 * g + 4)
-                nc.vector.tensor_tensor(out=degs[:, sl], in0=degv[:, sl], in1=dega[:, sl], op=ALU.add)
                 if pe_chunks(g) > 0:
                     nc.vector.scalar_tensor_tensor(
-                        out=deg1[:, sl], in0=o2s[g][:], scalar=1.0, in1=degs[:, sl], op0=ALU.add, op1=ALU.add
+                        out=deg1[:, sl], in0=o2s[g][:], scalar=1.0, in1=degv[:, sl], op0=ALU.add, op1=ALU.add
                     )
                 else:
+                    nc.vector.tensor_tensor(out=degs[:, sl], in0=degv[:, sl], in1=dega[:, sl], op=ALU.add)
                     nc.vector.tensor_scalar_add(out=deg1[:, sl], in0=degs[:, sl], scalar1=1.0)
 
             def chain3s(g):
@@ -337,10 +354,11 @@ def tile_gcnlayer_pa_t_kernel(tc, x, adj, W1, b1, ln_gamma, ln_beta, out):
                     chain4(g10)
                 if N_X <= it < N_ITEMS:
                     sum_v(it)
-                    sum_a(it)
+                    if pe_chunks((it - N_X) // 4) == 0:
+                        sum_a(it)
                 if it < N_ITEMS:
-                    transp(it, 0)
-                    transp(it, 1)
+                    for b in range(4):
+                        transp(it, b)
                 if it == 1:
                     bcps = psum.tile([P, 512], F32, tag="hps", bufs=2, name="bcps")
                     nc.tensor.matmul(out=bcps[:], lhsT=ones[:], rhs=zrow[:], start=True, stop=True)
@@ -349,11 +367,10 @@ def tile_gcnlayer_pa_t_kernel(tc, x, adj, W1, b1, ln_gamma, ln_beta, out):
                     chain2(g9)
                 if N_X <= k < N_ITEMS and pe_chunks((k - N_X) // 4) > 0:
                     degmm(k)
+                if N_X <= k < N_ITEMS - 1:
+                    warm(k, 3)
                 if 0 <= g8 < last:
                     chain1(g8)
-                if it < N_ITEMS:
-                    transp(it, 2)
-                    transp(it, 3)
                 if 0 <= g9 < last:
                     chain3a(g9)
                     chain3s(g9)

@@ -21,9 +21,9 @@ N_TILES = 32
 N_GROUPS = 8
 N_X = 4
 N_ITEMS = N_X + N_TILES
-HV = 1024
+HV = 768
 HV_LAST = 1536
-PE_CHUNKS = 4
+PE_CHUNKS = 5
 ND = 24
 XT_BUFS = 4
 
@@ -119,7 +119,6 @@ def tile_gcnlayer_pa_t_kernel(tc, x, adj, W1, b1, ln_gamma, ln_beta, out):
             dega = keep.tile([P, N_TILES], F32, name="dega")
             deg1 = keep.tile([P, N_TILES], F32, name="deg1")
             dinv = keep.tile([P, N_TILES], F32, name="dinv")
-            rdeg = keep.tile([P, N_TILES], F32, name="rdeg")
             sqd = keep.tile([P, N_TILES], F32, name="sqd")
             degs = keep.tile([P, N_TILES], F32, name="degs")
             junkv = keep.tile([P, HV_LAST], F32, name="junkv")
@@ -274,37 +273,44 @@ def tile_gcnlayer_pa_t_kernel(tc, x, adj, W1, b1, ln_gamma, ln_beta, out):
 
             def chain3b(g):
                 sl = slice(4 * g, 4 * g + 4)
-                nc.vector.reciprocal(out=rdeg[:, sl], in_=deg1[:, sl])
                 nc.vector.reciprocal(out=dinv[:, sl], in_=sqd[:, sl])
 
-            def chain4(g, between=None):
+            hsbs = {}
+
+            def hs_tile(g):
+                hsbs[g] = small.tile([P, F_OUT, 4], BF16, tag="hsb", name="hsb%d" % g, align_bytes=64)
+
+            def hs_mul(g):
                 sl = slice(4 * g, 4 * g + 4)
-                hsb = small.tile([P, F_OUT, 4], BF16, tag="hsb", name="hsb%d" % g, align_bytes=64)
                 nc.vector.tensor_tensor(
-                    out=hsb[:],
+                    out=h[:, sl, :],
+                    in0=h[:, sl, :],
+                    in1=dinv[:, sl].unsqueeze(2).to_broadcast([P, 4, F_OUT]),
+                    op=ALU.mult,
+                )
+
+            def hs_round(g):
+                hs_tile(g)
+                nc.vector.tensor_copy(
+                    out=hsbs[g][:], in_=h[:, 4 * g : 4 * g + 4, :].rearrange("p t f -> p f t")
+                )
+
+            def hs_mul_round(g):
+                hs_tile(g)
+                sl = slice(4 * g, 4 * g + 4)
+                nc.vector.tensor_tensor(
+                    out=hsbs[g][:],
                     in0=h[:, sl, :].rearrange("p t f -> p f t"),
                     in1=dinv[:, sl].unsqueeze(1).to_broadcast([P, F_OUT, 4]),
                     op=ALU.mult,
                 )
-                if between is not None:
-                    quant(between, (1,))
-                    nc.vector.quantize_mx(
-                        out=hcod[:, 128 * g : 128 * g + 128].bitcast(FP8X4),
-                        scales=hscl[:, 128 * g : 128 * g + 128],
-                        in_=hsb[:].rearrange("p f t -> p (f t)"),
-                    )
-                nc.vector.tensor_tensor(
-                    out=h[:, sl, :],
-                    in0=h[:, sl, :],
-                    in1=rdeg[:, sl].unsqueeze(2).to_broadcast([P, 4, F_OUT]),
-                    op=ALU.mult,
+
+            def hs_quant(g):
+                nc.vector.quantize_mx(
+                    out=hcod[:, 128 * g : 128 * g + 128].bitcast(FP8X4),
+                    scales=hscl[:, 128 * g : 128 * g + 128],
+                    in_=hsbs[g][:].rearrange("p f t -> p (f t)"),
                 )
-                if between is None:
-                    nc.vector.quantize_mx(
-                        out=hcod[:, 128 * g : 128 * g + 128].bitcast(FP8X4),
-                        scales=hscl[:, 128 * g : 128 * g + 128],
-                        in_=hsb[:].rearrange("p f t -> p (f t)"),
-                    )
 
             def mx2(acc, g, t4, c):
                 t = 4 * g + t4
@@ -337,21 +343,30 @@ def tile_gcnlayer_pa_t_kernel(tc, x, adj, W1, b1, ln_gamma, ln_beta, out):
                 g8 = (it - 8) // 4 if (it >= 8 and (it - 8) % 4 == 0) else -1
                 g9 = (it - 9) // 4 if (it >= 9 and (it - 9) % 4 == 0) else -1
                 g10 = (it - 10) // 4 if (it >= 10 and (it - 10) % 4 == 0) else -1
+                g11 = (it - 11) // 4 if (it >= 11 and (it - 11) % 4 == 0) else -1
                 if g8 == last:
                     chain3a(last)
                     chain3s(last)
                     nc.scalar.activation(out=dmy2[:], in_=dmy[:], func=ACTF.Gelu)
-                if 0 <= k < N_ITEMS - 1:
-                    quant(k)
-                if 0 <= it - 2 < N_X:
-                    hadd(it - 2)
                 if g8 == last:
                     quant(k, (0,))
                     chain3b(last)
-                    chain4(last, k)
+                    hs_mul_round(last)
+                    quant(k, (1,))
+                    hs_quant(last)
+                    hs_mul(last)
                 if 0 <= g10 < last:
                     chain3b(g10)
-                    chain4(g10)
+                if 0 <= k < N_ITEMS - 1:
+                    quant(k, (0,))
+                if 0 <= g10 < last:
+                    hs_mul(g10)
+                if 0 <= k < N_ITEMS - 1:
+                    quant(k, (1,))
+                if 0 <= g11 < last:
+                    hs_quant(g11)
+                if 0 <= it - 2 < N_X:
+                    hadd(it - 2)
                 if N_X <= it < N_ITEMS:
                     sum_v(it)
                     if pe_chunks((it - N_X) // 4) == 0:
@@ -376,6 +391,8 @@ def tile_gcnlayer_pa_t_kernel(tc, x, adj, W1, b1, ln_gamma, ln_beta, out):
                     chain3s(g9)
                 if 0 <= k < N_X:
                     mx1(k)
+                if 0 <= g10 < last:
+                    hs_round(g10)
                 if it + 4 < N_ITEMS:
                     load(it + 4)
             for g in range(N_GROUPS):
@@ -383,12 +400,17 @@ def tile_gcnlayer_pa_t_kernel(tc, x, adj, W1, b1, ln_gamma, ln_beta, out):
 
             zs = {}
             gls = {}
+            ns = {}
             ys = {}
-            mvall = keep.tile([P, N_TILES, 2], F32, name="mvall")
-            veall = keep.tile([P, N_TILES], F32, name="veall")
-            sdall = keep.tile([P, N_TILES], F32, name="sdall")
-            rstd = keep.tile([P, N_TILES], F32, name="rstd")
+            gsum = keep.tile([P, N_TILES], F32, name="gsum")
+            ssq = keep.tile([P, N_TILES], F32, name="ssq")
             nmu = keep.tile([P, N_TILES], F32, name="nmu")
+            var = keep.tile([P, N_TILES], F32, name="var")
+            rstd = keep.tile([P, N_TILES], F32, name="rstd")
+            nmr = keep.tile([P, N_TILES], F32, name="nmr")
+            mhalf = keep.tile([P, 4], F32, name="mhalf")
+            nc.vector.memset(mhalf[:], -0.5)
+            sqj = keep.tile([P, F_OUT], F32, name="sqj")
 
             def main(g):
                 mx2(accs[g], g, 0, 7)
@@ -398,127 +420,96 @@ def tile_gcnlayer_pa_t_kernel(tc, x, adj, W1, b1, ln_gamma, ln_beta, out):
 
             def e1(g, ep):
                 zs[g] = ep.tile([P, 4, F_OUT], F32, tag="z", bufs=3, name="z%d" % g)
-                for t4 in range(4):
-                    t = 4 * g + t4
-                    nc.vector.scalar_tensor_tensor(
-                        out=zs[g][:, t4, :],
-                        in0=accs[g][:, t4, :],
-                        scalar=dinv[:, t : t + 1],
-                        in1=h[:, t, :],
-                        op0=ALU.mult,
-                        op1=ALU.add,
-                    )
+                nc.vector.tensor_tensor(
+                    out=zs[g][:], in0=accs[g][:], in1=h[:, 4 * g : 4 * g + 4, :], op=ALU.add
+                )
 
-            def e2(g, ep):
-                gls[g] = ep.tile([P, 4, F_OUT], F32, tag="gl", bufs=N_GROUPS, name="gl%d" % g)
-                nc.scalar.activation(out=gls[g][:], in_=zs[g][:], func=ACTF.Gelu)
-
-            def e3(g):
-                st = small.tile([P, 4, 6], F32, tag="st", name="st%d" % g)
-                for t4 in range(4):
-                    nc.vector.bn_stats(out=st[:, t4, :], in_=gls[g][:, t4, :])
-                for t4 in range(4):
-                    nc.vector.bn_aggr(out=mvall[:, 4 * g + t4, :], in_=st[:, t4, :])
-
-            def centre(g):
-                sl = slice(4 * g, 4 * g + 4)
-                nc.vector.tensor_scalar_mul(out=nmu[:, sl], in0=mvall[:, sl, 0], scalar1=-1.0)
+            def act_gelu(g, ep):
+                gls[g] = ep.tile([P, 4, F_OUT], F32, tag="gl", bufs=4, name="gl%d" % g)
                 for t4 in range(4):
                     t = 4 * g + t4
                     nc.scalar.activation(
                         out=gls[g][:, t4, :],
+                        in_=zs[g][:, t4, :],
+                        func=ACTF.Gelu,
+                        scale=dinv[:, t : t + 1],
+                        accum_out=gsum[:, t : t + 1],
+                    )
+
+            def neg_mean(g):
+                sl = slice(4 * g, 4 * g + 4)
+                nc.vector.tensor_scalar_mul(out=nmu[:, sl], in0=gsum[:, sl], scalar1=-1.0 / F_OUT)
+
+            def act_square(g):
+                for t4 in range(4):
+                    t = 4 * g + t4
+                    nc.scalar.activation(
+                        out=sqj[:],
+                        in_=gls[g][:, t4, :],
+                        func=ACTF.Square,
+                        bias=nmu[:, t : t + 1],
+                        accum_out=ssq[:, t : t + 1],
+                    )
+
+            def inv_std(g):
+                sl = slice(4 * g, 4 * g + 4)
+                nc.vector.tensor_scalar(
+                    out=var[:, sl], in0=ssq[:, sl], scalar1=1.0 / F_OUT, scalar2=EPS, op0=ALU.mult, op1=ALU.add
+                )
+                nc.gpsimd.tensor_tensor(out=rstd[:, sl], in0=var[:, sl], in1=mhalf[:], op=ALU.pow)
+                nc.gpsimd.tensor_tensor(out=nmr[:, sl], in0=nmu[:, sl], in1=rstd[:, sl], op=ALU.mult)
+
+            def act_norm(g, ep):
+                ns[g] = ep.tile([P, 4, F_OUT], F32, tag="n", bufs=3, name="n%d" % g)
+                for t4 in range(4):
+                    t = 4 * g + t4
+                    nc.scalar.activation(
+                        out=ns[g][:, t4, :],
                         in_=gls[g][:, t4, :],
                         func=ACTF.Identity,
-                        bias=nmu[:, t : t + 1],
+                        bias=nmr[:, t : t + 1],
+                        scale=rstd[:, t : t + 1],
                     )
-                nc.gpsimd.tensor_tensor(
-                    out=gls[g][:],
-                    in0=gls[g][:],
+
+            def gam(g):
+                nc.vector.tensor_tensor(
+                    out=ns[g][:],
+                    in0=ns[g][:],
                     in1=bc[:, 128:256].unsqueeze(1).to_broadcast([P, 4, F_OUT]),
                     op=ALU.mult,
                 )
 
-            def centre_v(g):
-                for t4 in range(4):
-                    t = 4 * g + t4
-                    nc.vector.scalar_tensor_tensor(
-                        out=gls[g][:, t4, :],
-                        in0=gls[g][:, t4, :],
-                        scalar=mvall[:, t, 0:1],
-                        in1=bc[:, 128:256],
-                        op0=ALU.subtract,
-                        op1=ALU.mult,
-                    )
-
-            def finish_v(g, ep):
+            def bet(g, ep):
                 ys[g] = ep.tile([P, 4, F_OUT], F32, tag="y", bufs=4, name="y%d" % g)
-                for t4 in range(4):
-                    t = 4 * g + t4
-                    nc.vector.scalar_tensor_tensor(
-                        out=ys[g][:, t4, :],
-                        in0=gls[g][:, t4, :],
-                        scalar=rstd[:, t : t + 1],
-                        in1=bc[:, 256:384],
-                        op0=ALU.mult,
-                        op1=ALU.add,
-                    )
-
-            def finish_a(g, ep):
-                ys[g] = ep.tile([P, 4, F_OUT], F32, tag="y", bufs=4, name="y%d" % g)
-                for t4 in range(4):
-                    t = 4 * g + t4
-                    nc.scalar.activation(
-                        out=ys[g][:, t4, :],
-                        in_=gls[g][:, t4, :],
-                        func=ACTF.Identity,
-                        scale=rstd[:, t : t + 1],
-                    )
-
-            def finish_p(g):
-                nc.gpsimd.tensor_tensor(
+                nc.vector.tensor_tensor(
                     out=ys[g][:],
-                    in0=ys[g][:],
+                    in0=ns[g][:],
                     in1=bc[:, 256:384].unsqueeze(1).to_broadcast([P, 4, F_OUT]),
                     op=ALU.add,
                 )
-
-            def store(g):
                 nc.sync.dma_start(out=outv[g], in_=ys[g][:].rearrange("p (u e) f -> p u e f", u=2))
 
             def tail():
                 with tc.tile_pool(name="ep", bufs=4) as ep:
-                    for j in range(N_GROUPS + 1):
-                        if j < N_GROUPS:
+                    for j in range(N_GROUPS + 4):
+                        live = lambda i: 0 <= i < N_GROUPS
+                        if live(j):
                             main(j)
+                        if live(j - 1):
+                            neg_mean(j - 1)
+                        if live(j - 3):
+                            gam(j - 3)
+                        if live(j):
                             e1(j, ep)
-                            e2(j, ep)
-                        if j >= 1:
-                            e3(j - 1)
-                            if j < N_GROUPS:
-                                centre(j - 1)
-                    nc.vector.tensor_scalar_add(out=veall[:], in0=mvall[:, :, 1], scalar1=EPS)
-                    nc.scalar.activation(out=sdall[:], in_=veall[:], func=ACTF.Sqrt)
-                    centre_v(N_GROUPS - 1)
-                    nc.vector.reciprocal(out=rstd[:], in_=sdall[:])
-                    finish_a(0, ep)
-                    finish_v(1, ep)
-                    store(1)
-                    finish_p(0)
-                    store(0)
-                    finish_a(2, ep)
-                    finish_v(3, ep)
-                    store(3)
-                    finish_p(2)
-                    store(2)
-                    finish_a(4, ep)
-                    finish_v(5, ep)
-                    store(5)
-                    finish_p(4)
-                    store(4)
-                    finish_v(6, ep)
-                    store(6)
-                    finish_v(7, ep)
-                    store(7)
+                        if live(j - 1):
+                            act_square(j - 1)
+                            inv_std(j - 1)
+                        if live(j - 3):
+                            bet(j - 3, ep)
+                        if live(j):
+                            act_gelu(j, ep)
+                        if live(j - 2):
+                            act_norm(j - 2, ep)
 
             return tail
 

@@ -23,8 +23,8 @@ N_X = 4
 N_ITEMS = N_X + N_TILES
 HV = 768
 HV_LAST = 1536
-PE_CHUNKS = 5
-ND = 24
+C_PE = 3
+ND = 22
 XT_BUFS = 4
 
 FLOPS = 2 * N_NODES * K_IN * F_OUT + 2 * N_NODES * N_NODES * F_OUT
@@ -69,6 +69,11 @@ def tile_gcnlayer_pa_t_kernel(tc, x, adj, W1, b1, ln_gamma, ln_beta, out):
             for k in range(4):
                 load(k)
 
+            hot = keep.tile([P, 512], BF16, name="hot", align_bytes=64)
+            nc.vector.memset(hot[:], 1.0)
+            hotc = keep.tile([P, F_OUT], U32, name="hotc", align_bytes=64)
+            hots = keep.tile([P, F_OUT], U8, name="hots", align_bytes=64)
+            nc.vector.quantize_mx(out=hotc[:].bitcast(FP8X4), scales=hots[:], in_=hot[:])
             ident = keep.tile([P, P], F32, name="ident")
             make_identity(nc, ident[:])
             ones = keep.tile([P, P], BF16, name="ones")
@@ -106,6 +111,7 @@ def tile_gcnlayer_pa_t_kernel(tc, x, adj, W1, b1, ln_gamma, ln_beta, out):
             )
             bc = keep.tile([P, 384], F32, name="bc")
 
+            last = N_GROUPS - 1
             codes = [
                 keep.tile([P, 1024], U32, name="codes%d" % t, align_bytes=64) for t in range(N_TILES)
             ]
@@ -124,11 +130,7 @@ def tile_gcnlayer_pa_t_kernel(tc, x, adj, W1, b1, ln_gamma, ln_beta, out):
             junkv = keep.tile([P, HV_LAST], F32, name="junkv")
             junka = keep.tile([P, 1024], BF16, name="junka")
 
-            def hv_of(g):
-                return HV if g < N_GROUPS - 1 else HV_LAST
-
-            def pe_chunks(g):
-                return PE_CHUNKS if g < N_GROUPS - 1 else 0
+            nc.vector.memset(dega[:], 0.0)
 
             def slot_of(k):
                 return k - N_X if k >= N_X else N_TILES - N_X + k
@@ -149,7 +151,7 @@ def tile_gcnlayer_pa_t_kernel(tc, x, adj, W1, b1, ln_gamma, ln_beta, out):
 
             def sum_v(k):
                 t = k - N_X
-                hv = hv_of(t // 4)
+                hv = HV if t < N_TILES - 1 else HV_LAST
                 nc.vector.scalar_tensor_tensor(
                     out=junkv[:, 0:hv],
                     in0=nats[k][:, 0:hv],
@@ -162,53 +164,61 @@ def tile_gcnlayer_pa_t_kernel(tc, x, adj, W1, b1, ln_gamma, ln_beta, out):
 
             def sum_a(k):
                 t = k - N_X
-                hi = 4096 - 512 * pe_chunks(t // 4)
-                hv = hv_of(t // 4)
                 nc.scalar.activation(
-                    out=junka[:, 0 : hi - 2 * hv],
-                    in_=nats[k][:, 2 * hv : hi],
+                    out=junka[:, 0 : 4096 - 2 * HV_LAST],
+                    in_=nats[k][:, 2 * HV_LAST : 4096],
                     func=ACTF.Copy,
                     accum_out=dega[:, t : t + 1],
                 )
 
-            def warm(k, n):
-                for i in range(n):
-                    wps = psum.tile([P, 512], F32, tag="hps", bufs=2, name="warm%d_%d" % (k, i))
-                    if k < N_ITEMS - 5:
-                        c, p = codes[N_TILES - N_X], planes[N_GROUPS - 1]
-                    else:
-                        c, p = hcod, hscl
+            def warm(name, tag, bufs, codes_, planes_, n, reps=1):
+                wps = psum.tile([P, 512], F32, tag=tag, bufs=bufs, name=name)
+                for i in range(reps):
+                    c0 = n * (i % (512 // n))
                     nc.tensor.matmul_mx(
-                        out=wps[:],
-                        lhsT=c[:, 0:128].bitcast(FP8X4),
-                        lhsT_scale=p[:, 0:128],
-                        rhs=c[:, 0:512].bitcast(FP8X4),
-                        rhs_scale=p[:, 0:512],
+                        out=wps[:, c0 : c0 + n],
+                        lhsT=codes_[:, 0:128].bitcast(FP8X4),
+                        lhsT_scale=planes_[:, 0:128],
+                        rhs=codes_[:, 0:n].bitcast(FP8X4),
+                        rhs_scale=planes_[:, 0:n],
                         start=True,
                         stop=True,
                     )
 
-            def degmm(k):
+            def warm_half(it, b):
+                if it < N_ITEMS - 4:
+                    c, p = codes[N_TILES - N_X], planes[N_GROUPS - 1]
+                else:
+                    c, p = hcod, hscl
+                warm("wa%d_%d" % (it, b), "hps", 2, c, p, 512)
+                warm("wb%d_%d" % (it, b), "hps", 2, c, p, 256)
+
+            def degmm(k, quarters):
                 t = k - N_X
                 g = t // 4
                 t4 = t % 4
-                if t4 == 0:
+                if t4 == 0 and quarters[0] == 0:
                     dps[g] = psum.tile([P, 4, 4, ND], F32, tag="D", name="D%d" % g)
-                for s in range(4):
-                    for c in range(8 - PE_CHUNKS, 8):
+                for s in quarters:
+                    for c in range(C_PE, 8):
                         c0 = 512 * c + 128 * s
                         nc.tensor.matmul(
                             out=dps[g][:, t4, s, :],
                             lhsT=grps[k][:, c0 : c0 + 128],
                             rhs=ones[:, 0:ND],
-                            start=(c == 8 - PE_CHUNKS),
+                            start=(c == C_PE),
                             stop=(c == 7),
                         )
 
             def chain1(g):
                 dsb = small.tile([P, 4, 4], F32, tag="dsb", name="dsb%d" % g)
                 dsbs[g] = dsb
-                nc.vector.tensor_copy(out=dsb[:], in_=dps[g][:, :, :, 0].rearrange("p t s -> p s t"))
+                n = 4 if g < last else 3
+                if g == last:
+                    nc.vector.memset(dsb[:], 0.0)
+                nc.vector.tensor_copy(
+                    out=dsb[:, :, 0:n], in_=dps[g][:, 0:n, :, 0].rearrange("p t s -> p s t")
+                )
 
             def chain2(g):
                 o2 = psum.tile([P, 4], F32, tag="o2", name="o2_%d" % g)
@@ -259,13 +269,13 @@ def tile_gcnlayer_pa_t_kernel(tc, x, adj, W1, b1, ln_gamma, ln_beta, out):
 
             def chain3a(g):
                 sl = slice(4 * g, 4 * g + 4)
-                if pe_chunks(g) > 0:
-                    nc.vector.scalar_tensor_tensor(
-                        out=deg1[:, sl], in0=o2s[g][:], scalar=1.0, in1=degv[:, sl], op0=ALU.add, op1=ALU.add
-                    )
-                else:
+                dv = degv
+                if g == last:
                     nc.vector.tensor_tensor(out=degs[:, sl], in0=degv[:, sl], in1=dega[:, sl], op=ALU.add)
-                    nc.vector.tensor_scalar_add(out=deg1[:, sl], in0=degs[:, sl], scalar1=1.0)
+                    dv = degs
+                nc.vector.scalar_tensor_tensor(
+                    out=deg1[:, sl], in0=o2s[g][:], scalar=1.0, in1=dv[:, sl], op0=ALU.add, op1=ALU.add
+                )
 
             def chain3s(g):
                 sl = slice(4 * g, 4 * g + 4)
@@ -326,76 +336,91 @@ def tile_gcnlayer_pa_t_kernel(tc, x, adj, W1, b1, ln_gamma, ln_beta, out):
 
             accs = {}
 
-            acc_tags = [("xt", XT_BUFS)] * XT_BUFS + [("hps", 2), ("hps", 2), ("D", 1), ("o2", 1)]
+            acc_tags = [("hps", 2), ("hps", 2), ("D", 1)] + [("xt", XT_BUFS)] * XT_BUFS + [("o2", 1)]
 
-            def pre(g):
+            def acc_tile(g):
                 accs[g] = psum.tile(
                     [P, 4, F_OUT], F32, tag=acc_tags[g][0], bufs=acc_tags[g][1], name="acc%d" % g
                 )
+
+            def pre(g):
+                acc_tile(g)
                 for c in range(7):
                     mx2(accs[g], g, 0, c)
 
             ctx.enter_context(tc.manual_schedule())
 
-            last = N_GROUPS - 1
-            for it in range(N_ITEMS + 1):
+            warm("warm_head", "D", 1, hotc, hots, 128, 16)
+            for it in range(N_ITEMS):
                 k = it - 1
-                g8 = (it - 8) // 4 if (it >= 8 and (it - 8) % 4 == 0) else -1
-                g9 = (it - 9) // 4 if (it >= 9 and (it - 9) % 4 == 0) else -1
-                g10 = (it - 10) // 4 if (it >= 10 and (it - 10) % 4 == 0) else -1
-                g11 = (it - 11) // 4 if (it >= 11 and (it - 11) % 4 == 0) else -1
-                if g8 == last:
-                    chain3a(last)
-                    chain3s(last)
-                    nc.scalar.activation(out=dmy2[:], in_=dmy[:], func=ACTF.Gelu)
-                if g8 == last:
+
+                def group_at(lag):
+                    n = it - 7 - lag
+                    return n // 4 if n >= 0 and n % 4 == 0 else -1
+
+                g2, g3, g4, g5 = group_at(2), group_at(3), group_at(4), group_at(5)
+                if k >= 0:
                     quant(k, (0,))
-                    chain3b(last)
-                    hs_mul_round(last)
+                if g2 >= 0:
+                    chain1(g2)
+                if g3 >= 0:
+                    chain3a(g3)
+                if g4 >= 0:
+                    chain3b(g4)
+                if g5 >= 0:
+                    hs_quant(g5)
+                if k >= 0:
                     quant(k, (1,))
-                    hs_quant(last)
-                    hs_mul(last)
-                if 0 <= g10 < last:
-                    chain3b(g10)
-                if 0 <= k < N_ITEMS - 1:
-                    quant(k, (0,))
-                if 0 <= g10 < last:
-                    hs_mul(g10)
-                if 0 <= k < N_ITEMS - 1:
-                    quant(k, (1,))
-                if 0 <= g11 < last:
-                    hs_quant(g11)
+                if g4 >= 0:
+                    hs_mul(g4)
                 if 0 <= it - 2 < N_X:
                     hadd(it - 2)
-                if N_X <= it < N_ITEMS:
-                    sum_v(it)
-                    if pe_chunks((it - N_X) // 4) == 0:
-                        sum_a(it)
-                if it < N_ITEMS:
-                    for b in range(4):
-                        transp(it, b)
+                if N_X <= it + 1 < N_ITEMS:
+                    sum_v(it + 1)
+                if g4 >= 0:
+                    hs_round(g4)
+                transp(it, 0)
+                transp(it, 1)
                 if it == 1:
                     bcps = psum.tile([P, 512], F32, tag="hps", bufs=2, name="bcps")
                     nc.tensor.matmul(out=bcps[:], lhsT=ones[:], rhs=zrow[:], start=True, stop=True)
                     nc.vector.tensor_copy(out=bc[:], in_=bcps[:, 0:384])
-                if 0 <= g9 < last:
-                    chain2(g9)
-                if N_X <= k < N_ITEMS and pe_chunks((k - N_X) // 4) > 0:
-                    degmm(k)
-                if N_X <= k < N_ITEMS - 1:
-                    warm(k, 3)
-                if 0 <= g8 < last:
-                    chain1(g8)
-                if 0 <= g9 < last:
-                    chain3a(g9)
-                    chain3s(g9)
+                if it == N_ITEMS - 1:
+                    degmm(k, (0, 1, 2, 3))
+                elif k >= N_X:
+                    degmm(k, (0, 1))
+                    warm_half(it, 0)
+                elif it >= 2:
+                    warm("warmx%d" % it, "D", 1, codes[N_TILES - N_X], planes[N_GROUPS - 1], 512)
+                if it == N_ITEMS - 1:
+                    chain1(last)
+                    chain2(last)
+                    chain3a(last)
+                    hs_quant(last - 1)
+                    chain3s(last)
+                transp(it, 2)
+                transp(it, 3)
+                if g2 >= 0:
+                    chain2(g2)
+                if N_X <= k < N_ITEMS - 2:
+                    degmm(k, (2, 3))
+                    warm_half(it, 1)
                 if 0 <= k < N_X:
                     mx1(k)
-                if 0 <= g10 < last:
-                    hs_round(g10)
+                if g3 >= 0:
+                    chain3s(g3)
+                if it == N_ITEMS - 2:
+                    sum_a(it + 1)
                 if it + 4 < N_ITEMS:
                     load(it + 4)
-            for g in range(N_GROUPS):
+            nc.scalar.activation(out=dmy2[:], in_=dmy[:], func=ACTF.Gelu)
+            chain3b(last)
+            hs_mul_round(last)
+            quant(N_ITEMS - 1, (0,))
+            hs_quant(last)
+            quant(N_ITEMS - 1, (1,))
+            hs_mul(last)
+            for g in range(3):
                 pre(g)
 
             zs = {}
@@ -413,8 +438,11 @@ def tile_gcnlayer_pa_t_kernel(tc, x, adj, W1, b1, ln_gamma, ln_beta, out):
             sqj = keep.tile([P, F_OUT], F32, name="sqj")
 
             def main(g):
-                mx2(accs[g], g, 0, 7)
-                for t4 in range(1, 4):
+                if g in accs:
+                    mx2(accs[g], g, 0, 7)
+                else:
+                    acc_tile(g)
+                for t4 in range(1 if g < 3 else 0, 4):
                     for c in range(8):
                         mx2(accs[g], g, t4, c)
 
@@ -471,6 +499,19 @@ def tile_gcnlayer_pa_t_kernel(tc, x, adj, W1, b1, ln_gamma, ln_beta, out):
                         scale=rstd[:, t : t + 1],
                     )
 
+            def vec_norm(g, ep):
+                ns[g] = ep.tile([P, 4, F_OUT], F32, tag="n", bufs=3, name="n%d" % g)
+                for t4 in range(4):
+                    t = 4 * g + t4
+                    nc.vector.tensor_scalar(
+                        out=ns[g][:, t4, :],
+                        in0=gls[g][:, t4, :],
+                        scalar1=rstd[:, t : t + 1],
+                        scalar2=nmr[:, t : t + 1],
+                        op0=ALU.mult,
+                        op1=ALU.add,
+                    )
+
             def gam(g):
                 nc.vector.tensor_tensor(
                     out=ns[g][:],
@@ -498,6 +539,8 @@ def tile_gcnlayer_pa_t_kernel(tc, x, adj, W1, b1, ln_gamma, ln_beta, out):
                         if live(j - 1):
                             neg_mean(j - 1)
                         if live(j - 3):
+                            if j % 2 == 0:
+                                vec_norm(j - 3, ep)
                             gam(j - 3)
                         if live(j):
                             e1(j, ep)
@@ -508,7 +551,7 @@ def tile_gcnlayer_pa_t_kernel(tc, x, adj, W1, b1, ln_gamma, ln_beta, out):
                             bet(j - 3, ep)
                         if live(j):
                             act_gelu(j, ep)
-                        if live(j - 2):
+                        if live(j - 2) and j % 2 == 0:
                             act_norm(j - 2, ep)
 
             return tail

@@ -21,10 +21,13 @@ N_TILES = 32
 N_GROUPS = 8
 N_X = 4
 N_ITEMS = N_X + N_TILES
-HV = 768
+HV = 1024
 HV_LAST = 1536
-C_PE = 3
-ND = 22
+C_PE = 4
+HOT = (16, 1, 12, 4)
+HEAT = (512, 256)
+EARLY = 3
+ND = 28
 XT_BUFS = 4
 
 FLOPS = 2 * N_NODES * K_IN * F_OUT + 2 * N_NODES * N_NODES * F_OUT
@@ -131,6 +134,10 @@ def tile_gcnlayer_pa_t_kernel(tc, x, adj, W1, b1, ln_gamma, ln_beta, out):
             junka = keep.tile([P, 1024], BF16, name="junka")
 
             nc.vector.memset(dega[:], 0.0)
+            dsb_last = keep.tile([P, 4, 4], F32, name="dsb_last")
+            nc.vector.memset(dsb_last[:], 0.0)
+            mhalf = keep.tile([P, 4], F32, name="mhalf")
+            nc.vector.memset(mhalf[:], -0.5)
 
             def slot_of(k):
                 return k - N_X if k >= N_X else N_TILES - N_X + k
@@ -185,13 +192,16 @@ def tile_gcnlayer_pa_t_kernel(tc, x, adj, W1, b1, ln_gamma, ln_beta, out):
                         stop=True,
                     )
 
-            def warm_half(it, b):
+            def hot_fill(name, reps):
+                warm("hot_" + name, "D", 1, hotc, hots, 128, reps)
+
+            def warm_tile(it, half):
                 if it < N_ITEMS - 4:
                     c, p = codes[N_TILES - N_X], planes[N_GROUPS - 1]
                 else:
                     c, p = hcod, hscl
-                warm("wa%d_%d" % (it, b), "hps", 2, c, p, 512)
-                warm("wb%d_%d" % (it, b), "hps", 2, c, p, 256)
+                for i, n in enumerate(HEAT):
+                    warm("w%d_%d_%d" % (it, half, i), "hps", 2, c, p, n)
 
             def degmm(k, quarters):
                 t = k - N_X
@@ -211,11 +221,9 @@ def tile_gcnlayer_pa_t_kernel(tc, x, adj, W1, b1, ln_gamma, ln_beta, out):
                         )
 
             def chain1(g):
-                dsb = small.tile([P, 4, 4], F32, tag="dsb", name="dsb%d" % g)
+                dsb = small.tile([P, 4, 4], F32, tag="dsb", name="dsb%d" % g) if g < last else dsb_last
                 dsbs[g] = dsb
                 n = 4 if g < last else 3
-                if g == last:
-                    nc.vector.memset(dsb[:], 0.0)
                 nc.vector.tensor_copy(
                     out=dsb[:, :, 0:n], in_=dps[g][:, 0:n, :, 0].rearrange("p t s -> p s t")
                 )
@@ -238,24 +246,28 @@ def tile_gcnlayer_pa_t_kernel(tc, x, adj, W1, b1, ln_gamma, ln_beta, out):
                         in_=grps[k][:, 2048 * hf : 2048 * hf + 2048],
                     )
 
-            def mx1(k):
+            def mx1(k, gg):
                 sl = slot_of(k)
                 kk = 4 * (sl % 4)
-                for gg in range(2):
-                    g = 2 * k + gg
-                    hps = psum.tile([P, 4, F_OUT], F32, tag="hps", bufs=2, name="hps%d" % g)
-                    hpss[g] = hps
-                    for t4 in range(4):
-                        c0 = 128 * (4 * gg + t4)
-                        nc.tensor.matmul_mx(
-                            out=hps[:, t4, :],
-                            lhsT=codes[sl][:, c0 : c0 + 128].bitcast(FP8X4),
-                            lhsT_scale=planes[sl // 4][kk:P, c0 : c0 + 128],
-                            rhs=w1c[:].bitcast(FP8X4),
-                            rhs_scale=w1s[:],
-                            start=True,
-                            stop=True,
-                        )
+                g = 2 * k + gg
+                hps = psum.tile([P, 4, F_OUT], F32, tag="hps", bufs=2, name="hps%d" % g)
+                hpss[g] = hps
+                for t4 in range(4):
+                    c0 = 128 * (4 * gg + t4)
+                    nc.tensor.matmul_mx(
+                        out=hps[:, t4, :],
+                        lhsT=codes[sl][:, c0 : c0 + 128].bitcast(FP8X4),
+                        lhsT_scale=planes[sl // 4][kk:P, c0 : c0 + 128],
+                        rhs=w1c[:].bitcast(FP8X4),
+                        rhs_scale=w1s[:],
+                        start=True,
+                        stop=True,
+                    )
+
+            def bias_tile():
+                bcps = psum.tile([P, 512], F32, tag="hps", bufs=2, name="bcps")
+                nc.tensor.matmul(out=bcps[:], lhsT=ones[:], rhs=zrow[:], start=True, stop=True)
+                nc.vector.tensor_copy(out=bc[:], in_=bcps[:, 0:384])
 
             def hadd(k):
                 for gg in range(2):
@@ -322,7 +334,7 @@ def tile_gcnlayer_pa_t_kernel(tc, x, adj, W1, b1, ln_gamma, ln_beta, out):
                     in_=hsbs[g][:].rearrange("p f t -> p (f t)"),
                 )
 
-            def mx2(acc, g, t4, c):
+            def mx2(acc, g, t4, c, c_first=0, c_last=7):
                 t = 4 * g + t4
                 nc.tensor.matmul_mx(
                     out=acc[:, t4, :],
@@ -330,27 +342,43 @@ def tile_gcnlayer_pa_t_kernel(tc, x, adj, W1, b1, ln_gamma, ln_beta, out):
                     lhsT_scale=planes[g][4 * t4 : P, 128 * c : 128 * c + 128],
                     rhs=hcod[:, 128 * c : 128 * c + 128].bitcast(FP8X4),
                     rhs_scale=hscl[:, 128 * c : 128 * c + 128],
-                    start=(c == 0),
-                    stop=(c == 7),
+                    start=(c == c_first),
+                    stop=(c == c_last),
                 )
 
             accs = {}
 
             acc_tags = [("hps", 2), ("hps", 2), ("D", 1)] + [("xt", XT_BUFS)] * XT_BUFS + [("o2", 1)]
+            C_EARLY = 5
+            IT_EARLY = 4 * C_EARLY + 8
+            early = {}
+
+            def early_part(q):
+                g, t4 = q // 4, q % 4
+                if t4 == 0:
+                    early[g] = psum.tile([P, 4, F_OUT], F32, tag="hps", bufs=2, name="early%d" % g)
+                for c in range(C_EARLY):
+                    mx2(early[g], g, t4, c, 0, C_EARLY - 1)
+
+            def early_add(g):
+                nc.vector.tensor_tensor(
+                    out=h[:, 4 * g : 4 * g + 4, :],
+                    in0=early[g][:],
+                    in1=h[:, 4 * g : 4 * g + 4, :],
+                    op=ALU.add,
+                )
 
             def acc_tile(g):
                 accs[g] = psum.tile(
                     [P, 4, F_OUT], F32, tag=acc_tags[g][0], bufs=acc_tags[g][1], name="acc%d" % g
                 )
 
-            def pre(g):
-                acc_tile(g)
-                for c in range(7):
-                    mx2(accs[g], g, 0, c)
+            def first_chunk(g):
+                return C_EARLY if g < EARLY else 0
 
             ctx.enter_context(tc.manual_schedule())
 
-            warm("warm_head", "D", 1, hotc, hots, 128, 16)
+            hot_fill("head", HOT[0])
             for it in range(N_ITEMS):
                 k = it - 1
 
@@ -359,6 +387,10 @@ def tile_gcnlayer_pa_t_kernel(tc, x, adj, W1, b1, ln_gamma, ln_beta, out):
                     return n // 4 if n >= 0 and n % 4 == 0 else -1
 
                 g2, g3, g4, g5 = group_at(2), group_at(3), group_at(4), group_at(5)
+                if it == N_ITEMS - 1:
+                    break
+                if 0 <= it - 3 < N_X:
+                    hadd(it - 3)
                 if k >= 0:
                     quant(k, (0,))
                 if g2 >= 0:
@@ -373,55 +405,68 @@ def tile_gcnlayer_pa_t_kernel(tc, x, adj, W1, b1, ln_gamma, ln_beta, out):
                     quant(k, (1,))
                 if g4 >= 0:
                     hs_mul(g4)
-                if 0 <= it - 2 < N_X:
-                    hadd(it - 2)
+                if it - IT_EARLY - 2 in range(0, 2 * EARLY, 2):
+                    early_add((it - IT_EARLY - 2) // 2)
                 if N_X <= it + 1 < N_ITEMS:
                     sum_v(it + 1)
                 if g4 >= 0:
                     hs_round(g4)
-                transp(it, 0)
-                transp(it, 1)
-                if it == 1:
-                    bcps = psum.tile([P, 512], F32, tag="hps", bufs=2, name="bcps")
-                    nc.tensor.matmul(out=bcps[:], lhsT=ones[:], rhs=zrow[:], start=True, stop=True)
-                    nc.vector.tensor_copy(out=bc[:], in_=bcps[:, 0:384])
-                if it == N_ITEMS - 1:
-                    degmm(k, (0, 1, 2, 3))
-                elif k >= N_X:
-                    degmm(k, (0, 1))
-                    warm_half(it, 0)
-                elif it >= 2:
-                    warm("warmx%d" % it, "D", 1, codes[N_TILES - N_X], planes[N_GROUPS - 1], 512)
-                if it == N_ITEMS - 1:
-                    chain1(last)
-                    chain2(last)
-                    chain3a(last)
-                    hs_quant(last - 1)
-                    chain3s(last)
-                transp(it, 2)
-                transp(it, 3)
-                if g2 >= 0:
-                    chain2(g2)
-                if N_X <= k < N_ITEMS - 2:
-                    degmm(k, (2, 3))
-                    warm_half(it, 1)
-                if 0 <= k < N_X:
-                    mx1(k)
+                for half in range(2):
+                    for b in (2 * half, 2 * half + 1):
+                        transp(it, b)
+                        if it == 0:
+                            hot_fill("x%d" % b, HOT[1] if b < 3 else HOT[2])
+                    if it == 1 and half == 1:
+                        bias_tile()
+                        hot_fill("x4", HOT[3])
+                    if half == 1 and g2 >= 0:
+                        chain2(g2)
+                    if k >= N_X:
+                        degmm(k, (2 * half, 2 * half + 1))
+                    if 0 <= it - 2 < N_X:
+                        mx1(it - 2, half)
+                        if half == 1:
+                            tag = "D" if it < 5 else "o2"
+                            warm("warmx%d" % it, tag, 1, codes[N_TILES - N_X], planes[N_GROUPS - 1], 512)
+                    elif 0 <= it - IT_EARLY < 2 * EARLY:
+                        early_part(2 * (it - IT_EARLY) + half)
+                    elif it > 1:
+                        warm_tile(it, half)
                 if g3 >= 0:
                     chain3s(g3)
                 if it == N_ITEMS - 2:
                     sum_a(it + 1)
                 if it + 4 < N_ITEMS:
                     load(it + 4)
-            nc.scalar.activation(out=dmy2[:], in_=dmy[:], func=ACTF.Gelu)
+            it = N_ITEMS - 1
+            transp(it, 0)
+            transp(it, 1)
+            degmm(it - 1, (0, 1, 2, 3))
+            transp(it, 2)
+            transp(it, 3)
+            quant(it - 1, (0,))
+            chain3b(last - 1)
+            chain1(last)
+            chain2(last)
+            hs_mul(last - 1)
+            chain3a(last)
+            chain3s(last)
+            quant(it - 1, (1,))
+            hs_round(last - 1)
             chain3b(last)
+            hs_quant(last - 1)
             hs_mul_round(last)
-            quant(N_ITEMS - 1, (0,))
+            nc.scalar.activation(out=dmy2[:], in_=dmy[:], func=ACTF.Gelu)
+            quant(it, (0,))
             hs_quant(last)
-            quant(N_ITEMS - 1, (1,))
+            quant(it, (1,))
             hs_mul(last)
-            for g in range(3):
-                pre(g)
+            for g in range(N_GROUPS):
+                acc_tile(g)
+                for c in range(first_chunk(g), 6):
+                    mx2(accs[g], g, 0, c, first_chunk(g))
+            for g in range(N_GROUPS):
+                mx2(accs[g], g, 0, 6, first_chunk(g))
 
             zs = {}
             gls = {}
@@ -433,18 +478,13 @@ def tile_gcnlayer_pa_t_kernel(tc, x, adj, W1, b1, ln_gamma, ln_beta, out):
             var = keep.tile([P, N_TILES], F32, name="var")
             rstd = keep.tile([P, N_TILES], F32, name="rstd")
             nmr = keep.tile([P, N_TILES], F32, name="nmr")
-            mhalf = keep.tile([P, 4], F32, name="mhalf")
-            nc.vector.memset(mhalf[:], -0.5)
-            sqj = keep.tile([P, F_OUT], F32, name="sqj")
 
             def main(g):
-                if g in accs:
-                    mx2(accs[g], g, 0, 7)
-                else:
-                    acc_tile(g)
-                for t4 in range(1 if g < 3 else 0, 4):
-                    for c in range(8):
-                        mx2(accs[g], g, t4, c)
+                c0 = first_chunk(g)
+                mx2(accs[g], g, 0, 7, c0)
+                for t4 in range(1, 4):
+                    for c in range(c0, 8):
+                        mx2(accs[g], g, t4, c, c0)
 
             def e1(g, ep):
                 zs[g] = ep.tile([P, 4, F_OUT], F32, tag="z", bufs=3, name="z%d" % g)
@@ -453,7 +493,7 @@ def tile_gcnlayer_pa_t_kernel(tc, x, adj, W1, b1, ln_gamma, ln_beta, out):
                 )
 
             def act_gelu(g, ep):
-                gls[g] = ep.tile([P, 4, F_OUT], F32, tag="gl", bufs=4, name="gl%d" % g)
+                gls[g] = ep.tile([P, 4, F_OUT], F32, tag="gl", bufs=5, name="gl%d" % g)
                 for t4 in range(4):
                     t = 4 * g + t4
                     nc.scalar.activation(
@@ -472,7 +512,7 @@ def tile_gcnlayer_pa_t_kernel(tc, x, adj, W1, b1, ln_gamma, ln_beta, out):
                 for t4 in range(4):
                     t = 4 * g + t4
                     nc.scalar.activation(
-                        out=sqj[:],
+                        out=junkv[:, 128 * t4 : 128 * t4 + 128],
                         in_=gls[g][:, t4, :],
                         func=ACTF.Square,
                         bias=nmu[:, t : t + 1],
@@ -485,7 +525,8 @@ def tile_gcnlayer_pa_t_kernel(tc, x, adj, W1, b1, ln_gamma, ln_beta, out):
                     out=var[:, sl], in0=ssq[:, sl], scalar1=1.0 / F_OUT, scalar2=EPS, op0=ALU.mult, op1=ALU.add
                 )
                 nc.gpsimd.tensor_tensor(out=rstd[:, sl], in0=var[:, sl], in1=mhalf[:], op=ALU.pow)
-                nc.gpsimd.tensor_tensor(out=nmr[:, sl], in0=nmu[:, sl], in1=rstd[:, sl], op=ALU.mult)
+                if g < last:
+                    nc.gpsimd.tensor_tensor(out=nmr[:, sl], in0=nmu[:, sl], in1=rstd[:, sl], op=ALU.mult)
 
             def act_norm(g, ep):
                 ns[g] = ep.tile([P, 4, F_OUT], F32, tag="n", bufs=3, name="n%d" % g)
@@ -499,18 +540,35 @@ def tile_gcnlayer_pa_t_kernel(tc, x, adj, W1, b1, ln_gamma, ln_beta, out):
                         scale=rstd[:, t : t + 1],
                     )
 
-            def vec_norm(g, ep):
+            def centre(g, ep):
                 ns[g] = ep.tile([P, 4, F_OUT], F32, tag="n", bufs=3, name="n%d" % g)
                 for t4 in range(4):
                     t = 4 * g + t4
-                    nc.vector.tensor_scalar(
+                    nc.vector.scalar_tensor_tensor(
                         out=ns[g][:, t4, :],
                         in0=gls[g][:, t4, :],
-                        scalar1=rstd[:, t : t + 1],
-                        scalar2=nmr[:, t : t + 1],
+                        scalar=nmu[:, t : t + 1],
+                        in1=bc[:, 128:256],
+                        op0=ALU.add,
+                        op1=ALU.mult,
+                    )
+
+            def finish(g, ep):
+                ys[g] = ep.tile([P, 4, F_OUT], F32, tag="y", bufs=4, name="y%d" % g)
+                for t4 in range(4):
+                    t = 4 * g + t4
+                    nc.vector.scalar_tensor_tensor(
+                        out=ys[g][:, t4, :],
+                        in0=ns[g][:, t4, :],
+                        scalar=rstd[:, t : t + 1],
+                        in1=bc[:, 256:384],
                         op0=ALU.mult,
                         op1=ALU.add,
                     )
+                store(g)
+
+            def store(g):
+                nc.sync.dma_start(out=outv[g], in_=ys[g][:].rearrange("p (u e) f -> p u e f", u=2))
 
             def gam(g):
                 nc.vector.tensor_tensor(
@@ -528,31 +586,38 @@ def tile_gcnlayer_pa_t_kernel(tc, x, adj, W1, b1, ln_gamma, ln_beta, out):
                     in1=bc[:, 256:384].unsqueeze(1).to_broadcast([P, 4, F_OUT]),
                     op=ALU.add,
                 )
-                nc.sync.dma_start(out=outv[g], in_=ys[g][:].rearrange("p (u e) f -> p u e f", u=2))
+                store(g)
 
             def tail():
                 with tc.tile_pool(name="ep", bufs=4) as ep:
+                    def live(i):
+                        return 0 <= i < N_GROUPS
+
                     for j in range(N_GROUPS + 4):
-                        live = lambda i: 0 <= i < N_GROUPS
                         if live(j):
                             main(j)
-                        if live(j - 1):
-                            neg_mean(j - 1)
-                        if live(j - 3):
-                            if j % 2 == 0:
-                                vec_norm(j - 3, ep)
-                            gam(j - 3)
                         if live(j):
                             e1(j, ep)
                         if live(j - 1):
-                            act_square(j - 1)
-                            inv_std(j - 1)
-                        if live(j - 3):
-                            bet(j - 3, ep)
+                            neg_mean(j - 1)
+                        if j - 1 == last:
+                            centre(j - 1, ep)
+                        if j - 2 == last:
+                            inv_std(j - 2)
+                        if live(j - 4) and j - 4 < last:
+                            gam(j - 4)
+                        if live(j - 2) and j - 2 < last:
+                            inv_std(j - 2)
+                        if live(j - 4) and j - 4 < last:
+                            bet(j - 4, ep)
+                        if j - 3 == last:
+                            finish(j - 3, ep)
                         if live(j):
                             act_gelu(j, ep)
-                        if live(j - 2) and j % 2 == 0:
-                            act_norm(j - 2, ep)
+                        if live(j - 1):
+                            act_square(j - 1)
+                        if live(j - 3) and j - 3 < last:
+                            act_norm(j - 3, ep)
 
             return tail
 

@@ -24,9 +24,10 @@ N_ITEMS = N_X + N_TILES
 HV = 1024
 HV_LAST = 1536
 C_PE = 4
-HOT = (16, 1, 12, 4)
+HOT = (16, 4, 6, 8)
 HEAT = (512, 256)
-EARLY = 3
+EARLY = 1
+FINE = 1
 ND = 28
 XT_BUFS = 4
 
@@ -67,16 +68,30 @@ def tile_gcnlayer_pa_t_kernel(tc, x, adj, W1, b1, ln_gamma, ln_beta, out):
                     )
                 else:
                     t = k - N_X
-                    nc.sync.dma_start(out=nat[:], in_=adjv[t // 4, (t % 4) // 2, t % 2])
+                    pieces = 4 if t < FINE else 1
+                    w = 4096 // pieces
+                    for i in range(pieces):
+                        nc.sync.dma_start(
+                            out=nat[:, w * i : w * i + w],
+                            in_=adjv[t // 4, (t % 4) // 2, t % 2][:, w * i : w * i + w],
+                        )
 
-            for k in range(4):
+            order = []
+            for i in range(N_X):
+                order += [i] + [N_X + t for t in range(8 * i, 8 * i + 8)]
+            for k in order[0:4]:
                 load(k)
 
             hot = keep.tile([P, 512], BF16, name="hot", align_bytes=64)
             nc.vector.memset(hot[:], 1.0)
-            hotc = keep.tile([P, F_OUT], U32, name="hotc", align_bytes=64)
-            hots = keep.tile([P, F_OUT], U8, name="hots", align_bytes=64)
-            nc.vector.quantize_mx(out=hotc[:].bitcast(FP8X4), scales=hots[:], in_=hot[:])
+            hotc = keep.tile([P, 512], U32, name="hotc", align_bytes=64)
+            hots = keep.tile([P, 512], U8, name="hots", align_bytes=64)
+            for c in range(4):
+                nc.vector.quantize_mx(
+                    out=hotc[:, 128 * c : 128 * c + 128].bitcast(FP8X4),
+                    scales=hots[:, 128 * c : 128 * c + 128],
+                    in_=hot[:],
+                )
             ident = keep.tile([P, P], F32, name="ident")
             make_identity(nc, ident[:])
             ones = keep.tile([P, P], BF16, name="ones")
@@ -131,7 +146,7 @@ def tile_gcnlayer_pa_t_kernel(tc, x, adj, W1, b1, ln_gamma, ln_beta, out):
             sqd = keep.tile([P, N_TILES], F32, name="sqd")
             degs = keep.tile([P, N_TILES], F32, name="degs")
             junkv = keep.tile([P, HV_LAST], F32, name="junkv")
-            junka = keep.tile([P, 1024], BF16, name="junka")
+            junka = keep.tile([P, 4096 - 2 * HV_LAST], BF16, name="junka")
 
             nc.vector.memset(dega[:], 0.0)
             dsb_last = keep.tile([P, 4, 4], F32, name="dsb_last")
@@ -172,36 +187,32 @@ def tile_gcnlayer_pa_t_kernel(tc, x, adj, W1, b1, ln_gamma, ln_beta, out):
             def sum_a(k):
                 t = k - N_X
                 nc.scalar.activation(
-                    out=junka[:, 0 : 4096 - 2 * HV_LAST],
+                    out=junka[:],
                     in_=nats[k][:, 2 * HV_LAST : 4096],
                     func=ACTF.Copy,
                     accum_out=dega[:, t : t + 1],
                 )
 
-            def warm(name, tag, bufs, codes_, planes_, n, reps=1):
+            def warm(name, tag, bufs, n, reps=1):
                 wps = psum.tile([P, 512], F32, tag=tag, bufs=bufs, name=name)
                 for i in range(reps):
                     c0 = n * (i % (512 // n))
                     nc.tensor.matmul_mx(
                         out=wps[:, c0 : c0 + n],
-                        lhsT=codes_[:, 0:128].bitcast(FP8X4),
-                        lhsT_scale=planes_[:, 0:128],
-                        rhs=codes_[:, 0:n].bitcast(FP8X4),
-                        rhs_scale=planes_[:, 0:n],
+                        lhsT=hotc[:, 0:128].bitcast(FP8X4),
+                        lhsT_scale=hots[:, 0:128],
+                        rhs=hotc[:, 0:n].bitcast(FP8X4),
+                        rhs_scale=hots[:, 0:n],
                         start=True,
                         stop=True,
                     )
 
             def hot_fill(name, reps):
-                warm("hot_" + name, "D", 1, hotc, hots, 128, reps)
+                warm("hot_" + name, "D", 1, 128, reps)
 
-            def warm_tile(it, half):
-                if it < N_ITEMS - 4:
-                    c, p = codes[N_TILES - N_X], planes[N_GROUPS - 1]
-                else:
-                    c, p = hcod, hscl
-                for i, n in enumerate(HEAT):
-                    warm("w%d_%d_%d" % (it, half, i), "hps", 2, c, p, n)
+            def warm_half(p, half, tag="hps"):
+                for n in HEAT:
+                    warm("w%d_%d_%d" % (p, half, n), tag, 2 if tag == "hps" else 1, n)
 
             def degmm(k, quarters):
                 t = k - N_X
@@ -300,7 +311,7 @@ def tile_gcnlayer_pa_t_kernel(tc, x, adj, W1, b1, ln_gamma, ln_beta, out):
             hsbs = {}
 
             def hs_tile(g):
-                hsbs[g] = small.tile([P, F_OUT, 4], BF16, tag="hsb", name="hsb%d" % g, align_bytes=64)
+                hsbs[g] = small.tile([P, F_OUT, 4], BF16, tag="hsb", bufs=2, name="hsb%d" % g, align_bytes=64)
 
             def hs_mul(g):
                 sl = slice(4 * g, 4 * g + 4)
@@ -350,7 +361,7 @@ def tile_gcnlayer_pa_t_kernel(tc, x, adj, W1, b1, ln_gamma, ln_beta, out):
 
             acc_tags = [("hps", 2), ("hps", 2), ("D", 1)] + [("xt", XT_BUFS)] * XT_BUFS + [("o2", 1)]
             C_EARLY = 5
-            IT_EARLY = 4 * C_EARLY + 8
+            P_EARLY = [27, 28]
             early = {}
 
             def early_part(q):
@@ -379,94 +390,91 @@ def tile_gcnlayer_pa_t_kernel(tc, x, adj, W1, b1, ln_gamma, ln_beta, out):
             ctx.enter_context(tc.manual_schedule())
 
             hot_fill("head", HOT[0])
-            for it in range(N_ITEMS):
-                k = it - 1
+            for p in range(N_ITEMS - 1):
+                k = order[p]
+                kp = order[p - 1] if p >= 1 else -1
+                kx = order[p - 2] if p >= 2 else N_X
+                kh = order[p - 3] if p >= 3 else N_X
 
                 def group_at(lag):
-                    n = it - 7 - lag
-                    return n // 4 if n >= 0 and n % 4 == 0 else -1
+                    t = order[p - lag] - N_X if p >= lag else -1
+                    return t // 4 if t >= 0 and t % 4 == 3 else -1
 
-                g2, g3, g4, g5 = group_at(2), group_at(3), group_at(4), group_at(5)
-                if it == N_ITEMS - 1:
-                    break
-                if 0 <= it - 3 < N_X:
-                    hadd(it - 3)
-                if k >= 0:
-                    quant(k, (0,))
-                if g2 >= 0:
-                    chain1(g2)
+                g1, g2, g3, g4, g5 = [group_at(lag) for lag in range(1, 6)]
                 if g3 >= 0:
                     chain3a(g3)
+                if kh < N_X:
+                    hadd(kh)
+                if p >= 1:
+                    quant(kp, (0,))
                 if g4 >= 0:
                     chain3b(g4)
                 if g5 >= 0:
                     hs_quant(g5)
-                if k >= 0:
-                    quant(k, (1,))
+                if p >= 1:
+                    quant(kp, (1,))
                 if g4 >= 0:
                     hs_mul(g4)
-                if it - IT_EARLY - 2 in range(0, 2 * EARLY, 2):
-                    early_add((it - IT_EARLY - 2) // 2)
-                if N_X <= it + 1 < N_ITEMS:
-                    sum_v(it + 1)
-                if g4 >= 0:
-                    hs_round(g4)
+                for g in range(EARLY):
+                    if p == P_EARLY[2 * g + 1] + 1:
+                        early_add(g)
                 for half in range(2):
                     for b in (2 * half, 2 * half + 1):
-                        transp(it, b)
-                        if it == 0:
+                        transp(k, b)
+                        if p == 0:
                             hot_fill("x%d" % b, HOT[1] if b < 3 else HOT[2])
-                    if it == 1 and half == 1:
+                    if p == 1 and half == 1:
                         bias_tile()
-                        hot_fill("x4", HOT[3])
                     if half == 1 and g2 >= 0:
                         chain2(g2)
-                    if k >= N_X:
-                        degmm(k, (2 * half, 2 * half + 1))
-                    if 0 <= it - 2 < N_X:
-                        mx1(it - 2, half)
-                        if half == 1:
-                            tag = "D" if it < 5 else "o2"
-                            warm("warmx%d" % it, tag, 1, codes[N_TILES - N_X], planes[N_GROUPS - 1], 512)
-                    elif 0 <= it - IT_EARLY < 2 * EARLY:
-                        early_part(2 * (it - IT_EARLY) + half)
-                    elif it > 1:
-                        warm_tile(it, half)
+                    if kp >= N_X:
+                        degmm(kp, (2 * half,))
+                    if kx < N_X:
+                        mx1(kx, half)
+                        warm("wx%d_%d" % (p, half), "o2", 1, 256)
+                    elif p in P_EARLY:
+                        early_part(2 * P_EARLY.index(p) + half)
+                        second = P_EARLY.index(p) % 2
+                        warm("we%d_%d" % (p, half), "hps" if second else "o2", 1 + second, 128)
+                    elif p >= 1:
+                        warm_half(p, half, "o2" if kh < N_X and half == 0 else "hps")
+                    if kp >= N_X:
+                        degmm(kp, (2 * half + 1,))
+                if g1 >= 0:
+                    chain1(g1)
+                if order[p + 1] >= N_X:
+                    sum_v(order[p + 1])
+                if g4 >= 0:
+                    hs_round(g4)
                 if g3 >= 0:
                     chain3s(g3)
-                if it == N_ITEMS - 2:
-                    sum_a(it + 1)
-                if it + 4 < N_ITEMS:
-                    load(it + 4)
-            it = N_ITEMS - 1
+                if p == N_ITEMS - 2:
+                    sum_a(order[p + 1])
+                if p + 4 < N_ITEMS:
+                    load(order[p + 4])
+            it = order[-1]
             transp(it, 0)
             transp(it, 1)
             degmm(it - 1, (0, 1, 2, 3))
-            transp(it, 2)
-            transp(it, 3)
+            chain1(last)
             quant(it - 1, (0,))
             chain3b(last - 1)
-            chain1(last)
+            transp(it, 2)
             chain2(last)
-            hs_mul(last - 1)
             chain3a(last)
             chain3s(last)
-            quant(it - 1, (1,))
-            hs_round(last - 1)
+            transp(it, 3)
+            hs_mul_round(last - 1)
             chain3b(last)
             hs_quant(last - 1)
             hs_mul_round(last)
             nc.scalar.activation(out=dmy2[:], in_=dmy[:], func=ACTF.Gelu)
-            quant(it, (0,))
+            quant(it - 1, (1,))
             hs_quant(last)
-            quant(it, (1,))
-            hs_mul(last)
             for g in range(N_GROUPS):
                 acc_tile(g)
                 for c in range(first_chunk(g), 6):
                     mx2(accs[g], g, 0, c, first_chunk(g))
-            for g in range(N_GROUPS):
-                mx2(accs[g], g, 0, 6, first_chunk(g))
 
             zs = {}
             gls = {}
@@ -481,6 +489,7 @@ def tile_gcnlayer_pa_t_kernel(tc, x, adj, W1, b1, ln_gamma, ln_beta, out):
 
             def main(g):
                 c0 = first_chunk(g)
+                mx2(accs[g], g, 0, 6, c0)
                 mx2(accs[g], g, 0, 7, c0)
                 for t4 in range(1, 4):
                     for c in range(c0, 8):
@@ -593,34 +602,42 @@ def tile_gcnlayer_pa_t_kernel(tc, x, adj, W1, b1, ln_gamma, ln_beta, out):
                     def live(i):
                         return 0 <= i < N_GROUPS
 
+                    left = [
+                        lambda: quant(order[-1], (0,)),
+                        lambda: quant(order[-1], (1,)),
+                        lambda: hs_mul(last - 1),
+                        lambda: hs_mul(last),
+                    ]
                     for j in range(N_GROUPS + 4):
                         if live(j):
                             main(j)
-                        if live(j):
                             e1(j, ep)
-                        if live(j - 1):
-                            neg_mean(j - 1)
-                        if j - 1 == last:
-                            centre(j - 1, ep)
-                        if j - 2 == last:
-                            inv_std(j - 2)
+                        if j < len(left):
+                            left[j]()
                         if live(j - 4) and j - 4 < last:
                             gam(j - 4)
-                        if live(j - 2) and j - 2 < last:
+                        if live(j - 1):
+                            neg_mean(j - 1)
+                        if live(j - 2):
                             inv_std(j - 2)
+                        if j - 1 == last:
+                            centre(j - 1, ep)
                         if live(j - 4) and j - 4 < last:
                             bet(j - 4, ep)
                         if j - 3 == last:
                             finish(j - 3, ep)
                         if live(j):
                             act_gelu(j, ep)
-                        if live(j - 1):
+                        if j - 1 == last:
                             act_square(j - 1)
                         if live(j - 3) and j - 3 < last:
                             act_norm(j - 3, ep)
+                        if live(j - 1) and j - 1 < last:
+                            act_square(j - 1)
 
             return tail
 
-        with tc.tile_pool(name="natp", bufs=4) as natp, tc.tile_pool(name="grp", bufs=3) as grp:
-            tail = body(natp, grp)
-        tail()
+        with tc.tile_pool(name="grp", bufs=3) as grp:
+            with tc.tile_pool(name="natp", bufs=4) as natp:
+                tail = body(natp, grp)
+            tail()

@@ -24,7 +24,7 @@ N_ITEMS = N_X + N_TILES
 HV = 1024
 HV_LAST = 1536
 C_PE = 4
-HOT = (16, 4, 6, 8)
+HOT = (16, 4, 6)
 HEAT = (512, 256)
 EARLY = 1
 FINE = 1
@@ -436,6 +436,8 @@ def tile_gcnlayer_pa_t_kernel(tc, x, adj, W1, b1, ln_gamma, ln_beta, out):
                         early_part(2 * P_EARLY.index(p) + half)
                         second = P_EARLY.index(p) % 2
                         warm("we%d_%d" % (p, half), "hps" if second else "o2", 1 + second, 128)
+                    elif p == 1 and half == 1:
+                        warm("w1", "hps", 2, 256)
                     elif p >= 1:
                         warm_half(p, half, "o2" if kh < N_X and half == 0 else "hps")
                     if kp >= N_X:
@@ -485,7 +487,6 @@ def tile_gcnlayer_pa_t_kernel(tc, x, adj, W1, b1, ln_gamma, ln_beta, out):
             nmu = keep.tile([P, N_TILES], F32, name="nmu")
             var = keep.tile([P, N_TILES], F32, name="var")
             rstd = keep.tile([P, N_TILES], F32, name="rstd")
-            nmr = keep.tile([P, N_TILES], F32, name="nmr")
 
             def main(g):
                 c0 = first_chunk(g)
@@ -528,26 +529,35 @@ def tile_gcnlayer_pa_t_kernel(tc, x, adj, W1, b1, ln_gamma, ln_beta, out):
                         accum_out=ssq[:, t : t + 1],
                     )
 
+            def act_centre(g):
+                for t4 in range(4):
+                    t = 4 * g + t4
+                    nc.scalar.activation(
+                        out=gls[g][:, t4, :],
+                        in_=gls[g][:, t4, :],
+                        func=ACTF.Identity,
+                        bias=nmu[:, t : t + 1],
+                    )
+
+            def scale_gamma(g, ep):
+                ns[g] = ep.tile([P, 4, F_OUT], F32, tag="n", bufs=3, name="n%d" % g)
+                for t4 in range(4):
+                    t = 4 * g + t4
+                    nc.vector.scalar_tensor_tensor(
+                        out=ns[g][:, t4, :],
+                        in0=gls[g][:, t4, :],
+                        scalar=rstd[:, t : t + 1],
+                        in1=bc[:, 128:256],
+                        op0=ALU.mult,
+                        op1=ALU.mult,
+                    )
+
             def inv_std(g):
                 sl = slice(4 * g, 4 * g + 4)
                 nc.vector.tensor_scalar(
                     out=var[:, sl], in0=ssq[:, sl], scalar1=1.0 / F_OUT, scalar2=EPS, op0=ALU.mult, op1=ALU.add
                 )
                 nc.gpsimd.tensor_tensor(out=rstd[:, sl], in0=var[:, sl], in1=mhalf[:], op=ALU.pow)
-                if g < last:
-                    nc.gpsimd.tensor_tensor(out=nmr[:, sl], in0=nmu[:, sl], in1=rstd[:, sl], op=ALU.mult)
-
-            def act_norm(g, ep):
-                ns[g] = ep.tile([P, 4, F_OUT], F32, tag="n", bufs=3, name="n%d" % g)
-                for t4 in range(4):
-                    t = 4 * g + t4
-                    nc.scalar.activation(
-                        out=ns[g][:, t4, :],
-                        in_=gls[g][:, t4, :],
-                        func=ACTF.Identity,
-                        bias=nmr[:, t : t + 1],
-                        scale=rstd[:, t : t + 1],
-                    )
 
             def centre(g, ep):
                 ns[g] = ep.tile([P, 4, F_OUT], F32, tag="n", bufs=3, name="n%d" % g)
@@ -574,18 +584,11 @@ def tile_gcnlayer_pa_t_kernel(tc, x, adj, W1, b1, ln_gamma, ln_beta, out):
                         op0=ALU.mult,
                         op1=ALU.add,
                     )
-                store(g)
+                    if t4 % 2 == 1:
+                        nc.sync.dma_start(out=outv[g][:, t4 // 2], in_=ys[g][:, t4 - 1 : t4 + 1, :])
 
             def store(g):
                 nc.sync.dma_start(out=outv[g], in_=ys[g][:].rearrange("p (u e) f -> p u e f", u=2))
-
-            def gam(g):
-                nc.vector.tensor_tensor(
-                    out=ns[g][:],
-                    in0=ns[g][:],
-                    in1=bc[:, 128:256].unsqueeze(1).to_broadcast([P, 4, F_OUT]),
-                    op=ALU.mult,
-                )
 
             def bet(g, ep):
                 ys[g] = ep.tile([P, 4, F_OUT], F32, tag="y", bufs=4, name="y%d" % g)
@@ -608,14 +611,14 @@ def tile_gcnlayer_pa_t_kernel(tc, x, adj, W1, b1, ln_gamma, ln_beta, out):
                         lambda: hs_mul(last - 1),
                         lambda: hs_mul(last),
                     ]
-                    for j in range(N_GROUPS + 4):
+                    for j in range(N_GROUPS + 3):
                         if live(j):
                             main(j)
                             e1(j, ep)
                         if j < len(left):
                             left[j]()
                         if live(j - 4) and j - 4 < last:
-                            gam(j - 4)
+                            scale_gamma(j - 4, ep)
                         if live(j - 1):
                             neg_mean(j - 1)
                         if live(j - 2):
@@ -628,12 +631,10 @@ def tile_gcnlayer_pa_t_kernel(tc, x, adj, W1, b1, ln_gamma, ln_beta, out):
                             finish(j - 3, ep)
                         if live(j):
                             act_gelu(j, ep)
-                        if j - 1 == last:
+                        if live(j - 1):
                             act_square(j - 1)
-                        if live(j - 3) and j - 3 < last:
-                            act_norm(j - 3, ep)
-                        if live(j - 1) and j - 1 < last:
-                            act_square(j - 1)
+                            if j - 1 < last:
+                                act_centre(j - 1)
 
             return tail
 

@@ -24,8 +24,8 @@ N_ITEMS = N_X + N_TILES
 HV = 1024
 HV_LAST = 1536
 C_PE = 4
-HOT = (16, 4, 6)
-HEAT = (512, 256)
+HOT = (16, (0, 0, 8, 4))
+HEAT = ((512, 256), (512, 128))
 EARLY = 1
 FINE = 1
 ND = 28
@@ -211,7 +211,7 @@ def tile_gcnlayer_pa_t_kernel(tc, x, adj, W1, b1, ln_gamma, ln_beta, out):
                 warm("hot_" + name, "D", 1, 128, reps)
 
             def warm_half(p, half, tag="hps"):
-                for n in HEAT:
+                for n in HEAT[half]:
                     warm("w%d_%d_%d" % (p, half, n), tag, 2 if tag == "hps" else 1, n)
 
             def degmm(k, quarters):
@@ -393,8 +393,8 @@ def tile_gcnlayer_pa_t_kernel(tc, x, adj, W1, b1, ln_gamma, ln_beta, out):
             for p in range(N_ITEMS - 1):
                 k = order[p]
                 kp = order[p - 1] if p >= 1 else -1
-                kx = order[p - 2] if p >= 2 else N_X
-                kh = order[p - 3] if p >= 3 else N_X
+                kx = order[p - 3] if p >= 3 else N_X
+                kh = order[p - 4] if p >= 4 else N_X
 
                 def group_at(lag):
                     t = order[p - lag] - N_X if p >= lag else -1
@@ -421,8 +421,8 @@ def tile_gcnlayer_pa_t_kernel(tc, x, adj, W1, b1, ln_gamma, ln_beta, out):
                 for half in range(2):
                     for b in (2 * half, 2 * half + 1):
                         transp(k, b)
-                        if p == 0:
-                            hot_fill("x%d" % b, HOT[1] if b < 3 else HOT[2])
+                        if p == 0 and HOT[1][b] > 0:
+                            hot_fill("x%d" % b, HOT[1][b])
                     if p == 1 and half == 1:
                         bias_tile()
                     if half == 1 and g2 >= 0:

from contextlib import ExitStack

import concourse.mybir as mybir
from concourse.masks import make_identity

F32 = mybir.dt.float32
BF16 = mybir.dt.bfloat16
U32 = mybir.dt.uint32
U8 = mybir.dt.uint8
FP8X4 = mybir.dt.float8_e4m3fn_x4
ALU = mybir.AluOpType
ACTF = mybir.ActivationFunctionType
AX = mybir.AxisListType

P = 128
N_NODES = 4096
K_IN = 512
F_OUT = 128
EPS = 1e-6
N_TILES = 32
N_GROUPS = 8
N_X = 4
N_ITEMS = N_X + N_TILES
HV = 1024
HV_LAST = 1536
C_PE = 4
HOT = (16, (0, 0, 8, 4))
HEAT = ((512, 256), (512, 128))
EARLY = 1
FINE = 1
ND = 28
XT_BUFS = 4

FLOPS = 2 * N_NODES * K_IN * F_OUT + 2 * N_NODES * N_NODES * F_OUT


def tile_gcnlayer_pa_t_kernel(tc, x, adj, W1, b1, ln_gamma, ln_beta, out):
    nc = tc.nc
    xv = x.rearrange("(s a p e) k -> s p a e k", s=N_X, a=4, p=P, e=2)
    adjv = adj.rearrange("(g u p e) j -> g u e p j", g=N_GROUPS, u=2, p=P, e=2)
    outv = out.rearrange("(g u p e) f -> g p u e f", g=N_GROUPS, u=2, p=P, e=2)

    with ExitStack() as ctx:
        keep = ctx.enter_context(tc.tile_pool(name="keep", bufs=1))
        small = ctx.enter_context(tc.tile_pool(name="small", bufs=4))
        psum = ctx.enter_context(tc.psum_pool(name="psum", bufs=1))

        def body(natp, grp):
            nats = {}
            grps = {}
            hpss = {}
            dps = {}
            dsbs = {}
            o2s = {}

            def load(k):
                nat = natp.tile([P, 4096], BF16, tag="nat", name="nat%d" % k)
                nats[k] = nat
                if k == 0:
                    for a in range(4):
                        nc.sync.dma_start(
                            out=nat[:, 1024 * a : 1024 * a + 1024].rearrange("p (e k) -> p e k", e=2),
                            in_=xv[0][:, a],
                        )
                elif k < N_X:
                    nc.sync.dma_start(
                        out=nat[:].rearrange("p (a e k) -> p a e k", a=4, e=2, k=K_IN), in_=xv[k]
                    )
                else:
                    t = k - N_X
                    pieces = 4 if t < FINE else 1
                    w = 4096 // pieces
                    for i in range(pieces):
                        nc.sync.dma_start(
                            out=nat[:, w * i : w * i + w],
                            in_=adjv[t // 4, (t % 4) // 2, t % 2][:, w * i : w * i + w],
                        )

            order = []
            for i in range(N_X):
                order += [i] + [N_X + t for t in range(8 * i, 8 * i + 8)]
            for k in order[0:4]:
                load(k)

            hot = keep.tile([P, 512], BF16, name="hot", align_bytes=64)
            nc.vector.memset(hot[:], 1.0)
            hotc = keep.tile([P, 512], U32, name="hotc", align_bytes=64)
            hots = keep.tile([P, 512], U8, name="hots", align_bytes=64)
            for c in range(4):
                nc.vector.quantize_mx(
                    out=hotc[:, 128 * c : 128 * c + 128].bitcast(FP8X4),
                    scales=hots[:, 128 * c : 128 * c + 128],
                    in_=hot[:],
                )
            ident = keep.tile([P, P], F32, name="ident")
            make_identity(nc, ident[:])
            ones = keep.tile([P, P], BF16, name="ones")
            nc.vector.memset(ones[:], 1.0)
            zrow = keep.tile([P, 512], BF16, name="zrow")
            nc.vector.memset(zrow[:], 0.0)
            w1n = keep.tile([P, 4, F_OUT], BF16, name="w1n")
            nc.scalar.dma_start(
                out=w1n[:].rearrange("q (u e) f -> q u e f", u=2),
                in_=W1.rearrange("(u q e) f -> q u e f", u=2, q=P, e=2),
            )
            nc.scalar.dma_start(out=zrow[0:1, 0:128], in_=b1.rearrange("(o f) -> o f", o=1))
            nc.scalar.dma_start(out=zrow[0:1, 128:256], in_=ln_gamma.rearrange("(o f) -> o f", o=1))
            nc.scalar.dma_start(out=zrow[0:1, 256:384], in_=ln_beta.rearrange("(o f) -> o f", o=1))
            dmy = keep.tile([P, 1], F32, name="dmy")
            nc.vector.memset(dmy[:], 1.0)
            dmy2 = keep.tile([P, 1], F32, name="dmy2")
            nc.scalar.activation(out=dmy2[:], in_=dmy[:], func=ACTF.Sqrt)

            rsel = keep.tile([P, 32], F32, name="rsel")
            nc.vector.tensor_reduce(
                out=rsel[:], in_=ident[:].rearrange("k (a t) -> k a t", t=4), axis=AX.X, op=ALU.add
            )
            sel4 = keep.tile([P, 4, P], F32, name="sel4")
            nc.vector.memset(sel4[:], 0.0)
            for s in range(4):
                nc.vector.tensor_copy(out=sel4[:, s, 32 * s : 32 * s + 32], in_=rsel[:])

            w1g = keep.tile([P, F_OUT, 4], BF16, name="w1g", align_bytes=64)
            nc.vector.tensor_copy(out=w1g[:], in_=w1n[:].rearrange("q t f -> q f t"))
            w1c = keep.tile([P, F_OUT], U32, name="w1c", align_bytes=64)
            w1s = keep.tile([P, F_OUT], U8, name="w1s", align_bytes=64)
            nc.vector.quantize_mx(
                out=w1c[:].bitcast(FP8X4), scales=w1s[:], in_=w1g[:].rearrange("q f t -> q (f t)")
            )
            bc = keep.tile([P, 384], F32, name="bc")

            last = N_GROUPS - 1
            codes = [
                keep.tile([P, 1024], U32, name="codes%d" % t, align_bytes=64) for t in range(N_TILES)
            ]
            planes = [
                keep.tile([P, 1024], U8, name="planes%d" % g, align_bytes=64) for g in range(N_GROUPS)
            ]
            h = keep.tile([P, N_TILES, F_OUT], F32, name="h")
            hcod = keep.tile([P, N_GROUPS * F_OUT], U32, name="hcod", align_bytes=64)
            hscl = keep.tile([P, N_GROUPS * F_OUT], U8, name="hscl", align_bytes=64)
            degv = keep.tile([P, N_TILES], F32, name="degv")
            dega = keep.tile([P, N_TILES], F32, name="dega")
            deg1 = keep.tile([P, N_TILES], F32, name="deg1")
            dinv = keep.tile([P, N_TILES], F32, name="dinv")
            sqd = keep.tile([P, N_TILES], F32, name="sqd")
            degs = keep.tile([P, N_TILES], F32, name="degs")
            junkv = keep.tile([P, HV_LAST], F32, name="junkv")
            junka = keep.tile([P, 4096 - 2 * HV_LAST], BF16, name="junka")

            nc.vector.memset(dega[:], 0.0)
            dsb_last = keep.tile([P, 4, 4], F32, name="dsb_last")
            nc.vector.memset(dsb_last[:], 0.0)
            mhalf = keep.tile([P, 4], F32, name="mhalf")
            nc.vector.memset(mhalf[:], -0.5)

            def slot_of(k):
                return k - N_X if k >= N_X else N_TILES - N_X + k

            def transp(k, b):
                if b == 0:
                    grps[k] = grp.tile([P, 4096], BF16, tag="G", name="G%d" % k, align_bytes=64)
                nat_w = nats[k][:].bitcast(F32)
                g_w = grps[k][:].bitcast(F32).rearrange("p (c i u) -> p c i u", c=8, i=P, u=2)
                xt = psum.tile([P, 2, 2, P], F32, tag="xt", bufs=XT_BUFS, name="xt%d_%d" % (k, b))
                for cc in range(2):
                    for u in range(2):
                        w0 = 256 * (2 * b + cc) + 128 * u
                        nc.tensor.transpose(xt[:, cc, u, :], nat_w[:, w0 : w0 + 128], ident[:])
                nc.scalar.copy(
                    out=g_w[:, 2 * b : 2 * b + 2, :, :], in_=xt[:].rearrange("p c u i -> p c i u")
                )

            def sum_v(k):
                t = k - N_X
                hv = HV if t < N_TILES - 1 else HV_LAST
                nc.vector.scalar_tensor_tensor(
                    out=junkv[:, 0:hv],
                    in0=nats[k][:, 0:hv],
                    scalar=1.0,
                    in1=nats[k][:, hv : 2 * hv],
                    op0=ALU.mult,
                    op1=ALU.add,
                    accum_out=degv[:, t : t + 1],
                )

            def sum_a(k):
                t = k - N_X
                nc.scalar.activation(
                    out=junka[:],
                    in_=nats[k][:, 2 * HV_LAST : 4096],
                    func=ACTF.Copy,
                    accum_out=dega[:, t : t + 1],
                )

            def warm(name, tag, bufs, n, reps=1):
                wps = psum.tile([P, 512], F32, tag=tag, bufs=bufs, name=name)
                for i in range(reps):
                    c0 = n * (i % (512 // n))
                    nc.tensor.matmul_mx(
                        out=wps[:, c0 : c0 + n],
                        lhsT=hotc[:, 0:128].bitcast(FP8X4),
                        lhsT_scale=hots[:, 0:128],
                        rhs=hotc[:, 0:n].bitcast(FP8X4),
                        rhs_scale=hots[:, 0:n],
                        start=True,
                        stop=True,
                    )

            def hot_fill(name, reps):
                warm("hot_" + name, "D", 1, 128, reps)

            def warm_half(p, half, tag="hps"):
                for n in HEAT[half]:
                    warm("w%d_%d_%d" % (p, half, n), tag, 2 if tag == "hps" else 1, n)

            def degmm(k, quarters):
                t = k - N_X
                g = t // 4
                t4 = t % 4
                if t4 == 0 and quarters[0] == 0:
                    dps[g] = psum.tile([P, 4, 4, ND], F32, tag="D", name="D%d" % g)
                for s in quarters:
                    for c in range(C_PE, 8):
                        c0 = 512 * c + 128 * s
                        nc.tensor.matmul(
                            out=dps[g][:, t4, s, :],
                            lhsT=grps[k][:, c0 : c0 + 128],
                            rhs=ones[:, 0:ND],
                            start=(c == C_PE),
                            stop=(c == 7),
                        )

            def chain1(g):
                dsb = small.tile([P, 4, 4], F32, tag="dsb", name="dsb%d" % g) if g < last else dsb_last
                dsbs[g] = dsb
                n = 4 if g < last else 3
                nc.vector.tensor_copy(
                    out=dsb[:, :, 0:n], in_=dps[g][:, 0:n, :, 0].rearrange("p t s -> p s t")
                )

            def chain2(g):
                o2 = psum.tile([P, 4], F32, tag="o2", name="o2_%d" % g)
                o2s[g] = o2
                for s in range(4):
                    nc.tensor.matmul(
                        out=o2[:], lhsT=sel4[:, s, :], rhs=dsbs[g][:, s, :], start=(s == 0), stop=(s == 3)
                    )

            def quant(k, halves=(0, 1)):
                sl = slot_of(k)
                kk = 4 * (sl % 4)
                for hf in halves:
                    nc.vector.quantize_mx(
                        out=codes[sl][:, 512 * hf : 512 * hf + 512].bitcast(FP8X4),
                        scales=planes[sl // 4][kk:P, 512 * hf : 512 * hf + 512],
                        in_=grps[k][:, 2048 * hf : 2048 * hf + 2048],
                    )

            def mx1(k, gg):
                sl = slot_of(k)
                kk = 4 * (sl % 4)
                g = 2 * k + gg
                hps = psum.tile([P, 4, F_OUT], F32, tag="hps", bufs=2, name="hps%d" % g)
                hpss[g] = hps
                for t4 in range(4):
                    c0 = 128 * (4 * gg + t4)
                    nc.tensor.matmul_mx(
                        out=hps[:, t4, :],
                        lhsT=codes[sl][:, c0 : c0 + 128].bitcast(FP8X4),
                        lhsT_scale=planes[sl // 4][kk:P, c0 : c0 + 128],
                        rhs=w1c[:].bitcast(FP8X4),
                        rhs_scale=w1s[:],
                        start=True,
                        stop=True,
                    )

            def bias_tile():
                bcps = psum.tile([P, 512], F32, tag="hps", bufs=2, name="bcps")
                nc.tensor.matmul(out=bcps[:], lhsT=ones[:], rhs=zrow[:], start=True, stop=True)
                nc.vector.tensor_copy(out=bc[:], in_=bcps[:, 0:384])

            def hadd(k):
                for gg in range(2):
                    g = 2 * k + gg
                    nc.vector.tensor_tensor(
                        out=h[:, 4 * g : 4 * g + 4, :],
                        in0=hpss[g][:],
                        in1=bc[:, 0:128].unsqueeze(1).to_broadcast([P, 4, F_OUT]),
                        op=ALU.add,
                    )

            def chain3a(g):
                sl = slice(4 * g, 4 * g + 4)
                dv = degv
                if g == last:
                    nc.vector.tensor_tensor(out=degs[:, sl], in0=degv[:, sl], in1=dega[:, sl], op=ALU.add)
                    dv = degs
                nc.vector.scalar_tensor_tensor(
                    out=deg1[:, sl], in0=o2s[g][:], scalar=1.0, in1=dv[:, sl], op0=ALU.add, op1=ALU.add
                )

            def chain3s(g):
                sl = slice(4 * g, 4 * g + 4)
                nc.scalar.activation(out=sqd[:, sl], in_=deg1[:, sl], func=ACTF.Sqrt)

            def chain3b(g):
                sl = slice(4 * g, 4 * g + 4)
                nc.vector.reciprocal(out=dinv[:, sl], in_=sqd[:, sl])

            hsbs = {}

            def hs_tile(g):
                hsbs[g] = small.tile([P, F_OUT, 4], BF16, tag="hsb", bufs=2, name="hsb%d" % g, align_bytes=64)

            def hs_mul(g):
                sl = slice(4 * g, 4 * g + 4)
                nc.vector.tensor_tensor(
                    out=h[:, sl, :],
                    in0=h[:, sl, :],
                    in1=dinv[:, sl].unsqueeze(2).to_broadcast([P, 4, F_OUT]),
                    op=ALU.mult,
                )

            def hs_round(g):
                hs_tile(g)
                nc.vector.tensor_copy(
                    out=hsbs[g][:], in_=h[:, 4 * g : 4 * g + 4, :].rearrange("p t f -> p f t")
                )

            def hs_mul_round(g):
                hs_tile(g)
                sl = slice(4 * g, 4 * g + 4)
                nc.vector.tensor_tensor(
                    out=hsbs[g][:],
                    in0=h[:, sl, :].rearrange("p t f -> p f t"),
                    in1=dinv[:, sl].unsqueeze(1).to_broadcast([P, F_OUT, 4]),
                    op=ALU.mult,
                )

            def hs_quant(g):
                nc.vector.quantize_mx(
                    out=hcod[:, 128 * g : 128 * g + 128].bitcast(FP8X4),
                    scales=hscl[:, 128 * g : 128 * g + 128],
                    in_=hsbs[g][:].rearrange("p f t -> p (f t)"),
                )

            def mx2(acc, g, t4, c, c_first=0, c_last=7):
                t = 4 * g + t4
                nc.tensor.matmul_mx(
                    out=acc[:, t4, :],
                    lhsT=codes[t][:, 128 * c : 128 * c + 128].bitcast(FP8X4),
                    lhsT_scale=planes[g][4 * t4 : P, 128 * c : 128 * c + 128],
                    rhs=hcod[:, 128 * c : 128 * c + 128].bitcast(FP8X4),
                    rhs_scale=hscl[:, 128 * c : 128 * c + 128],
                    start=(c == c_first),
                    stop=(c == c_last),
                )

            accs = {}

            acc_tags = [("hps", 2), ("hps", 2), ("D", 1)] + [("xt", XT_BUFS)] * XT_BUFS + [("o2", 1)]
            C_EARLY = 5
            P_EARLY = [27, 28]
            early = {}

            def early_part(q):
                g, t4 = q // 4, q % 4
                if t4 == 0:
                    early[g] = psum.tile([P, 4, F_OUT], F32, tag="hps", bufs=2, name="early%d" % g)
                for c in range(C_EARLY):
                    mx2(early[g], g, t4, c, 0, C_EARLY - 1)

            def early_add(g):
                nc.vector.tensor_tensor(
                    out=h[:, 4 * g : 4 * g + 4, :],
                    in0=early[g][:],
                    in1=h[:, 4 * g : 4 * g + 4, :],
                    op=ALU.add,
                )

            def acc_tile(g):
                accs[g] = psum.tile(
                    [P, 4, F_OUT], F32, tag=acc_tags[g][0], bufs=acc_tags[g][1], name="acc%d" % g
                )

            def first_chunk(g):
                return C_EARLY if g < EARLY else 0

            ctx.enter_context(tc.manual_schedule())

            hot_fill("head", HOT[0])
            for p in range(N_ITEMS - 1):
                k = order[p]
                kp = order[p - 1] if p >= 1 else -1
                kx = order[p - 3] if p >= 3 else N_X
                kh = order[p - 4] if p >= 4 else N_X

                def group_at(lag):
                    t = order[p - lag] - N_X if p >= lag else -1
                    return t // 4 if t >= 0 and t % 4 == 3 else -1

                g1, g2, g3, g4, g5 = [group_at(lag) for lag in range(1, 6)]
                if g3 >= 0:
                    chain3a(g3)
                if kh < N_X:
                    hadd(kh)
                if p >= 1:
                    quant(kp, (0,))
                if g4 >= 0:
                    chain3b(g4)
                if g5 >= 0:
                    hs_quant(g5)
                if p >= 1:
                    quant(kp, (1,))
                if g4 >= 0:
                    hs_mul(g4)
                for g in range(EARLY):
                    if p == P_EARLY[2 * g + 1] + 1:
                        early_add(g)
                for half in range(2):
                    for b in (2 * half, 2 * half + 1):
                        transp(k, b)
                        if p == 0 and HOT[1][b] > 0:
                            hot_fill("x%d" % b, HOT[1][b])
                    if p == 1 and half == 1:
                        bias_tile()
                    if half == 1 and g2 >= 0:
                        chain2(g2)
                    if kp >= N_X:
                        degmm(kp, (2 * half,))
                    if kx < N_X:
                        mx1(kx, half)
                        warm("wx%d_%d" % (p, half), "o2", 1, 256)
                    elif p in P_EARLY:
                        early_part(2 * P_EARLY.index(p) + half)
                        second = P_EARLY.index(p) % 2
                        warm("we%d_%d" % (p, half), "hps" if second else "o2", 1 + second, 128)
                    elif p == 1 and half == 1:
                        warm("w1", "hps", 2, 256)
                    elif p >= 1:
                        warm_half(p, half, "o2" if kh < N_X and half == 0 else "hps")
                    if kp >= N_X:
                        degmm(kp, (2 * half + 1,))
                if g1 >= 0:
                    chain1(g1)
                if order[p + 1] >= N_X:
                    sum_v(order[p + 1])
                if g4 >= 0:
                    hs_round(g4)
                if g3 >= 0:
                    chain3s(g3)
                if p == N_ITEMS - 2:
                    sum_a(order[p + 1])
                if p + 4 < N_ITEMS:
                    load(order[p + 4])
            it = order[-1]
            transp(it, 0)
            transp(it, 1)
            degmm(it - 1, (0, 1, 2, 3))
            chain1(last)
            quant(it - 1, (0,))
            chain3b(last - 1)
            transp(it, 2)
            chain2(last)
            chain3a(last)
            chain3s(last)
            transp(it, 3)
            hs_mul_round(last - 1)
            chain3b(last)
            hs_quant(last - 1)
            hs_mul_round(last)
            nc.scalar.activation(out=dmy2[:], in_=dmy[:], func=ACTF.Gelu)
            quant(it - 1, (1,))
            hs_quant(last)
            for g in range(N_GROUPS):
                acc_tile(g)
                for c in range(first_chunk(g), 6):
                    mx2(accs[g], g, 0, c, first_chunk(g))

            zs = {}
            gls = {}
            ns = {}
            ys = {}
            gsum = keep.tile([P, N_TILES], F32, name="gsum")
            ssq = keep.tile([P, N_TILES], F32, name="ssq")
            nmu = keep.tile([P, N_TILES], F32, name="nmu")
            var = keep.tile([P, N_TILES], F32, name="var")
            rstd = keep.tile([P, N_TILES], F32, name="rstd")

            def main(g):
                c0 = first_chunk(g)
                mx2(accs[g], g, 0, 6, c0)
                mx2(accs[g], g, 0, 7, c0)
                for t4 in range(1, 4):
                    for c in range(c0, 8):
                        mx2(accs[g], g, t4, c, c0)

            def e1(g, ep):
                zs[g] = ep.tile([P, 4, F_OUT], F32, tag="z", bufs=3, name="z%d" % g)
                nc.vector.tensor_tensor(
                    out=zs[g][:], in0=accs[g][:], in1=h[:, 4 * g : 4 * g + 4, :], op=ALU.add
                )

            def act_gelu(g, ep):
                gls[g] = ep.tile([P, 4, F_OUT], F32, tag="gl", bufs=5, name="gl%d" % g)
                for t4 in range(4):
                    t = 4 * g + t4
                    nc.scalar.activation(
                        out=gls[g][:, t4, :],
                        in_=zs[g][:, t4, :],
                        func=ACTF.Gelu,
                        scale=dinv[:, t : t + 1],
                        accum_out=gsum[:, t : t + 1],
                    )

            def neg_mean(g):
                sl = slice(4 * g, 4 * g + 4)
                nc.vector.tensor_scalar_mul(out=nmu[:, sl], in0=gsum[:, sl], scalar1=-1.0 / F_OUT)

            def act_square(g):
                for t4 in range(4):
                    t = 4 * g + t4
                    nc.scalar.activation(
                        out=junkv[:, 128 * t4 : 128 * t4 + 128],
                        in_=gls[g][:, t4, :],
                        func=ACTF.Square,
                        bias=nmu[:, t : t + 1],
                        accum_out=ssq[:, t : t + 1],
                    )

            def act_centre(g):
                for t4 in range(4):
                    t = 4 * g + t4
                    nc.scalar.activation(
                        out=gls[g][:, t4, :],
                        in_=gls[g][:, t4, :],
                        func=ACTF.Identity,
                        bias=nmu[:, t : t + 1],
                    )

            def scale_gamma(g, ep):
                ns[g] = ep.tile([P, 4, F_OUT], F32, tag="n", bufs=3, name="n%d" % g)
                for t4 in range(4):
                    t = 4 * g + t4
                    nc.vector.scalar_tensor_tensor(
                        out=ns[g][:, t4, :],
                        in0=gls[g][:, t4, :],
                        scalar=rstd[:, t : t + 1],
                        in1=bc[:, 128:256],
                        op0=ALU.mult,
                        op1=ALU.mult,
                    )

            def inv_std(g):
                sl = slice(4 * g, 4 * g + 4)
                nc.vector.tensor_scalar(
                    out=var[:, sl], in0=ssq[:, sl], scalar1=1.0 / F_OUT, scalar2=EPS, op0=ALU.mult, op1=ALU.add
                )
                nc.gpsimd.tensor_tensor(out=rstd[:, sl], in0=var[:, sl], in1=mhalf[:], op=ALU.pow)

            def centre(g, ep):
                ns[g] = ep.tile([P, 4, F_OUT], F32, tag="n", bufs=3, name="n%d" % g)
                for t4 in range(4):
                    t = 4 * g + t4
                    nc.vector.scalar_tensor_tensor(
                        out=ns[g][:, t4, :],
                        in0=gls[g][:, t4, :],
                        scalar=nmu[:, t : t + 1],
                        in1=bc[:, 128:256],
                        op0=ALU.add,
                        op1=ALU.mult,
                    )

            def finish(g, ep):
                ys[g] = ep.tile([P, 4, F_OUT], F32, tag="y", bufs=4, name="y%d" % g)
                for t4 in range(4):
                    t = 4 * g + t4
                    nc.vector.scalar_tensor_tensor(
                        out=ys[g][:, t4, :],
                        in0=ns[g][:, t4, :],
                        scalar=rstd[:, t : t + 1],
                        in1=bc[:, 256:384],
                        op0=ALU.mult,
                        op1=ALU.add,
                    )
                    if t4 % 2 == 1:
                        nc.sync.dma_start(out=outv[g][:, t4 // 2], in_=ys[g][:, t4 - 1 : t4 + 1, :])

            def store(g):
                nc.sync.dma_start(out=outv[g], in_=ys[g][:].rearrange("p (u e) f -> p u e f", u=2))

            def bet(g, ep):
                ys[g] = ep.tile([P, 4, F_OUT], F32, tag="y", bufs=4, name="y%d" % g)
                nc.vector.tensor_tensor(
                    out=ys[g][:],
                    in0=ns[g][:],
                    in1=bc[:, 256:384].unsqueeze(1).to_broadcast([P, 4, F_OUT]),
                    op=ALU.add,
                )
                store(g)

            def tail():
                with tc.tile_pool(name="ep", bufs=4) as ep:
                    def live(i):
                        return 0 <= i < N_GROUPS

                    left = [
                        lambda: quant(order[-1], (0,)),
                        lambda: quant(order[-1], (1,)),
                        lambda: hs_mul(last - 1),
                        lambda: hs_mul(last),
                    ]
                    for j in range(N_GROUPS + 3):
                        if live(j):
                            main(j)
                            e1(j, ep)
                        if j < len(left):
                            left[j]()
                        if live(j - 4) and j - 4 < last:
                            scale_gamma(j - 4, ep)
                        if live(j - 1):
                            neg_mean(j - 1)
                        if live(j - 2):
                            inv_std(j - 2)
                        if j - 1 == last:
                            centre(j - 1, ep)
                        if live(j - 4) and j - 4 < last:
                            bet(j - 4, ep)
                        if j - 3 == last:
                            finish(j - 3, ep)
                        if live(j):
                            act_gelu(j, ep)
                        if live(j - 1):
                            act_square(j - 1)
                            if j - 1 < last:
                                act_centre(j - 1)

            return tail

        with tc.tile_pool(name="grp", bufs=3) as grp:
            with tc.tile_pool(name="natp", bufs=4) as natp:
                tail = body(natp, grp)
            tail()
